import numpy as np
import ml_dtypes


def mxq(x, axis, fmt="e4m3"):
    dtype, down = {"e4m3": (ml_dtypes.float8_e4m3fn, 7), "e5m2": (ml_dtypes.float8_e5m2, 14)}[fmt]
    v = np.moveaxis(np.asarray(x, np.float32).astype(ml_dtypes.bfloat16).astype(np.float64), axis, -1)
    blocks = v.reshape(v.shape[:-1] + (-1, 32))
    amax = np.abs(blocks).max(-1, keepdims=True)
    byte = np.maximum(np.where(amax > 0, np.frexp(amax)[1] - 1 + 127, 0) - down, 1)
    scale = np.exp2(byte - 127.0)
    codes = (blocks / scale).astype(np.float32).astype(dtype).astype(np.float64)
    return np.moveaxis((codes * scale).reshape(v.shape), -1, axis)


WIDE = False


def mx_kscale(k):
    if not WIDE:
        return np.ones(k)
    levels = np.array([18, -18])
    if k % 512:
        return np.exp2(np.random.permutation(np.resize(levels, k // 32))).repeat(32)
    a = np.empty((k // 512, 16))
    for p in range(k // 512):
        a[p, :8] = np.random.permutation(np.resize(levels, 8))
        for g in range(8):
            far = levels[np.abs(levels - a[p, g]) >= 10]
            a[p, g + 8] = far[np.random.randint(len(far))]
    return np.exp2(a.ravel()).repeat(32)


BF16 = ml_dtypes.bfloat16


def bf(x):
    return np.asarray(x, np.float32).astype(BF16)


def f64(x):
    return np.asarray(x).astype(np.float64)


T, HS, WS, WT, WH, WW, NH, HD, VID_DIM = 8, 8, 16, 8, 8, 8, 4, 128, 1536
EPS = 1e-6
L_VID = T * HS * WS
N_WIN = (T // WT) * (HS // WH) * (WS // WW)
WIN_LEN = WT * WH * WW
INNER = NH * HD


def window_partition(x):
    x = x.reshape(T // WT, WT, HS // WH, WH, WS // WW, WW, NH, HD)
    x = x.transpose(0, 2, 4, 1, 3, 5, 6, 7)
    return x.reshape(N_WIN, WIN_LEN, NH, HD)


def window_reverse(y):
    y = y.reshape(T // WT, HS // WH, WS // WW, WT, WH, WW, NH, HD)
    y = y.transpose(0, 3, 1, 4, 2, 5, 6, 7)
    return y.reshape(L_VID, NH, HD)


def rmsnorm_back(g, gain, x, r):
    gg = g * gain
    xh = x * r
    return r * (gg - xh * np.mean(gg * xh, axis=-1, keepdims=True))


def setup_inputs():
    s = mx_kscale(L_VID)
    sw = window_partition(np.ones((L_VID, NH, HD)) * s[:, None, None])
    u = mx_kscale(3 * INNER).reshape(3, NH, HD)
    uh = u[:2, np.arange(NH), 32 * np.arange(NH)]
    u = np.concatenate([np.repeat(uh[:, :, None], HD, axis=2), u[2:]], axis=0)
    vid0 = bf(np.random.standard_normal((L_VID, VID_DIM)))
    w0 = bf(np.random.standard_normal((VID_DIM, 3 * INNER)) / np.sqrt(VID_DIM))
    b = bf(0.1 * np.random.standard_normal(3 * INNER))
    q_scale = bf(1.0 + 0.1 * np.random.standard_normal(HD))
    k_scale = bf(1.0 + 0.1 * np.random.standard_normal(HD))
    grads = []
    for i in range(3):
        e = np.exp2(np.random.randint(-6, 1, (N_WIN, WIN_LEN, 1, 1)))
        grads.append(bf(2.0 * np.random.standard_normal((N_WIN, WIN_LEN, NH, HD)) * e / sw * u[i]))
    qk = (f64(vid0) @ f64(w0) + f64(b))[:, :2 * INNER].reshape(L_VID, 2, NH, HD)
    rstd = 1.0 / np.sqrt(np.mean(qk * qk, axis=-1) + EPS)
    return {
        "vid": bf(f64(vid0) * s[:, None]),
        "Wqkv_vid": bf(f64(w0) / u.reshape(-1)),
        "bqkv_vid": b,
        "q_scale_vid": q_scale,
        "k_scale_vid": k_scale,
        "qk_pre": np.asarray(qk, np.float32),
        "qk_rstd": np.asarray(rstd, np.float32),
        "grad_0": grads[0],
        "grad_1": grads[1],
        "grad_2": grads[2],
    }


def reference(vid, Wqkv_vid, bqkv_vid, q_scale_vid, k_scale_vid, qk_pre, qk_rstd, grad_0, grad_1, grad_2):
    qk = f64(qk_pre)
    r = f64(qk_rstd)[:, :, :, None]
    dq = rmsnorm_back(window_reverse(f64(grad_0)), f64(q_scale_vid), qk[:, 0], r[:, 0])
    dk = rmsnorm_back(window_reverse(f64(grad_1)), f64(k_scale_vid), qk[:, 1], r[:, 1])
    dv = window_reverse(f64(grad_2))
    dz = np.concatenate([dq.reshape(L_VID, INNER), dk.reshape(L_VID, INNER), dv.reshape(L_VID, INNER)], axis=1)
    dx = mxq(dz, 1, "e5m2") @ mxq(f64(Wqkv_vid), 1, "e4m3").T
    dw = mxq(f64(vid), 0, "e4m3").T @ mxq(dz, 0, "e5m2")
    return dx, dw

@@ -1,0 +1,692 @@
+from contextlib import ExitStack
+
+import concourse.mybir as mybir
+from concourse.masks import make_identity
+
+F32 = mybir.dt.float32
+BF16 = mybir.dt.bfloat16
+U32 = mybir.dt.uint32
+U8 = mybir.dt.uint8
+E4M3X4 = mybir.dt.float8_e4m3fn_x4
+E5M2X4 = mybir.dt.float8_e5m2_x4
+MULT = mybir.AluOpType.mult
+ADD = mybir.AluOpType.add
+COPY = mybir.ActivationFunctionType.Copy
+
+P = 128
+TOK, DIM, FEAT = 1024, 1536, 1536
+HEADS, HD = 4, 128
+INNER = HEADS * HD
+J = 4
+GROUP = P * J
+GROUPS = TOK // GROUP
+FLOPS = 2 * 2 * TOK * DIM * FEAT
+BYTES = 2 * (TOK * DIM + DIM * FEAT + 2 * HD + TOK * FEAT) + 4 * (
+    TOK * 2 * INNER + TOK * 2 * HEADS + TOK * DIM + DIM * FEAT
+)
+
+
+def tile_naswinattention_pa_v_kernel(
+    tc, vid, w_qkv, b_qkv, q_scale, k_scale, qk_pre, qk_rstd, grad_q, grad_k, grad_v, out_0, out_1
+):
+    nc = tc.nc
+    TP_BUFS, ACC_BUFS = 3, 5
+    BIG_BUFS, PRE_BUFS, INTER_BUFS, GROUPED_BUFS, RES_BUFS, DZ_BUFS, LEAD_BUFS = 4, 3, 4, 6, 4, 2, 5
+    SEQ = [
+        ('D', ('ld', 'g2')),
+        ('D', ('ld', 'g0')),
+        ('V', ('DI', 2, 0)),
+        ('PE', ('PI', 'DI', 2, 1, 0)),
+        ('PE', ('PI', 'DI', 2, 1, 1)),
+        ('S', ('IC', 'DI', 2, 1, 0)),
+        ('PE', ('DT', 2, 0, 0)),
+        ('V', ('IC', 'DI', 2, 1, 1)),
+        ('D', ('ld', 'p00')),
+        ('PE', ('DT', 2, 0, 1)),
+        ('S', ('DC', 2, 0, 0)),
+        ('V', ('DQ', 2, 0)),
+        ('PE', ('DT', 2, 1, 0)),
+        ('S', ('DC', 2, 0, 1)),
+        ('V', ('DQ', 2, 1)),
+        ('PE', ('DT', 2, 1, 1)),
+        ('S', ('DC', 2, 1, 0)),
+        ('V', ('TQ', 2, 0, 0)),
+        ('V', ('TQ', 2, 0, 1)),
+        ('S', ('DC', 2, 1, 1)),
+        ('V', ('TQ', 2, 1, 0)),
+        ('D', ('ld', 'v0')),
+        ('V', ('L', 0, 0, 0)),
+        ('V', ('TQ', 2, 1, 1)),
+        ('V', ('L', 0, 0, 1)),
+        ('V', ('D', 0, 0, 0)),
+        ('V', ('L', 0, 0, 2)),
+        ('V', ('C', 0, 0, 0)),
+        ('V', ('D', 0, 0, 1)),
+        ('D', ('ld', 'p01')),
+        ('V', ('F', 0, 0, 0)),
+        ('PE', ('PI', 'VI', 0, 1, 0)),
+        ('V', ('VI', 0, 0)),
+        ('PE', ('PI', 'VI', 0, 1, 1)),
+        ('S', ('IC', 'VI', 0, 1, 0)),
+        ('PE', ('PI', 'VI', 0, 2, 0)),
+        ('D', ('ld', 'v1')),
+        ('S', ('IC', 'VI', 0, 1, 1)),
+        ('V', ('C', 0, 0, 1)),
+        ('V', ('L', 0, 0, 3)),
+        ('PE', ('PI', 'VI', 0, 2, 1)),
+        ('S', ('IC', 'VI', 0, 2, 0)),
+        ('V', ('VQ', 0, 0)),
+        ('S', ('IC', 'VI', 0, 2, 1)),
+        ('V', ('VQ', 0, 1)),
+        ('V', ('VQ', 0, 2)),
+        ('V', ('F', 0, 0, 1)),
+        ('V', ('D', 0, 0, 2)),
+        ('PE', ('DT', 0, 0, 0)),
+        ('D', ('ld', 'g1')),
+        ('S', ('DC', 0, 0, 0)),
+        ('V', ('L', 0, 1, 0)),
+        ('S', ('VI', 1, 0)),
+        ('V', ('VI', 1, 1)),
+        ('V', ('TQ', 0, 0, 0)),
+        ('D', ('ld', 'w1')),
+        ('V', ('VQ', 1, 1)),
+        ('V', ('C', 0, 0, 2)),
+        ('V', ('D', 0, 0, 3)),
+        ('PE', ('O1', 2, 4)),
+        ('S', ('VI', 1, 2)),
+        ('PE', ('O1', 2, 5)),
+        ('V', ('VQ', 1, 0)),
+        ('PE', ('O1', 2, 6)),
+        ('V', ('F', 0, 0, 2)),
+        ('PE', ('O1', 2, 0)),
+        ('V', ('C', 0, 0, 3)),
+        ('V', ('L', 0, 1, 1)),
+        ('PE', ('O1', 2, 1)),
+        ('D', ('ld', 'p10')),
+        ('S', ('X1', 2, 0)),
+        ('V', ('F', 0, 0, 3)),
+        ('S', ('X1', 2, 1)),
+        ('V', ('VQ', 1, 2)),
+        ('PE', ('O1', 2, 2)),
+        ('S', ('X1', 2, 4)),
+        ('PE', ('O1', 2, 3)),
+        ('V', ('D', 0, 1, 0)),
+        ('S', ('X1', 2, 2)),
+        ('PE', ('O1', 2, 7)),
+        ('V', ('L', 0, 1, 2)),
+        ('D', ('ld', 'w2')),
+        ('S', ('X1', 2, 3)),
+        ('PE', ('O1', 2, 8)),
+        ('V', ('C', 0, 1, 0)),
+        ('S', ('X1', 2, 5)),
+        ('V', ('D', 0, 1, 1)),
+        ('PE', ('O1', 2, 9)),
+        ('S', ('X1', 2, 6)),
+        ('PE', ('O1', 2, 10)),
+        ('V', ('F', 0, 1, 0)),
+        ('S', ('X1', 2, 7)),
+        ('PE', ('O1', 2, 11)),
+        ('V', ('C', 0, 1, 1)),
+        ('V', ('L', 0, 1, 3)),
+        ('S', ('X1', 2, 9)),
+        ('PE', ('PI', 'DI', 0, 0, 0)),
+        ('S', ('X1', 2, 11)),
+        ('V', ('F', 0, 1, 1)),
+        ('PE', ('PI', 'DI', 0, 0, 1)),
+        ('S', ('IC', 'DI', 0, 0, 0)),
+        ('V', ('D', 0, 1, 2)),
+        ('D', ('ld', 'w0')),
+        ('PE', ('DT', 0, 0, 1)),
+        ('S', ('IC', 'DI', 0, 0, 1)),
+        ('PE', ('WT', 1, 0, 0)),
+        ('V', ('L', 1, 0, 0)),
+        ('S', ('DC', 0, 0, 1)),
+        ('PE', ('WT', 1, 0, 1)),
+        ('V', ('DQ', 0, 0)),
+        ('S', ('WC', 1, 0, 0)),
+        ('PE', ('WT', 1, 1, 0)),
+        ('V', ('TQ', 0, 0, 1)),
+        ('S', ('WC', 1, 0, 1)),
+        ('PE', ('DT', 0, 1, 0)),
+        ('V', ('WQ', 1, 0, 0)),
+        ('S', ('WC', 1, 1, 0)),
+        ('V', ('C', 0, 1, 2)),
+        ('V', ('WQ', 1, 0, 1)),
+        ('PE', ('WT', 1, 1, 1)),
+        ('V', ('F', 0, 1, 2)),
+        ('S', ('DC', 0, 1, 0)),
+        ('PE', ('WT', 1, 2, 0)),
+        ('D', ('ld', 'p11')),
+        ('V', ('WQ', 1, 1, 0)),
+        ('S', ('WC', 1, 1, 1)),
+        ('PE', ('WT', 1, 2, 1)),
+        ('V', ('TQ', 0, 1, 0)),
+        ('V', ('D', 0, 1, 3)),
+        ('S', ('WC', 1, 2, 0)),
+        ('PE', ('WT', 2, 0, 0)),
+        ('S', ('WC', 1, 2, 1)),
+        ('PE', ('WT', 2, 0, 1)),
+        ('V', ('WQ', 1, 1, 1)),
+        ('S', ('WC', 2, 0, 0)),
+        ('V', ('WQ', 1, 2, 0)),
+        ('PE', ('WT', 2, 1, 0)),
+        ('V', ('WQ', 1, 2, 1)),
+        ('S', ('WC', 2, 0, 1)),
+        ('D', ('S1', 2, 0)),
+        ('V', ('WQ', 2, 0, 0)),
+        ('PE', ('WT', 2, 1, 1)),
+        ('V', ('C', 0, 1, 3)),
+        ('V', ('L', 1, 0, 1)),
+        ('S', ('WC', 2, 1, 0)),
+        ('PE', ('WT', 2, 2, 0)),
+        ('S', ('WC', 2, 1, 1)),
+        ('V', ('WQ', 2, 0, 1)),
+        ('PE', ('WT', 2, 2, 1)),
+        ('D', ('S1', 2, 2)),
+        ('V', ('WQ', 2, 1, 0)),
+        ('S', ('WC', 2, 2, 0)),
+        ('V', ('F', 0, 1, 3)),
+        ('PE', ('WT', 0, 0, 0)),
+        ('S', ('WC', 2, 2, 1)),
+        ('PE', ('WT', 0, 0, 1)),
+        ('V', ('WQ', 2, 1, 1)),
+        ('D', ('S1', 2, 4)),
+        ('V', ('DI', 0, 1)),
+        ('S', ('X1', 2, 8)),
+        ('PE', ('DT', 0, 1, 1)),
+        ('S', ('WC', 0, 0, 0)),
+        ('D', ('S1', 2, 6)),
+        ('S', ('X1', 2, 10)),
+        ('PE', ('WT', 0, 1, 0)),
+        ('V', ('WQ', 2, 2, 0)),
+        ('V', ('DQ', 0, 1)),
+        ('S', ('DC', 0, 1, 1)),
+        ('D', ('S1', 2, 8)),
+        ('V', ('WQ', 2, 2, 1)),
+        ('S', ('WC', 0, 0, 1)),
+        ('PE', ('O1', 0, 0)),
+        ('V', ('TQ', 0, 1, 1)),
+        ('V', ('D', 1, 0, 0)),
+        ('S', ('WC', 0, 1, 0)),
+        ('PE', ('O1', 0, 1)),
+        ('D', ('S1', 2, 10)),
+        ('S', ('X1', 0, 0)),
+        ('PE', ('O1', 0, 2)),
+        ('V', ('L', 1, 0, 2)),
+        ('S', ('X1', 0, 1)),
+        ('PE', ('O1', 0, 3)),
+        ('V', ('C', 1, 0, 0)),
+        ('V', ('D', 1, 0, 1)),
+        ('S', ('X1', 0, 2)),
+        ('D', ('S1', 0, 0)),
+        ('PE', ('O1', 0, 4)),
+        ('S', ('X1', 0, 3)),
+        ('PE', ('O1', 0, 5)),
+        ('V', ('F', 1, 0, 0)),
+        ('S', ('X1', 0, 4)),
+        ('D', ('S1', 0, 2)),
+        ('PE', ('O1', 0, 6)),
+        ('V', ('C', 1, 0, 1)),
+        ('V', ('L', 1, 0, 3)),
+        ('S', ('X1', 0, 5)),
+        ('PE', ('O1', 0, 7)),
+        ('V', ('F', 1, 0, 1)),
+        ('S', ('X1', 0, 6)),
+        ('PE', ('O1', 0, 8)),
+        ('D', ('S1', 0, 4)),
+        ('V', ('D', 1, 0, 2)),
+        ('S', ('X1', 0, 7)),
+        ('PE', ('O1', 0, 9)),
+        ('S', ('X1', 0, 8)),
+        ('PE', ('O1', 0, 10)),
+        ('V', ('L', 1, 1, 0)),
+        ('D', ('S1', 0, 6)),
+        ('S', ('X1', 0, 9)),
+        ('PE', ('O1', 0, 11)),
+        ('V', ('C', 1, 0, 2)),
+        ('V', ('D', 1, 0, 3)),
+        ('S', ('X1', 0, 10)),
+        ('PE', ('DT', 1, 0, 0)),
+        ('D', ('S1', 0, 8)),
+        ('S', ('X1', 0, 11)),
+        ('V', ('F', 1, 0, 2)),
+        ('PE', ('WT', 0, 1, 1)),
+        ('S', ('DC', 1, 0, 0)),
+        ('V', ('C', 1, 0, 3)),
+        ('V', ('WQ', 0, 0, 0)),
+        ('PE', ('WT', 0, 2, 0)),
+        ('D', ('S1', 0, 10)),
+        ('S', ('WC', 0, 1, 1)),
+        ('V', ('F', 1, 0, 3)),
+        ('PE', ('WT', 0, 2, 1)),
+        ('S', ('WC', 0, 2, 0)),
+        ('V', ('TQ', 1, 0, 0)),
+        ('PE', ('DT', 1, 0, 1)),
+        ('V', ('WQ', 0, 0, 1)),
+        ('S', ('DI', 1, 0)),
+        ('V', ('WQ', 0, 1, 0)),
+        ('PE', ('O0', 0, 0, 1)),
+        ('V', ('L', 1, 1, 1)),
+        ('V', ('DC', 1, 0, 1)),
+        ('PE', ('O0', 0, 0, 2)),
+        ('V', ('WQ', 0, 1, 1)),
+        ('V', ('TQ', 1, 0, 1)),
+        ('PE', ('O0', 0, 1, 1)),
+        ('V', ('WQ', 0, 2, 0)),
+        ('V', ('D', 1, 1, 0)),
+        ('S', ('WC', 0, 2, 1)),
+        ('PE', ('O0', 0, 1, 2)),
+        ('S', ('X0', 0, 0, 1)),
+        ('V', ('DQ', 1, 0)),
+        ('S', ('X0', 0, 0, 2)),
+        ('PE', ('O0', 0, 2, 1)),
+        ('V', ('WQ', 0, 2, 1)),
+        ('S', ('X0', 0, 1, 1)),
+        ('V', ('C', 1, 1, 0)),
+        ('V', ('L', 1, 1, 2)),
+        ('PE', ('O0', 0, 0, 0)),
+        ('S', ('X0', 0, 1, 2)),
+        ('V', ('F', 1, 1, 0)),
+        ('S', ('X0', 0, 2, 1)),
+        ('PE', ('O0', 0, 1, 0)),
+        ('V', ('D', 1, 1, 1)),
+        ('S', ('X0', 0, 0, 0)),
+        ('PE', ('O0', 0, 2, 0)),
+        ('D', ('S0', 0, 0)),
+        ('V', ('L', 1, 1, 3)),
+        ('S', ('X0', 0, 1, 0)),
+        ('V', ('C', 1, 1, 1)),
+        ('PE', ('O0', 0, 2, 2)),
+        ('V', ('D', 1, 1, 2)),
+        ('S', ('X0', 0, 2, 0)),
+        ('PE', ('O0', 0, 3, 0)),
+        ('V', ('F', 1, 1, 1)),
+        ('S', ('X0', 0, 2, 2)),
+        ('D', ('S0', 0, 1)),
+        ('V', ('C', 1, 1, 2)),
+        ('V', ('D', 1, 1, 3)),
+        ('PE', ('DT', 1, 1, 0)),
+        ('S', ('X0', 0, 3, 0)),
+        ('PE', ('O0', 0, 3, 1)),
+        ('V', ('F', 1, 1, 2)),
+        ('S', ('DC', 1, 1, 0)),
+        ('D', ('S0', 0, 2)),
+        ('V', ('C', 1, 1, 3)),
+        ('V', ('TQ', 1, 1, 0)),
+        ('PE', ('O0', 0, 3, 2)),
+        ('V', ('F', 1, 1, 3)),
+        ('S', ('X0', 0, 3, 1)),
+        ('PE', ('O0', 1, 0, 0)),
+        ('V', ('DI', 1, 1)),
+        ('S', ('X0', 0, 3, 2)),
+        ('D', ('S0', 0, 3)),
+        ('PE', ('DT', 1, 1, 1)),
+        ('S', ('X0', 1, 0, 0)),
+        ('V', ('DQ', 1, 1)),
+        ('PE', ('O0', 1, 0, 1)),
+        ('S', ('DC', 1, 1, 1)),
+        ('V', ('TQ', 1, 1, 1)),
+        ('PE', ('O1', 1, 0)),
+        ('V', ('X0', 1, 0, 1)),
+        ('PE', ('O1', 1, 1)),
+        ('V', ('X1', 1, 0)),
+        ('PE', ('O1', 1, 2)),
+        ('V', ('X1', 1, 1)),
+        ('PE', ('O1', 1, 3)),
+        ('V', ('X1', 1, 2)),
+        ('D', ('S1', 1, 0)),
+        ('PE', ('O1', 1, 4)),
+        ('V', ('X1', 1, 3)),
+        ('PE', ('O1', 1, 5)),
+        ('V', ('X1', 1, 4)),
+        ('D', ('S1', 1, 2)),
+        ('PE', ('O1', 1, 6)),
+        ('V', ('X1', 1, 5)),
+        ('PE', ('O1', 1, 7)),
+        ('V', ('X1', 1, 6)),
+        ('D', ('S1', 1, 4)),
+        ('PE', ('O1', 1, 8)),
+        ('S', ('X1', 1, 7)),
+        ('PE', ('O1', 1, 9)),
+        ('V', ('X1', 1, 8)),
+        ('D', ('S1', 1, 6)),
+        ('PE', ('O1', 1, 10)),
+        ('S', ('X1', 1, 9)),
+        ('PE', ('O1', 1, 11)),
+        ('V', ('X1', 1, 10)),
+        ('PE', ('O0', 1, 0, 2)),
+        ('D', ('S1', 1, 8)),
+        ('S', ('X1', 1, 11)),
+        ('PE', ('O0', 1, 1, 0)),
+        ('V', ('X0', 1, 0, 2)),
+        ('D', ('S1', 1, 10)),
+        ('PE', ('O0', 1, 1, 1)),
+        ('V', ('X0', 1, 1, 0)),
+        ('D', ('S0', 1, 0)),
+        ('PE', ('O0', 1, 1, 2)),
+        ('V', ('X0', 1, 1, 1)),
+        ('PE', ('O0', 1, 2, 0)),
+        ('V', ('X0', 1, 1, 2)),
+        ('PE', ('O0', 1, 2, 1)),
+        ('D', ('S0', 1, 1)),
+        ('V', ('X0', 1, 2, 0)),
+        ('PE', ('O0', 1, 2, 2)),
+        ('V', ('X0', 1, 2, 1)),
+        ('PE', ('O0', 1, 3, 0)),
+        ('V', ('X0', 1, 2, 2)),
+        ('PE', ('O0', 1, 3, 1)),
+        ('D', ('S0', 1, 2)),
+        ('V', ('X0', 1, 3, 0)),
+        ('PE', ('O0', 1, 3, 2)),
+        ('V', ('X0', 1, 3, 1)),
+        ('V', ('X0', 1, 3, 2)),
+        ('D', ('S0', 1, 3)),
+    ]
+
+    with ExitStack() as ctx:
+        keep = ctx.enter_context(tc.tile_pool(name="keep", bufs=1))
+        raws = ctx.enter_context(tc.tile_pool(name="raws", bufs=1))
+        work = ctx.enter_context(tc.tile_pool(name="work", bufs=2))
+        outs = ctx.enter_context(tc.tile_pool(name="outs", bufs=8))
+        tps = ctx.enter_context(tc.psum_pool(name="tps", bufs=TP_BUFS))
+        accs = ctx.enter_context(tc.psum_pool(name="accs", bufs=ACC_BUFS))
+        ctx.enter_context(tc.manual_schedule())
+
+        dz_codes = [keep.tile([P, FEAT], U32, align_bytes=64, name=f"dzc{g}") for g in range(GROUPS)]
+        dz_scales = [keep.tile([P, FEAT], U8, align_bytes=64, name=f"dzs{g}") for g in range(GROUPS)]
+        vid_codes = [keep.tile([P, DIM], U32, align_bytes=64, name=f"vc{g}") for g in range(GROUPS)]
+        vid_scales = [keep.tile([P, DIM], U8, align_bytes=64, name=f"vs{g}") for g in range(GROUPS)]
+        dzt_codes = [keep.tile([P, TOK], U32, align_bytes=64, name=f"dtc{f}") for f in range(3)]
+        dzt_scales = [keep.tile([P, TOK], U8, align_bytes=64, name=f"dts{f}") for f in range(3)]
+        w_codes = [keep.tile([P, DIM], U32, align_bytes=64, name=f"wc{f}") for f in range(3)]
+        w_scales = [keep.tile([P, DIM], U8, align_bytes=64, name=f"ws{f}") for f in range(3)]
+
+        gains_row = keep.tile([P, 2 * HD], BF16, name="gains_row")
+        nc.vector.memset(gains_row[:], 0.0)
+        nc.scalar.dma_start(out=gains_row[0:1, 0:HD], in_=q_scale.unsqueeze(0))
+        nc.scalar.dma_start(out=gains_row[0:1, HD : 2 * HD], in_=k_scale.unsqueeze(0))
+        rstd = keep.tile([P, GROUPS, J * 2 * HEADS], F32, name="rstd")
+        nc.scalar.dma_start(out=rstd[:], in_=qk_rstd.rearrange("(g p j) c h -> p g (j c h)", g=GROUPS, j=J))
+
+        def load_grad(grad, name):
+            raw = raws.tile([P, GROUPS, J * INNER], BF16, name=name)
+            for n in range(2):
+                rows = grad[n].rearrange("(g x b j) h d -> b x g (j h d)", g=GROUPS, b=2, j=J)
+                for b in range(2):
+                    nc.sync.dma_start(out=raw[2 * n + b : P : 4, :, :], in_=rows[b])
+            return raw
+
+        vid_raw = {}
+        pre_raw = {}
+        w_raw = {}
+        grad_raw = {}
+        vid_rows = vid.rearrange("(g p j) w -> g p j w", g=GROUPS, j=J)
+        pre_rows = qk_pre.rearrange("(g p j) c h d -> g c p j (h d)", g=GROUPS, j=J)
+        w_rows = w_qkv.rearrange("(n i r) f -> n r i f", n=3, i=4)
+
+        def load_vid(g):
+            vid_raw[g] = raws.tile([P, J, DIM], BF16, tag="big", bufs=BIG_BUFS, name=f"vid{g}")
+            for c in range(3):
+                cols = slice(c * 512, (c + 1) * 512)
+                nc.sync.dma_start(out=vid_raw[g][:, :, cols], in_=vid_rows[g][:, :, cols])
+
+        def load_w(n):
+            w_raw[n] = raws.tile([P, 4, FEAT], BF16, tag="big", bufs=BIG_BUFS, name=f"w{n}")
+            for h in range(2):
+                nc.sync.dma_start(out=w_raw[n][:, 2 * h : 2 * h + 2, :], in_=w_rows[n][:, 2 * h : 2 * h + 2, :])
+
+        def load_pre(f, g):
+            t = raws.tile([P, J, INNER], F32, tag="pre", bufs=PRE_BUFS, name=f"pre{f}{g}")
+            for h in range(2):
+                nc.sync.dma_start(out=t[:, 2 * h : 2 * h + 2, :], in_=pre_rows[g, f][:, 2 * h : 2 * h + 2, :])
+            pre_raw[f, g] = t
+
+        def load(name):
+            k = [int(x) for x in name[1:]]
+            if name[0] == "g":
+                grad_raw[k[0]] = load_grad((grad_q, grad_k, grad_v)[k[0]], f"grad{k[0]}")
+            elif name[0] == "v":
+                load_vid(*k)
+            elif name[0] == "w":
+                load_w(*k)
+            else:
+                load_pre(*k)
+
+        ident = keep.tile([P, P], F32, name="ident")
+        make_identity(nc, ident[:])
+        ones = keep.tile([P, P], BF16, name="ones")
+        nc.vector.memset(ones[:], 1.0)
+        ident_bf = keep.tile([P, P], BF16, name="ident_bf")
+        make_identity(nc, ident_bf[:])
+        warm = keep.tile([P, 1], F32, name="warm")
+        nc.vector.memset(warm[:], 0.0)
+        nc.scalar.copy(warm[:], warm[:])
+        gains = keep.tile([P, 2 * HD], F32, name="gains")
+        gains_ps = tps.tile([P, 2 * HD], F32, tag="tp", name="gains_ps")
+        nc.tensor.matmul(gains_ps[:], lhsT=ones[:], rhs=gains_row[:], start=True, stop=True)
+        nc.scalar.copy(gains[:], gains_ps[:])
+        nr2 = keep.tile([P, GROUPS, J * 2 * HEADS], F32, name="nr2")
+        nc.vector.scalar_tensor_tensor(out=nr2[:], in0=rstd[:], scalar=-1.0 / HD, in1=rstd[:], op0=MULT, op1=MULT)
+
+        t_inter, t_bank, t_grp, t_acc, t_res = {}, {}, {}, {}, {}
+        dz_tiles, lead, sums, coef = {}, {}, {}, {}
+
+        def copy(engine, dst, src):
+            if engine == "V":
+                nc.vector.tensor_copy(out=dst, in_=src)
+            else:
+                nc.scalar.copy(dst, src)
+
+        def il_source(kind, a, c):
+            if kind == "VI":
+                return vid_raw[a][:, :, c * 512 : (c + 1) * 512]
+            if a == 2:
+                return grad_raw[2][:, c, :].rearrange("p (j w) -> p j w", j=J)
+            return dz_tiles[a, c][:]
+
+        def new_inter(key):
+            t_inter[key] = work.tile([P, J * INNER], BF16, align_bytes=64, tag="inter", bufs=INTER_BUFS, name="inter")
+            return t_inter[key]
+
+        def il_direct(engine, kind, a, c):
+            copy(
+                engine,
+                new_inter((kind, a, c))[:].rearrange("p (c i t) -> p c t i", i=4, t=J),
+                il_source(kind, a, c).rearrange("p t (c i) -> p c t i", i=4),
+            )
+
+        def il_tensor(kind, a, c, h):
+            bank = tps.tile([P, 1024], BF16, tag="tp", name="bank")
+            t_bank["PI", kind, a, c, h] = bank
+            src = il_source(kind, a, c).rearrange("p t w -> p w t")
+            for q in range(2):
+                lo = 256 * h + 128 * q
+                nc.tensor.matmul(
+                    bank[:, 512 * q : 512 * (q + 1)].rearrange("p (w t) -> p w t", t=J),
+                    lhsT=ident_bf[:],
+                    rhs=src[:, lo : lo + 128, :],
+                    start=True,
+                    stop=True,
+                )
+
+        def il_copy(engine, kind, a, c, h):
+            if h == 0:
+                new_inter((kind, a, c))
+            copy(engine, t_inter[kind, a, c][:, 1024 * h : 1024 * (h + 1)], t_bank.pop(("PI", kind, a, c, h))[:])
+
+        def quantize(codes, scales, src, fmt):
+            nc.vector.quantize_mx(out=codes.bitcast(fmt), scales=scales, in_=src)
+
+        def vid_quantize(g, c):
+            cols = slice(c * 512, (c + 1) * 512)
+            quantize(vid_codes[g][:, cols], vid_scales[g][:, cols], t_inter.pop(("VI", g, c))[:], E4M3X4)
+
+        def dz_quantize(f, g):
+            cols = slice(f * 512, (f + 1) * 512)
+            quantize(dz_codes[g][:, cols], dz_scales[g][:, cols], t_inter.pop(("DI", f, g))[:], E5M2X4)
+
+        def transposes(key, words):
+            bank = tps.tile([P, 2, 256], F32, tag="tp", name="bank")
+            t_bank[key] = bank
+            for jj in range(2):
+                for u in range(2):
+                    nc.tensor.transpose(bank[:, u, jj * P : (jj + 1) * P], words[:, jj, u : 256 : 2], ident[:])
+
+        def transposed_copy(engine, key):
+            t = work.tile([P, 1024], BF16, align_bytes=64, tag="grouped", bufs=GROUPED_BUFS, name="grouped")
+            t_grp[key] = t
+            dst = t[:].bitcast(F32).rearrange("p (r u) -> p r u", u=2)
+            copy(engine, dst, t_bank.pop(key)[:].rearrange("p u r -> p r u"))
+
+        def dz_transpose(f, g, h):
+            if f == 2:
+                words = grad_raw[2][:, g, :].bitcast(F32).rearrange("p (j w) -> p j w", j=J)
+            else:
+                words = dz_tiles[f, g][:].bitcast(F32)
+            transposes(("D", f, g, h), words[:, 2 * h : 2 * h + 2, :])
+
+        def dzt_quantize(f, g, h):
+            cols = slice(g * 512 + h * 256, g * 512 + (h + 1) * 256)
+            quantize(dzt_codes[f][:, cols], dzt_scales[f][:, cols], t_grp.pop(("D", f, g, h))[:], E5M2X4)
+
+        def w_transpose(n, f, h):
+            words = w_raw[n][:].bitcast(F32)
+            transposes(("W", n, f, h), words[:, 2 * h : 2 * h + 2, 256 * f : 256 * (f + 1)])
+
+        def w_quantize(n, f, h):
+            cols = slice(n * 512 + h * 256, n * 512 + (h + 1) * 256)
+            quantize(w_codes[f][:, cols], w_scales[f][:, cols], t_grp.pop(("W", n, f, h))[:], E4M3X4)
+
+        def out1(f, i):
+            acc = accs.tile([P, 512], F32, tag="acc", name="acc")
+            t_acc[1, f, i] = acc
+            for g in range(GROUPS):
+                nc.tensor.matmul_mx(
+                    out=acc[:],
+                    lhsT=vid_codes[g][:, i * P : (i + 1) * P].bitcast(E4M3X4),
+                    lhsT_scale=vid_scales[g][:, i * P : (i + 1) * P],
+                    rhs=dz_codes[g][:, f * 512 : (f + 1) * 512].bitcast(E5M2X4),
+                    rhs_scale=dz_scales[g][:, f * 512 : (f + 1) * 512],
+                    start=(g == 0),
+                    stop=(g == GROUPS - 1),
+                )
+
+        def out1_copy(engine, f, i):
+            if (1, f, i // 2) not in t_res:
+                t_res[1, f, i // 2] = outs.tile([P, 3, 512], F32, tag="res", bufs=RES_BUFS, name="res")
+            copy(engine, t_res[1, f, i // 2][:, i % 2, :], t_acc.pop((1, f, i))[:])
+
+        def out1_store(f, i):
+            rows = out_1[i * P : (i + 2) * P, f * 512 : (f + 1) * 512]
+            nc.sync.dma_start(out=rows.rearrange("(a p) w -> p a w", p=P), in_=t_res[1, f, i // 2][:, 0:2, :])
+
+        out0_rows = out_0.rearrange("(g p j) w -> g j p w", g=GROUPS, j=J)
+
+        def out0(g, j, n):
+            cols = slice((J * g + j) * P, (J * g + j + 1) * P)
+            acc = accs.tile([P, 512], F32, tag="acc", name="acc")
+            t_acc[0, g, j, n] = acc
+            order = (2, 0, 1)
+            for f in order:
+                nc.tensor.matmul_mx(
+                    out=acc[:],
+                    lhsT=dzt_codes[f][:, cols].bitcast(E5M2X4),
+                    lhsT_scale=dzt_scales[f][:, cols],
+                    rhs=w_codes[f][:, n * 512 : (n + 1) * 512].bitcast(E4M3X4),
+                    rhs_scale=w_scales[f][:, n * 512 : (n + 1) * 512],
+                    start=(f == order[0]),
+                    stop=(f == order[-1]),
+                )
+
+        def out0_copy(engine, g, j, n):
+            if (0, g, j) not in t_res:
+                t_res[0, g, j] = outs.tile([P, 3, 512], F32, tag="res", bufs=RES_BUFS, name="res")
+            copy(engine, t_res[0, g, j][:, n, :], t_acc.pop((0, g, j, n))[:])
+
+        def out0_store(g, j):
+            nc.sync.dma_start(out=out0_rows[g, j], in_=t_res.pop((0, g, j))[:].rearrange("p n w -> p (n w)"))
+
+        def scaled_grad(f, g, j):
+            lead[f, g, j] = work.tile([P, INNER], F32, tag="lead", bufs=LEAD_BUFS, name="lead")
+            for h in range(HEADS):
+                nc.vector.scalar_tensor_tensor(
+                    out=lead[f, g, j][:, h * HD : (h + 1) * HD],
+                    in0=grad_raw[f][:, g, j * INNER + h * HD : j * INNER + (h + 1) * HD],
+                    scalar=rstd[:, g, (2 * j + f) * HEADS + h : (2 * j + f) * HEADS + h + 1],
+                    in1=gains[:, f * HD : (f + 1) * HD],
+                    op0=MULT,
+                    op1=MULT,
+                )
+
+        def dots(f, g, j):
+            s = work.tile([P, HEADS], F32, tag="sums", bufs=3, name="sums")
+            sums[f, g, j] = s
+            for h in range(HEADS):
+                junk = work.tile([P, HD], BF16, tag="junk", bufs=2, name="junk")
+                nc.vector.scalar_tensor_tensor(
+                    out=junk[:],
+                    in0=lead[f, g, j][:, h * HD : (h + 1) * HD],
+                    scalar=1.0,
+                    in1=pre_raw[f, g][:, j, h * HD : (h + 1) * HD],
+                    op0=MULT,
+                    op1=MULT,
+                    accum_out=s[:, h : h + 1],
+                )
+
+        def coefs(f, g, j):
+            c = work.tile([P, HEADS], F32, tag="coefs", bufs=3, name="coefs")
+            coef[f, g, j] = c
+            nc.vector.tensor_tensor(
+                out=c[:],
+                in0=sums.pop((f, g, j))[:],
+                in1=nr2[:, g, (2 * j + f) * HEADS : (2 * j + f + 1) * HEADS],
+                op=MULT,
+            )
+
+        def finish(f, g, j):
+            if j == 0:
+                dz_tiles[f, g] = work.tile([P, J, INNER], BF16, tag="dz", bufs=DZ_BUFS, name="dz")
+            for h in range(HEADS):
+                nc.vector.scalar_tensor_tensor(
+                    out=dz_tiles[f, g][:, j, h * HD : (h + 1) * HD],
+                    in0=pre_raw[f, g][:, j, h * HD : (h + 1) * HD],
+                    scalar=coef[f, g, j][:, h : h + 1],
+                    in1=lead[f, g, j][:, h * HD : (h + 1) * HD],
+                    op0=MULT,
+                    op1=ADD,
+                )
+
+        tasks = {
+            "ld": load,
+            "PI": il_tensor,
+            "VQ": vid_quantize,
+            "DQ": dz_quantize,
+            "DT": dz_transpose,
+            "TQ": dzt_quantize,
+            "WT": w_transpose,
+            "WQ": w_quantize,
+            "O1": out1,
+            "O0": out0,
+            "S1": out1_store,
+            "S0": out0_store,
+            "L": scaled_grad,
+            "D": dots,
+            "C": coefs,
+            "F": finish,
+        }
+        for engine, node in SEQ:
+            t = node[0]
+            if t in ("DI", "VI"):
+                il_direct(engine, *node)
+            elif t == "IC":
+                il_copy(engine, *node[1:])
+            elif t == "X1":
+                out1_copy(engine, *node[1:])
+            elif t == "X0":
+                out0_copy(engine, *node[1:])
+            elif t == "DC":
+                transposed_copy(engine, ("D",) + node[1:])
+            elif t == "WC":
+                transposed_copy(engine, ("W",) + node[1:])
+            else:
+                tasks[t](*node[1:])

@@ -31,355 +31,360 @@ def tile_naswinattention_pa_v_kernel(
 ):
     nc = tc.nc
     TP_BUFS, ACC_BUFS = 3, 5
-    BIG_BUFS, PRE_BUFS, INTER_BUFS, GROUPED_BUFS, RES_BUFS, DZ_BUFS, LEAD_BUFS = 4, 3, 4, 6, 4, 2, 5
+    BIG_BUFS, PRE_BUFS, INTER_BUFS, GROUPED_BUFS, RES_BUFS, DZ_BUFS, LEAD_BUFS, PROD_BUFS = 4, 3, 3, 5, 4, 3, 4, 1
     SEQ = [
-        ('D', ('ld', 'g2')),
         ('D', ('ld', 'g0')),
-        ('V', ('DI', 2, 0)),
-        ('PE', ('PI', 'DI', 2, 1, 0)),
-        ('PE', ('PI', 'DI', 2, 1, 1)),
-        ('S', ('IC', 'DI', 2, 1, 0)),
-        ('PE', ('DT', 2, 0, 0)),
-        ('V', ('IC', 'DI', 2, 1, 1)),
-        ('D', ('ld', 'p00')),
-        ('PE', ('DT', 2, 0, 1)),
-        ('S', ('DC', 2, 0, 0)),
-        ('V', ('DQ', 2, 0)),
-        ('PE', ('DT', 2, 1, 0)),
-        ('S', ('DC', 2, 0, 1)),
-        ('V', ('DQ', 2, 1)),
-        ('PE', ('DT', 2, 1, 1)),
-        ('S', ('DC', 2, 1, 0)),
-        ('V', ('TQ', 2, 0, 0)),
-        ('V', ('TQ', 2, 0, 1)),
-        ('S', ('DC', 2, 1, 1)),
-        ('V', ('TQ', 2, 1, 0)),
-        ('D', ('ld', 'v0')),
+        ('D', ('ld', 'g2')),
         ('V', ('L', 0, 0, 0)),
-        ('V', ('TQ', 2, 1, 1)),
         ('V', ('L', 0, 0, 1)),
-        ('V', ('D', 0, 0, 0)),
+        ('D', ('ld', 'p00')),
         ('V', ('L', 0, 0, 2)),
-        ('V', ('C', 0, 0, 0)),
-        ('V', ('D', 0, 0, 1)),
-        ('D', ('ld', 'p01')),
-        ('V', ('F', 0, 0, 0)),
-        ('PE', ('PI', 'VI', 0, 1, 0)),
-        ('V', ('VI', 0, 0)),
-        ('PE', ('PI', 'VI', 0, 1, 1)),
-        ('S', ('IC', 'VI', 0, 1, 0)),
-        ('PE', ('PI', 'VI', 0, 2, 0)),
-        ('D', ('ld', 'v1')),
-        ('S', ('IC', 'VI', 0, 1, 1)),
-        ('V', ('C', 0, 0, 1)),
         ('V', ('L', 0, 0, 3)),
-        ('PE', ('PI', 'VI', 0, 2, 1)),
+        ('PE', ('DT', 2, 0, 0)),
+        ('V', ('DI', 2, 1)),
+        ('PE', ('DT', 2, 1, 1)),
+        ('S', ('DC', 2, 0, 0)),
+        ('D', ('ld', 'v1')),
+        ('V', ('DQ', 2, 1)),
+        ('PE', ('DT', 2, 0, 1)),
+        ('V', ('TQ', 2, 0, 0)),
+        ('S', ('DC', 2, 1, 1)),
+        ('V', ('DP', 0, 0, 0)),
+        ('V', ('D', 0, 0, 3)),
+        ('PE', ('DT', 2, 1, 0)),
+        ('S', ('D', 0, 0, 0)),
+        ('S', ('DC', 2, 0, 1)),
+        ('V', ('D', 0, 0, 1)),
+        ('PE', ('PI', 'DI', 2, 0, 0)),
+        ('S', ('DC', 2, 1, 0)),
+        ('V', ('TQ', 2, 0, 1)),
+        ('D', ('ld', 'v0')),
+        ('V', ('C', 0, 0, 3)),
+        ('V', ('C', 0, 0, 0)),
+        ('V', ('DP', 0, 0, 2)),
+        ('S', ('IC', 'DI', 2, 0, 0)),
+        ('PE', ('PI', 'DI', 2, 0, 1)),
+        ('V', ('F', 0, 0, 0)),
+        ('S', ('D', 0, 0, 2)),
+        ('V', ('TQ', 2, 1, 1)),
+        ('V', ('L', 0, 1, 0)),
+        ('S', ('VI', 1, 1)),
+        ('V', ('C', 0, 0, 2)),
+        ('V', ('TQ', 2, 1, 0)),
+        ('V', ('C', 0, 0, 1)),
+        ('V', ('IC', 'DI', 2, 0, 1)),
+        ('D', ('ld', 'p01')),
+        ('V', ('F', 0, 0, 1)),
+        ('V', ('DQ', 2, 0)),
+        ('PE', ('DT', 0, 0, 0)),
+        ('S', ('VI', 1, 0)),
+        ('V', ('L', 0, 1, 1)),
+        ('PE', ('PI', 'VI', 0, 1, 0)),
+        ('V', ('VQ', 1, 1)),
+        ('V', ('F', 0, 0, 2)),
+        ('D', ('ld', 'w0')),
+        ('PE', ('PI', 'VI', 0, 2, 0)),
+        ('V', ('L', 0, 1, 2)),
+        ('S', ('IC', 'VI', 0, 1, 0)),
+        ('V', ('D', 0, 1, 0)),
         ('S', ('IC', 'VI', 0, 2, 0)),
-        ('V', ('VQ', 0, 0)),
+        ('PE', ('PI', 'VI', 0, 1, 1)),
+        ('S', ('DC', 0, 0, 0)),
+        ('V', ('D', 0, 1, 1)),
+        ('PE', ('PI', 'VI', 0, 2, 1)),
+        ('S', ('IC', 'VI', 0, 1, 1)),
+        ('V', ('TQ', 0, 0, 0)),
         ('S', ('IC', 'VI', 0, 2, 1)),
         ('V', ('VQ', 0, 1)),
-        ('V', ('VQ', 0, 2)),
-        ('V', ('F', 0, 0, 1)),
-        ('V', ('D', 0, 0, 2)),
-        ('PE', ('DT', 0, 0, 0)),
         ('D', ('ld', 'g1')),
-        ('S', ('DC', 0, 0, 0)),
-        ('V', ('L', 0, 1, 0)),
-        ('S', ('VI', 1, 0)),
-        ('V', ('VI', 1, 1)),
-        ('V', ('TQ', 0, 0, 0)),
-        ('D', ('ld', 'w1')),
-        ('V', ('VQ', 1, 1)),
-        ('V', ('C', 0, 0, 2)),
-        ('V', ('D', 0, 0, 3)),
-        ('PE', ('O1', 2, 4)),
-        ('S', ('VI', 1, 2)),
-        ('PE', ('O1', 2, 5)),
-        ('V', ('VQ', 1, 0)),
-        ('PE', ('O1', 2, 6)),
-        ('V', ('F', 0, 0, 2)),
-        ('PE', ('O1', 2, 0)),
-        ('V', ('C', 0, 0, 3)),
-        ('V', ('L', 0, 1, 1)),
-        ('PE', ('O1', 2, 1)),
-        ('D', ('ld', 'p10')),
-        ('S', ('X1', 2, 0)),
         ('V', ('F', 0, 0, 3)),
-        ('S', ('X1', 2, 1)),
-        ('V', ('VQ', 1, 2)),
-        ('PE', ('O1', 2, 2)),
-        ('S', ('X1', 2, 4)),
-        ('PE', ('O1', 2, 3)),
-        ('V', ('D', 0, 1, 0)),
-        ('S', ('X1', 2, 2)),
-        ('PE', ('O1', 2, 7)),
-        ('V', ('L', 0, 1, 2)),
-        ('D', ('ld', 'w2')),
-        ('S', ('X1', 2, 3)),
-        ('PE', ('O1', 2, 8)),
-        ('V', ('C', 0, 1, 0)),
-        ('S', ('X1', 2, 5)),
-        ('V', ('D', 0, 1, 1)),
-        ('PE', ('O1', 2, 9)),
-        ('S', ('X1', 2, 6)),
-        ('PE', ('O1', 2, 10)),
-        ('V', ('F', 0, 1, 0)),
-        ('S', ('X1', 2, 7)),
-        ('PE', ('O1', 2, 11)),
+        ('S', ('VI', 0, 0)),
+        ('PE', ('O1', 2, 4)),
         ('V', ('C', 0, 1, 1)),
+        ('V', ('C', 0, 1, 0)),
         ('V', ('L', 0, 1, 3)),
-        ('S', ('X1', 2, 9)),
-        ('PE', ('PI', 'DI', 0, 0, 0)),
-        ('S', ('X1', 2, 11)),
-        ('V', ('F', 0, 1, 1)),
-        ('PE', ('PI', 'DI', 0, 0, 1)),
-        ('S', ('IC', 'DI', 0, 0, 0)),
-        ('V', ('D', 0, 1, 2)),
-        ('D', ('ld', 'w0')),
-        ('PE', ('DT', 0, 0, 1)),
-        ('S', ('IC', 'DI', 0, 0, 1)),
-        ('PE', ('WT', 1, 0, 0)),
-        ('V', ('L', 1, 0, 0)),
-        ('S', ('DC', 0, 0, 1)),
-        ('PE', ('WT', 1, 0, 1)),
-        ('V', ('DQ', 0, 0)),
-        ('S', ('WC', 1, 0, 0)),
-        ('PE', ('WT', 1, 1, 0)),
-        ('V', ('TQ', 0, 0, 1)),
-        ('S', ('WC', 1, 0, 1)),
-        ('PE', ('DT', 0, 1, 0)),
-        ('V', ('WQ', 1, 0, 0)),
-        ('S', ('WC', 1, 1, 0)),
-        ('V', ('C', 0, 1, 2)),
-        ('V', ('WQ', 1, 0, 1)),
-        ('PE', ('WT', 1, 1, 1)),
-        ('V', ('F', 0, 1, 2)),
-        ('S', ('DC', 0, 1, 0)),
-        ('PE', ('WT', 1, 2, 0)),
-        ('D', ('ld', 'p11')),
-        ('V', ('WQ', 1, 1, 0)),
-        ('S', ('WC', 1, 1, 1)),
-        ('PE', ('WT', 1, 2, 1)),
-        ('V', ('TQ', 0, 1, 0)),
-        ('V', ('D', 0, 1, 3)),
-        ('S', ('WC', 1, 2, 0)),
-        ('PE', ('WT', 2, 0, 0)),
-        ('S', ('WC', 1, 2, 1)),
-        ('PE', ('WT', 2, 0, 1)),
-        ('V', ('WQ', 1, 1, 1)),
-        ('S', ('WC', 2, 0, 0)),
-        ('V', ('WQ', 1, 2, 0)),
-        ('PE', ('WT', 2, 1, 0)),
-        ('V', ('WQ', 1, 2, 1)),
-        ('S', ('WC', 2, 0, 1)),
-        ('D', ('S1', 2, 0)),
-        ('V', ('WQ', 2, 0, 0)),
-        ('PE', ('WT', 2, 1, 1)),
-        ('V', ('C', 0, 1, 3)),
-        ('V', ('L', 1, 0, 1)),
-        ('S', ('WC', 2, 1, 0)),
-        ('PE', ('WT', 2, 2, 0)),
-        ('S', ('WC', 2, 1, 1)),
-        ('V', ('WQ', 2, 0, 1)),
-        ('PE', ('WT', 2, 2, 1)),
-        ('D', ('S1', 2, 2)),
-        ('V', ('WQ', 2, 1, 0)),
-        ('S', ('WC', 2, 2, 0)),
-        ('V', ('F', 0, 1, 3)),
         ('PE', ('WT', 0, 0, 0)),
-        ('S', ('WC', 2, 2, 1)),
-        ('PE', ('WT', 0, 0, 1)),
-        ('V', ('WQ', 2, 1, 1)),
-        ('D', ('S1', 2, 4)),
-        ('V', ('DI', 0, 1)),
-        ('S', ('X1', 2, 8)),
-        ('PE', ('DT', 0, 1, 1)),
-        ('S', ('WC', 0, 0, 0)),
-        ('D', ('S1', 2, 6)),
-        ('S', ('X1', 2, 10)),
-        ('PE', ('WT', 0, 1, 0)),
-        ('V', ('WQ', 2, 2, 0)),
-        ('V', ('DQ', 0, 1)),
-        ('S', ('DC', 0, 1, 1)),
-        ('D', ('S1', 2, 8)),
-        ('V', ('WQ', 2, 2, 1)),
-        ('S', ('WC', 0, 0, 1)),
-        ('PE', ('O1', 0, 0)),
-        ('V', ('TQ', 0, 1, 1)),
-        ('V', ('D', 1, 0, 0)),
-        ('S', ('WC', 0, 1, 0)),
-        ('PE', ('O1', 0, 1)),
-        ('D', ('S1', 2, 10)),
-        ('S', ('X1', 0, 0)),
-        ('PE', ('O1', 0, 2)),
-        ('V', ('L', 1, 0, 2)),
-        ('S', ('X1', 0, 1)),
-        ('PE', ('O1', 0, 3)),
-        ('V', ('C', 1, 0, 0)),
-        ('V', ('D', 1, 0, 1)),
-        ('S', ('X1', 0, 2)),
-        ('D', ('S1', 0, 0)),
-        ('PE', ('O1', 0, 4)),
-        ('S', ('X1', 0, 3)),
-        ('PE', ('O1', 0, 5)),
-        ('V', ('F', 1, 0, 0)),
-        ('S', ('X1', 0, 4)),
-        ('D', ('S1', 0, 2)),
-        ('PE', ('O1', 0, 6)),
-        ('V', ('C', 1, 0, 1)),
-        ('V', ('L', 1, 0, 3)),
-        ('S', ('X1', 0, 5)),
-        ('PE', ('O1', 0, 7)),
-        ('V', ('F', 1, 0, 1)),
-        ('S', ('X1', 0, 6)),
-        ('PE', ('O1', 0, 8)),
-        ('D', ('S1', 0, 4)),
-        ('V', ('D', 1, 0, 2)),
-        ('S', ('X1', 0, 7)),
-        ('PE', ('O1', 0, 9)),
-        ('S', ('X1', 0, 8)),
-        ('PE', ('O1', 0, 10)),
-        ('V', ('L', 1, 1, 0)),
-        ('D', ('S1', 0, 6)),
-        ('S', ('X1', 0, 9)),
-        ('PE', ('O1', 0, 11)),
-        ('V', ('C', 1, 0, 2)),
-        ('V', ('D', 1, 0, 3)),
-        ('S', ('X1', 0, 10)),
-        ('PE', ('DT', 1, 0, 0)),
-        ('D', ('S1', 0, 8)),
-        ('S', ('X1', 0, 11)),
-        ('V', ('F', 1, 0, 2)),
-        ('PE', ('WT', 0, 1, 1)),
-        ('S', ('DC', 1, 0, 0)),
-        ('V', ('C', 1, 0, 3)),
-        ('V', ('WQ', 0, 0, 0)),
+        ('V', ('F', 0, 1, 0)),
         ('PE', ('WT', 0, 2, 0)),
-        ('D', ('S1', 0, 10)),
-        ('S', ('WC', 0, 1, 1)),
-        ('V', ('F', 1, 0, 3)),
-        ('PE', ('WT', 0, 2, 1)),
+        ('PE', ('WT', 0, 1, 1)),
+        ('V', ('DP', 0, 1, 3)),
+        ('D', ('ld', 'w2')),
+        ('V', ('F', 0, 1, 1)),
+        ('S', ('WC', 0, 0, 0)),
+        ('PE', ('O1', 2, 5)),
+        ('V', ('VQ', 0, 0)),
         ('S', ('WC', 0, 2, 0)),
-        ('V', ('TQ', 1, 0, 0)),
-        ('PE', ('DT', 1, 0, 1)),
-        ('V', ('WQ', 0, 0, 1)),
-        ('S', ('DI', 1, 0)),
-        ('V', ('WQ', 0, 1, 0)),
-        ('PE', ('O0', 0, 0, 1)),
-        ('V', ('L', 1, 1, 1)),
-        ('V', ('DC', 1, 0, 1)),
-        ('PE', ('O0', 0, 0, 2)),
-        ('V', ('WQ', 0, 1, 1)),
-        ('V', ('TQ', 1, 0, 1)),
-        ('PE', ('O0', 0, 1, 1)),
-        ('V', ('WQ', 0, 2, 0)),
-        ('V', ('D', 1, 1, 0)),
+        ('PE', ('O1', 2, 6)),
+        ('S', ('D', 0, 1, 3)),
+        ('V', ('L', 1, 0, 0)),
+        ('PE', ('WT', 0, 1, 0)),
+        ('V', ('DI', 0, 0)),
+        ('PE', ('WT', 0, 2, 1)),
+        ('S', ('X1', 2, 6)),
+        ('S', ('WC', 0, 1, 1)),
+        ('PE', ('O1', 2, 7)),
+        ('D', ('ld', 'w1')),
         ('S', ('WC', 0, 2, 1)),
-        ('PE', ('O0', 0, 1, 2)),
-        ('S', ('X0', 0, 0, 1)),
-        ('V', ('DQ', 1, 0)),
-        ('S', ('X0', 0, 0, 2)),
-        ('PE', ('O0', 0, 2, 1)),
+        ('V', ('L', 1, 0, 1)),
+        ('PE', ('WT', 0, 0, 1)),
+        ('S', ('WC', 0, 1, 0)),
+        ('V', ('WQ', 0, 1, 1)),
+        ('PE', ('DT', 0, 0, 1)),
+        ('V', ('WQ', 0, 0, 0)),
+        ('S', ('X1', 2, 7)),
+        ('PE', ('WT', 2, 2, 0)),
+        ('V', ('WQ', 0, 1, 0)),
+        ('S', ('DC', 0, 0, 1)),
+        ('V', ('DQ', 0, 0)),
+        ('S', ('WC', 0, 0, 1)),
         ('V', ('WQ', 0, 2, 1)),
-        ('S', ('X0', 0, 1, 1)),
-        ('V', ('C', 1, 1, 0)),
-        ('V', ('L', 1, 1, 2)),
+        ('PE', ('WT', 2, 1, 0)),
+        ('V', ('TQ', 0, 0, 1)),
+        ('S', ('VI', 1, 2)),
+        ('PE', ('WT', 2, 2, 1)),
+        ('V', ('WQ', 0, 0, 1)),
+        ('V', ('C', 0, 1, 3)),
+        ('V', ('X1', 2, 4)),
+        ('D', ('S1', 2, 6)),
+        ('V', ('VQ', 1, 0)),
+        ('V', ('VQ', 0, 2)),
+        ('PE', ('O1', 2, 0)),
+        ('D', ('ld', 'p11')),
+        ('V', ('D', 0, 1, 2)),
+        ('S', ('WC', 2, 1, 0)),
+        ('PE', ('O1', 2, 2)),
+        ('S', ('X1', 2, 5)),
+        ('V', ('VQ', 1, 2)),
+        ('S', ('X1', 2, 0)),
+        ('PE', ('WT', 1, 0, 1)),
+        ('V', ('C', 0, 1, 2)),
+        ('V', ('WQ', 2, 1, 0)),
+        ('V', ('F', 0, 1, 2)),
+        ('S', ('X1', 2, 2)),
+        ('PE', ('O1', 2, 10)),
+        ('D', ('S1', 2, 4)),
+        ('V', ('WQ', 0, 2, 0)),
+        ('S', ('WC', 2, 2, 1)),
+        ('PE', ('O1', 2, 1)),
+        ('V', ('F', 0, 1, 3)),
+        ('S', ('WC', 2, 2, 0)),
+        ('PE', ('WT', 2, 0, 0)),
+        ('V', ('L', 1, 0, 2)),
+        ('D', ('ld', 'p10')),
+        ('S', ('DI', 0, 1)),
+        ('PE', ('WT', 1, 2, 1)),
+        ('V', ('X1', 2, 1)),
+        ('V', ('L', 1, 0, 3)),
+        ('PE', ('O1', 2, 11)),
+        ('PE', ('O1', 2, 3)),
+        ('V', ('WQ', 2, 2, 1)),
+        ('V', ('WQ', 2, 2, 0)),
+        ('PE', ('O1', 2, 8)),
+        ('V', ('WC', 2, 0, 0)),
+        ('D', ('S1', 2, 0)),
+        ('S', ('WC', 1, 2, 1)),
+        ('V', ('DQ', 0, 1)),
+        ('PE', ('WT', 1, 0, 0)),
+        ('S', ('WC', 1, 0, 1)),
+        ('V', ('WQ', 2, 0, 0)),
+        ('PE', ('WT', 1, 1, 0)),
+        ('V', ('X1', 2, 10)),
+        ('S', ('X1', 2, 3)),
+        ('PE', ('O1', 2, 9)),
+        ('V', ('DP', 1, 0, 2)),
+        ('S', ('WC', 1, 0, 0)),
+        ('D', ('S1', 2, 2)),
+        ('PE', ('O1', 0, 6)),
+        ('V', ('WQ', 1, 0, 1)),
+        ('S', ('WC', 1, 1, 0)),
+        ('V', ('WQ', 1, 0, 0)),
+        ('PE', ('O1', 0, 8)),
+        ('S', ('D', 1, 0, 2)),
+        ('V', ('D', 1, 0, 0)),
+        ('PE', ('DT', 0, 1, 0)),
+        ('S', ('X1', 2, 11)),
+        ('V', ('C', 1, 0, 2)),
+        ('V', ('DP', 1, 0, 1)),
+        ('PE', ('WT', 1, 1, 1)),
+        ('S', ('X1', 0, 8)),
+        ('D', ('S1', 2, 10)),
+        ('V', ('C', 1, 0, 0)),
+        ('V', ('WQ', 1, 1, 0)),
+        ('PE', ('WT', 2, 1, 1)),
+        ('S', ('DC', 0, 1, 0)),
+        ('V', ('F', 1, 0, 0)),
+        ('S', ('D', 1, 0, 1)),
+        ('PE', ('O1', 0, 9)),
+        ('V', ('TQ', 0, 1, 0)),
+        ('V', ('WQ', 1, 2, 1)),
+        ('S', ('WC', 2, 1, 1)),
+        ('PE', ('WT', 2, 0, 1)),
+        ('V', ('DP', 1, 0, 3)),
+        ('S', ('WC', 1, 1, 1)),
+        ('V', ('C', 1, 0, 1)),
+        ('PE', ('O1', 0, 4)),
+        ('V', ('WQ', 2, 1, 1)),
+        ('V', ('F', 1, 0, 1)),
+        ('S', ('WC', 2, 0, 1)),
+        ('PE', ('WT', 1, 2, 0)),
+        ('V', ('WQ', 1, 1, 1)),
+        ('S', ('X1', 0, 9)),
+        ('PE', ('DT', 1, 0, 0)),
+        ('V', ('WQ', 2, 0, 1)),
+        ('S', ('X1', 0, 4)),
+        ('V', ('WC', 1, 2, 0)),
+        ('D', ('S1', 0, 8)),
+        ('PE', ('O1', 0, 5)),
+        ('S', ('X1', 0, 6)),
+        ('V', ('DC', 1, 0, 0)),
+        ('PE', ('O1', 0, 0)),
+        ('S', ('X1', 2, 8)),
+        ('V', ('WQ', 1, 2, 0)),
+        ('V', ('TQ', 1, 0, 0)),
+        ('PE', ('O1', 0, 2)),
+        ('S', ('X1', 0, 5)),
+        ('V', ('F', 1, 0, 2)),
+        ('PE', ('O1', 0, 1)),
+        ('S', ('X1', 2, 9)),
+        ('D', ('S1', 0, 4)),
+        ('V', ('L', 1, 1, 0)),
         ('PE', ('O0', 0, 0, 0)),
-        ('S', ('X0', 0, 1, 2)),
-        ('V', ('F', 1, 1, 0)),
-        ('S', ('X0', 0, 2, 1)),
-        ('PE', ('O0', 0, 1, 0)),
-        ('V', ('D', 1, 1, 1)),
+        ('S', ('X1', 0, 0)),
+        ('V', ('L', 1, 1, 1)),
+        ('S', ('D', 1, 0, 3)),
+        ('PE', ('O1', 0, 3)),
+        ('D', ('S1', 2, 8)),
+        ('V', ('D', 1, 1, 0)),
+        ('S', ('X1', 0, 1)),
+        ('PE', ('O0', 0, 0, 2)),
+        ('V', ('C', 1, 0, 3)),
+        ('V', ('L', 1, 1, 2)),
         ('S', ('X0', 0, 0, 0)),
-        ('PE', ('O0', 0, 2, 0)),
+        ('PE', ('O0', 0, 0, 1)),
+        ('D', ('S1', 0, 0)),
+        ('V', ('F', 1, 0, 3)),
+        ('PE', ('O0', 0, 1, 0)),
+        ('V', ('X0', 0, 0, 2)),
+        ('S', ('X0', 0, 0, 1)),
+        ('V', ('X1', 0, 2)),
         ('D', ('S0', 0, 0)),
-        ('V', ('L', 1, 1, 3)),
+        ('PE', ('DT', 1, 0, 1)),
+        ('V', ('DI', 1, 0)),
+        ('S', ('X1', 0, 3)),
+        ('PE', ('O0', 0, 1, 1)),
         ('S', ('X0', 0, 1, 0)),
-        ('V', ('C', 1, 1, 1)),
-        ('PE', ('O0', 0, 2, 2)),
-        ('V', ('D', 1, 1, 2)),
-        ('S', ('X0', 0, 2, 0)),
-        ('PE', ('O0', 0, 3, 0)),
-        ('V', ('F', 1, 1, 1)),
-        ('S', ('X0', 0, 2, 2)),
+        ('S', ('DC', 1, 0, 1)),
+        ('PE', ('O0', 0, 1, 2)),
+        ('V', ('L', 1, 1, 3)),
+        ('D', ('S1', 0, 2)),
+        ('S', ('X0', 0, 1, 1)),
+        ('V', ('TQ', 1, 0, 1)),
+        ('PE', ('O1', 0, 7)),
+        ('V', ('DQ', 1, 0)),
+        ('S', ('X0', 0, 1, 2)),
+        ('PE', ('O0', 0, 2, 0)),
+        ('V', ('DP', 1, 1, 3)),
+        ('S', ('X1', 0, 7)),
         ('D', ('S0', 0, 1)),
-        ('V', ('C', 1, 1, 2)),
-        ('V', ('D', 1, 1, 3)),
-        ('PE', ('DT', 1, 1, 0)),
+        ('V', ('C', 1, 1, 0)),
+        ('V', ('D', 1, 1, 2)),
+        ('PE', ('O0', 0, 3, 0)),
+        ('S', ('D', 1, 1, 3)),
+        ('S', ('X0', 0, 2, 0)),
+        ('PE', ('O0', 0, 2, 2)),
+        ('V', ('F', 1, 1, 0)),
+        ('D', ('S1', 0, 6)),
         ('S', ('X0', 0, 3, 0)),
-        ('PE', ('O0', 0, 3, 1)),
-        ('V', ('F', 1, 1, 2)),
-        ('S', ('DC', 1, 1, 0)),
-        ('D', ('S0', 0, 2)),
         ('V', ('C', 1, 1, 3)),
-        ('V', ('TQ', 1, 1, 0)),
-        ('PE', ('O0', 0, 3, 2)),
-        ('V', ('F', 1, 1, 3)),
+        ('V', ('DP', 1, 1, 1)),
+        ('PE', ('O0', 0, 3, 1)),
+        ('V', ('X0', 0, 2, 2)),
+        ('S', ('D', 1, 1, 1)),
+        ('PE', ('O0', 0, 2, 1)),
+        ('V', ('C', 1, 1, 2)),
         ('S', ('X0', 0, 3, 1)),
-        ('PE', ('O0', 1, 0, 0)),
-        ('V', ('DI', 1, 1)),
+        ('V', ('C', 1, 1, 1)),
+        ('V', ('F', 1, 1, 1)),
+        ('PE', ('O0', 0, 3, 2)),
+        ('S', ('X0', 0, 2, 1)),
+        ('V', ('F', 1, 1, 2)),
+        ('PE', ('O1', 0, 10)),
+        ('D', ('S0', 0, 2)),
         ('S', ('X0', 0, 3, 2)),
-        ('D', ('S0', 0, 3)),
+        ('V', ('F', 1, 1, 3)),
+        ('PE', ('DT', 1, 1, 0)),
+        ('S', ('X1', 0, 10)),
         ('PE', ('DT', 1, 1, 1)),
-        ('S', ('X0', 1, 0, 0)),
-        ('V', ('DQ', 1, 1)),
-        ('PE', ('O0', 1, 0, 1)),
-        ('S', ('DC', 1, 1, 1)),
-        ('V', ('TQ', 1, 1, 1)),
-        ('PE', ('O1', 1, 0)),
-        ('V', ('X0', 1, 0, 1)),
-        ('PE', ('O1', 1, 1)),
-        ('V', ('X1', 1, 0)),
-        ('PE', ('O1', 1, 2)),
-        ('V', ('X1', 1, 1)),
-        ('PE', ('O1', 1, 3)),
-        ('V', ('X1', 1, 2)),
-        ('D', ('S1', 1, 0)),
-        ('PE', ('O1', 1, 4)),
-        ('V', ('X1', 1, 3)),
-        ('PE', ('O1', 1, 5)),
-        ('V', ('X1', 1, 4)),
-        ('D', ('S1', 1, 2)),
-        ('PE', ('O1', 1, 6)),
-        ('V', ('X1', 1, 5)),
-        ('PE', ('O1', 1, 7)),
-        ('V', ('X1', 1, 6)),
-        ('D', ('S1', 1, 4)),
-        ('PE', ('O1', 1, 8)),
-        ('S', ('X1', 1, 7)),
-        ('PE', ('O1', 1, 9)),
-        ('V', ('X1', 1, 8)),
-        ('D', ('S1', 1, 6)),
-        ('PE', ('O1', 1, 10)),
-        ('S', ('X1', 1, 9)),
-        ('PE', ('O1', 1, 11)),
-        ('V', ('X1', 1, 10)),
-        ('PE', ('O0', 1, 0, 2)),
-        ('D', ('S1', 1, 8)),
-        ('S', ('X1', 1, 11)),
+        ('S', ('DI', 1, 1)),
+        ('V', ('DC', 1, 1, 0)),
+        ('PE', ('DT', 0, 1, 1)),
+        ('D', ('S0', 0, 3)),
+        ('V', ('TQ', 1, 1, 0)),
+        ('PE', ('O1', 0, 11)),
+        ('V', ('DC', 0, 1, 1)),
+        ('PE', ('O0', 1, 0, 0)),
+        ('V', ('TQ', 0, 1, 1)),
         ('PE', ('O0', 1, 1, 0)),
-        ('V', ('X0', 1, 0, 2)),
-        ('D', ('S1', 1, 10)),
-        ('PE', ('O0', 1, 1, 1)),
+        ('S', ('X1', 0, 11)),
+        ('V', ('DQ', 1, 1)),
+        ('S', ('X0', 1, 0, 0)),
+        ('D', ('S1', 0, 10)),
+        ('PE', ('O1', 1, 0)),
         ('V', ('X0', 1, 1, 0)),
-        ('D', ('S0', 1, 0)),
-        ('PE', ('O0', 1, 1, 2)),
+        ('S', ('DC', 1, 1, 1)),
+        ('PE', ('O0', 1, 1, 1)),
+        ('S', ('X1', 1, 0)),
+        ('V', ('TQ', 1, 1, 1)),
+        ('PE', ('O1', 1, 1)),
         ('V', ('X0', 1, 1, 1)),
-        ('PE', ('O0', 1, 2, 0)),
+        ('PE', ('O0', 1, 1, 2)),
+        ('S', ('X1', 1, 1)),
+        ('PE', ('O1', 1, 2)),
+        ('D', ('S1', 1, 0)),
         ('V', ('X0', 1, 1, 2)),
-        ('PE', ('O0', 1, 2, 1)),
+        ('PE', ('O1', 1, 6)),
+        ('S', ('X1', 1, 2)),
+        ('PE', ('O1', 1, 3)),
         ('D', ('S0', 1, 1)),
-        ('V', ('X0', 1, 2, 0)),
+        ('PE', ('O1', 1, 7)),
+        ('V', ('X1', 1, 3)),
+        ('PE', ('O1', 1, 8)),
+        ('S', ('X1', 1, 6)),
+        ('PE', ('O0', 1, 0, 2)),
+        ('D', ('S1', 1, 2)),
+        ('V', ('X1', 1, 7)),
+        ('PE', ('O1', 1, 9)),
+        ('S', ('X0', 1, 0, 2)),
+        ('V', ('X1', 1, 8)),
+        ('PE', ('O0', 1, 0, 1)),
+        ('D', ('S1', 1, 6)),
+        ('V', ('X1', 1, 9)),
+        ('PE', ('O1', 1, 4)),
+        ('S', ('X0', 1, 0, 1)),
+        ('PE', ('O0', 1, 2, 0)),
+        ('D', ('S1', 1, 8)),
+        ('V', ('X1', 1, 4)),
+        ('PE', ('O1', 1, 5)),
+        ('S', ('X0', 1, 2, 0)),
+        ('D', ('S0', 1, 0)),
         ('PE', ('O0', 1, 2, 2)),
-        ('V', ('X0', 1, 2, 1)),
+        ('S', ('X1', 1, 5)),
+        ('PE', ('O0', 1, 2, 1)),
+        ('S', ('X0', 1, 2, 2)),
+        ('D', ('S1', 1, 4)),
+        ('PE', ('O1', 1, 10)),
+        ('S', ('X0', 1, 2, 1)),
         ('PE', ('O0', 1, 3, 0)),
-        ('V', ('X0', 1, 2, 2)),
-        ('PE', ('O0', 1, 3, 1)),
+        ('V', ('X1', 1, 10)),
         ('D', ('S0', 1, 2)),
+        ('PE', ('O1', 1, 11)),
         ('V', ('X0', 1, 3, 0)),
+        ('PE', ('O0', 1, 3, 1)),
+        ('S', ('X1', 1, 11)),
         ('PE', ('O0', 1, 3, 2)),
-        ('V', ('X0', 1, 3, 1)),
-        ('V', ('X0', 1, 3, 2)),
+        ('D', ('S1', 1, 10)),
+        ('S', ('X0', 1, 3, 1)),
+        ('S', ('X0', 1, 3, 2)),
         ('D', ('S0', 1, 3)),
     ]
 
@@ -422,13 +427,12 @@ def tile_naswinattention_pa_v_kernel(
         grad_raw = {}
         vid_rows = vid.rearrange("(g p j) w -> g p j w", g=GROUPS, j=J)
         pre_rows = qk_pre.rearrange("(g p j) c h d -> g c p j (h d)", g=GROUPS, j=J)
-        w_rows = w_qkv.rearrange("(n i r) f -> n r i f", n=3, i=4)
+        w_rows = w_qkv.rearrange("(n r i) f -> n r i f", n=3, i=4)
 
         def load_vid(g):
             vid_raw[g] = raws.tile([P, J, DIM], BF16, tag="big", bufs=BIG_BUFS, name=f"vid{g}")
-            for c in range(3):
-                cols = slice(c * 512, (c + 1) * 512)
-                nc.sync.dma_start(out=vid_raw[g][:, :, cols], in_=vid_rows[g][:, :, cols])
+            for h in range(2):
+                nc.sync.dma_start(out=vid_raw[g][:, 2 * h : 2 * h + 2, :], in_=vid_rows[g][:, 2 * h : 2 * h + 2, :])
 
         def load_w(n):
             w_raw[n] = raws.tile([P, 4, FEAT], BF16, tag="big", bufs=BIG_BUFS, name=f"w{n}")
@@ -436,10 +440,11 @@ def tile_naswinattention_pa_v_kernel(
                 nc.sync.dma_start(out=w_raw[n][:, 2 * h : 2 * h + 2, :], in_=w_rows[n][:, 2 * h : 2 * h + 2, :])
 
         def load_pre(f, g):
-            t = raws.tile([P, J, INNER], F32, tag="pre", bufs=PRE_BUFS, name=f"pre{f}{g}")
-            for h in range(2):
-                nc.sync.dma_start(out=t[:, 2 * h : 2 * h + 2, :], in_=pre_rows[g, f][:, 2 * h : 2 * h + 2, :])
-            pre_raw[f, g] = t
+            pre_raw[f, g] = raws.tile([P, J, INNER], F32, tag="pre", bufs=PRE_BUFS, name=f"pre{f}{g}")
+            nc.sync.dma_start(out=pre_raw[f, g][:], in_=pre_rows[g, f])
+
+        def pre(f, g, j, lo, hi):
+            return pre_raw[f, g][:, j, lo:hi]
 
         def load(name):
             k = [int(x) for x in name[1:]]
@@ -469,7 +474,7 @@ def tile_naswinattention_pa_v_kernel(
         nc.vector.scalar_tensor_tensor(out=nr2[:], in0=rstd[:], scalar=-1.0 / HD, in1=rstd[:], op0=MULT, op1=MULT)
 
         t_inter, t_bank, t_grp, t_acc, t_res = {}, {}, {}, {}, {}
-        dz_tiles, lead, sums, coef = {}, {}, {}, {}
+        dz_tiles, lead, sums, coef, prods = {}, {}, {}, {}, {}
 
         def copy(engine, dst, src):
             if engine == "V":
@@ -601,7 +606,11 @@ def tile_naswinattention_pa_v_kernel(
         def out0_copy(engine, g, j, n):
             if (0, g, j) not in t_res:
                 t_res[0, g, j] = outs.tile([P, 3, 512], F32, tag="res", bufs=RES_BUFS, name="res")
-            copy(engine, t_res[0, g, j][:, n, :], t_acc.pop((0, g, j, n))[:])
+            copy(
+                engine,
+                t_res[0, g, j][:, n, :].rearrange("p (r i) -> p r i", i=4),
+                t_acc.pop((0, g, j, n))[:].rearrange("p (i r) -> p r i", i=4),
+            )
 
         def out0_store(g, j):
             nc.sync.dma_start(out=out0_rows[g, j], in_=t_res.pop((0, g, j))[:].rearrange("p n w -> p (n w)"))
@@ -619,7 +628,7 @@ def tile_naswinattention_pa_v_kernel(
                 )
 
         def dots(f, g, j):
-            s = work.tile([P, HEADS], F32, tag="sums", bufs=3, name="sums")
+            s = work.tile([P, HEADS], F32, tag="sums", bufs=6, name="sums")
             sums[f, g, j] = s
             for h in range(HEADS):
                 junk = work.tile([P, HD], BF16, tag="junk", bufs=2, name="junk")
@@ -627,14 +636,26 @@ def tile_naswinattention_pa_v_kernel(
                     out=junk[:],
                     in0=lead[f, g, j][:, h * HD : (h + 1) * HD],
                     scalar=1.0,
-                    in1=pre_raw[f, g][:, j, h * HD : (h + 1) * HD],
+                    in1=pre(f, g, j, h * HD, (h + 1) * HD),
                     op0=MULT,
                     op1=MULT,
                     accum_out=s[:, h : h + 1],
                 )
 
+        def products(f, g, j):
+            prods[f, g, j] = work.tile([P, INNER], F32, tag="prod", bufs=PROD_BUFS, name="prod")
+            nc.vector.tensor_tensor(out=prods[f, g, j][:], in0=lead[f, g, j][:], in1=pre(f, g, j, 0, INNER), op=MULT)
+
+        def dots_scalar(f, g, j):
+            s = work.tile([P, HEADS], F32, tag="sums", bufs=6, name="sums")
+            sums[f, g, j] = s
+            t = prods.pop((f, g, j))
+            for h in range(HEADS):
+                junk = work.tile([P, HD], BF16, tag="sjunk", bufs=2, name="sjunk")
+                nc.scalar.activation(junk[:], t[:, h * HD : (h + 1) * HD], COPY, accum_out=s[:, h : h + 1])
+
         def coefs(f, g, j):
-            c = work.tile([P, HEADS], F32, tag="coefs", bufs=3, name="coefs")
+            c = work.tile([P, HEADS], F32, tag="coefs", bufs=6, name="coefs")
             coef[f, g, j] = c
             nc.vector.tensor_tensor(
                 out=c[:],
@@ -649,7 +670,7 @@ def tile_naswinattention_pa_v_kernel(
             for h in range(HEADS):
                 nc.vector.scalar_tensor_tensor(
                     out=dz_tiles[f, g][:, j, h * HD : (h + 1) * HD],
-                    in0=pre_raw[f, g][:, j, h * HD : (h + 1) * HD],
+                    in0=pre(f, g, j, h * HD, (h + 1) * HD),
                     scalar=coef[f, g, j][:, h : h + 1],
                     in1=lead[f, g, j][:, h * HD : (h + 1) * HD],
                     op0=MULT,
@@ -670,7 +691,7 @@ def tile_naswinattention_pa_v_kernel(
             "S1": out1_store,
             "S0": out0_store,
             "L": scaled_grad,
-            "D": dots,
+            "DP": products,
             "C": coefs,
             "F": finish,
         }
@@ -678,6 +699,8 @@ def tile_naswinattention_pa_v_kernel(
             t = node[0]
             if t in ("DI", "VI"):
                 il_direct(engine, *node)
+            elif t == "D":
+                (dots if engine == "V" else dots_scalar)(*node[1:])
             elif t == "IC":
                 il_copy(engine, *node[1:])
             elif t == "X1":

@@ -32,360 +32,382 @@ def tile_naswinattention_pa_v_kernel(
     nc = tc.nc
     TP_BUFS, ACC_BUFS = 3, 5
     BIG_BUFS, PRE_BUFS, INTER_BUFS, GROUPED_BUFS, RES_BUFS, DZ_BUFS, LEAD_BUFS, PROD_BUFS = 4, 3, 3, 5, 4, 3, 4, 1
+    UNITS = {(0, 0): [[0, 1], [2, 3]], (0, 1): [[0, 1], [2, 3]], (1, 0): [[0, 1], [2, 3]], (1, 1): [[0, 1], [2], [3]], (2, 0): [[0, 1], [2, 3]], (2, 1): [[0, 1], [2, 3]]}
     SEQ = [
-        ('D', ('ld', 'g0')),
         ('D', ('ld', 'g2')),
-        ('V', ('L', 0, 0, 0)),
-        ('V', ('L', 0, 0, 1)),
-        ('D', ('ld', 'p00')),
-        ('V', ('L', 0, 0, 2)),
-        ('V', ('L', 0, 0, 3)),
+        ('PE', ('DM', 11)),
+        ('D', ('ld', 'g0')),
+        ('PE', ('DM', 10)),
+        ('PE', ('DM', 7)),
+        ('V', ('DI', 2, 0)),
         ('PE', ('DT', 2, 0, 0)),
-        ('V', ('DI', 2, 1)),
-        ('PE', ('DT', 2, 1, 1)),
-        ('S', ('DC', 2, 0, 0)),
-        ('D', ('ld', 'v1')),
-        ('V', ('DQ', 2, 1)),
-        ('PE', ('DT', 2, 0, 1)),
-        ('V', ('TQ', 2, 0, 0)),
-        ('S', ('DC', 2, 1, 1)),
-        ('V', ('DP', 0, 0, 0)),
-        ('V', ('D', 0, 0, 3)),
         ('PE', ('DT', 2, 1, 0)),
-        ('S', ('D', 0, 0, 0)),
-        ('S', ('DC', 2, 0, 1)),
-        ('V', ('D', 0, 0, 1)),
-        ('PE', ('PI', 'DI', 2, 0, 0)),
+        ('S', ('DC', 2, 0, 0)),
+        ('PE', ('PI', 'DI', 2, 1, 0)),
+        ('D', ('ld', 'p00')),
         ('S', ('DC', 2, 1, 0)),
+        ('V', ('DQ', 2, 0)),
+        ('PE', ('DT', 2, 0, 1)),
+        ('S', ('IC', 'DI', 2, 1, 0)),
+        ('V', ('TQ', 2, 0, 0)),
+        ('PE', ('PI', 'DI', 2, 1, 1)),
+        ('V', ('TQ', 2, 1, 0)),
+        ('S', ('DC', 2, 0, 1)),
+        ('V', ('L', 0, 0, 0)),
+        ('PE', ('DM', 15)),
+        ('S', ('IC', 'DI', 2, 1, 1)),
+        ('PE', ('DM', 12)),
         ('V', ('TQ', 2, 0, 1)),
+        ('PE', ('DM', 1)),
+        ('V', ('L', 0, 0, 1)),
+        ('PE', ('DM', 0)),
         ('D', ('ld', 'v0')),
-        ('V', ('C', 0, 0, 3)),
+        ('PE', ('DM', 4)),
+        ('V', ('DQ', 2, 1)),
+        ('PE', ('DT', 2, 1, 1)),
+        ('V', ('L', 0, 0, 2)),
+        ('PE', ('DM', 2)),
+        ('S', ('DC', 2, 1, 1)),
+        ('PE', ('DM', 14)),
+        ('V', ('DP', 0, 0, 1)),
+        ('V', ('D', 0, 0, 0)),
+        ('S', ('D', 0, 0, 1)),
+        ('V', ('TQ', 2, 1, 1)),
         ('V', ('C', 0, 0, 0)),
         ('V', ('DP', 0, 0, 2)),
-        ('S', ('IC', 'DI', 2, 0, 0)),
-        ('PE', ('PI', 'DI', 2, 0, 1)),
+        ('D', ('ld', 'w0')),
         ('V', ('F', 0, 0, 0)),
         ('S', ('D', 0, 0, 2)),
-        ('V', ('TQ', 2, 1, 1)),
-        ('V', ('L', 0, 1, 0)),
-        ('S', ('VI', 1, 1)),
-        ('V', ('C', 0, 0, 2)),
-        ('V', ('TQ', 2, 1, 0)),
         ('V', ('C', 0, 0, 1)),
-        ('V', ('IC', 'DI', 2, 0, 1)),
-        ('D', ('ld', 'p01')),
-        ('V', ('F', 0, 0, 1)),
-        ('V', ('DQ', 2, 0)),
-        ('PE', ('DT', 0, 0, 0)),
-        ('S', ('VI', 1, 0)),
-        ('V', ('L', 0, 1, 1)),
-        ('PE', ('PI', 'VI', 0, 1, 0)),
-        ('V', ('VQ', 1, 1)),
-        ('V', ('F', 0, 0, 2)),
-        ('D', ('ld', 'w0')),
+        ('V', ('L', 0, 0, 3)),
         ('PE', ('PI', 'VI', 0, 2, 0)),
-        ('V', ('L', 0, 1, 2)),
-        ('S', ('IC', 'VI', 0, 1, 0)),
-        ('V', ('D', 0, 1, 0)),
-        ('S', ('IC', 'VI', 0, 2, 0)),
-        ('PE', ('PI', 'VI', 0, 1, 1)),
-        ('S', ('DC', 0, 0, 0)),
-        ('V', ('D', 0, 1, 1)),
-        ('PE', ('PI', 'VI', 0, 2, 1)),
-        ('S', ('IC', 'VI', 0, 1, 1)),
-        ('V', ('TQ', 0, 0, 0)),
-        ('S', ('IC', 'VI', 0, 2, 1)),
-        ('V', ('VQ', 0, 1)),
-        ('D', ('ld', 'g1')),
-        ('V', ('F', 0, 0, 3)),
         ('S', ('VI', 0, 0)),
-        ('PE', ('O1', 2, 4)),
-        ('V', ('C', 0, 1, 1)),
-        ('V', ('C', 0, 1, 0)),
-        ('V', ('L', 0, 1, 3)),
-        ('PE', ('WT', 0, 0, 0)),
-        ('V', ('F', 0, 1, 0)),
-        ('PE', ('WT', 0, 2, 0)),
-        ('PE', ('WT', 0, 1, 1)),
-        ('V', ('DP', 0, 1, 3)),
-        ('D', ('ld', 'w2')),
-        ('V', ('F', 0, 1, 1)),
-        ('S', ('WC', 0, 0, 0)),
-        ('PE', ('O1', 2, 5)),
+        ('V', ('C', 0, 0, 2)),
+        ('V', ('F', 0, 0, 1)),
+        ('PE', ('PI', 'VI', 0, 1, 0)),
+        ('V', ('D', 0, 0, 3)),
+        ('V', ('F', 0, 0, 2)),
+        ('PE', ('DT', 0, 0, 0)),
+        ('D', ('ld', 'g1')),
+        ('S', ('IC', 'VI', 0, 1, 0)),
         ('V', ('VQ', 0, 0)),
+        ('S', ('DC', 0, 0, 0)),
+        ('PE', ('PI', 'VI', 0, 1, 1)),
+        ('V', ('C', 0, 0, 3)),
+        ('V', ('IC', 'VI', 0, 2, 0)),
+        ('PE', ('WT', 0, 2, 0)),
+        ('V', ('F', 0, 0, 3)),
+        ('S', ('IC', 'VI', 0, 1, 1)),
+        ('PE', ('WT', 0, 1, 1)),
         ('S', ('WC', 0, 2, 0)),
-        ('PE', ('O1', 2, 6)),
-        ('S', ('D', 0, 1, 3)),
-        ('V', ('L', 1, 0, 0)),
-        ('PE', ('WT', 0, 1, 0)),
-        ('V', ('DI', 0, 0)),
-        ('PE', ('WT', 0, 2, 1)),
-        ('S', ('X1', 2, 6)),
-        ('S', ('WC', 0, 1, 1)),
-        ('PE', ('O1', 2, 7)),
-        ('D', ('ld', 'w1')),
-        ('S', ('WC', 0, 2, 1)),
-        ('V', ('L', 1, 0, 1)),
-        ('PE', ('WT', 0, 0, 1)),
-        ('S', ('WC', 0, 1, 0)),
-        ('V', ('WQ', 0, 1, 1)),
+        ('V', ('TQ', 0, 0, 0)),
+        ('D', ('ld', 'w2')),
         ('PE', ('DT', 0, 0, 1)),
-        ('V', ('WQ', 0, 0, 0)),
-        ('S', ('X1', 2, 7)),
-        ('PE', ('WT', 2, 2, 0)),
-        ('V', ('WQ', 0, 1, 0)),
-        ('S', ('DC', 0, 0, 1)),
-        ('V', ('DQ', 0, 0)),
-        ('S', ('WC', 0, 0, 1)),
-        ('V', ('WQ', 0, 2, 1)),
-        ('PE', ('WT', 2, 1, 0)),
-        ('V', ('TQ', 0, 0, 1)),
-        ('S', ('VI', 1, 2)),
-        ('PE', ('WT', 2, 2, 1)),
-        ('V', ('WQ', 0, 0, 1)),
-        ('V', ('C', 0, 1, 3)),
-        ('V', ('X1', 2, 4)),
-        ('D', ('S1', 2, 6)),
-        ('V', ('VQ', 1, 0)),
-        ('V', ('VQ', 0, 2)),
-        ('PE', ('O1', 2, 0)),
-        ('D', ('ld', 'p11')),
-        ('V', ('D', 0, 1, 2)),
-        ('S', ('WC', 2, 1, 0)),
-        ('PE', ('O1', 2, 2)),
-        ('S', ('X1', 2, 5)),
-        ('V', ('VQ', 1, 2)),
-        ('S', ('X1', 2, 0)),
-        ('PE', ('WT', 1, 0, 1)),
-        ('V', ('C', 0, 1, 2)),
-        ('V', ('WQ', 2, 1, 0)),
-        ('V', ('F', 0, 1, 2)),
-        ('S', ('X1', 2, 2)),
-        ('PE', ('O1', 2, 10)),
-        ('D', ('S1', 2, 4)),
+        ('V', ('VQ', 0, 1)),
+        ('S', ('WC', 0, 1, 1)),
+        ('PE', ('PI', 'DI', 0, 0, 0)),
         ('V', ('WQ', 0, 2, 0)),
-        ('S', ('WC', 2, 2, 1)),
-        ('PE', ('O1', 2, 1)),
-        ('V', ('F', 0, 1, 3)),
-        ('S', ('WC', 2, 2, 0)),
-        ('PE', ('WT', 2, 0, 0)),
+        ('S', ('DC', 0, 0, 1)),
+        ('V', ('WQ', 0, 1, 1)),
+        ('PE', ('WT', 0, 1, 0)),
+        ('V', ('L', 1, 0, 0)),
+        ('S', ('IC', 'DI', 0, 0, 0)),
+        ('PE', ('WT', 0, 0, 1)),
+        ('V', ('TQ', 0, 0, 1)),
+        ('S', ('WC', 0, 1, 0)),
+        ('V', ('L', 1, 0, 1)),
+        ('PE', ('PI', 'VI', 0, 2, 1)),
+        ('S', ('WC', 0, 0, 1)),
+        ('PE', ('WT', 0, 2, 1)),
+        ('V', ('WQ', 0, 1, 0)),
+        ('S', ('IC', 'VI', 0, 2, 1)),
         ('V', ('L', 1, 0, 2)),
-        ('D', ('ld', 'p10')),
-        ('S', ('DI', 0, 1)),
-        ('PE', ('WT', 1, 2, 1)),
-        ('V', ('X1', 2, 1)),
+        ('PE', ('WT', 0, 0, 0)),
+        ('D', ('ld', 'v1')),
+        ('S', ('WC', 0, 2, 1)),
+        ('V', ('VQ', 0, 2)),
+        ('PE', ('PI', 'DI', 0, 0, 1)),
+        ('V', ('WC', 0, 0, 0)),
+        ('PE', ('WT', 2, 2, 1)),
+        ('S', ('IC', 'DI', 0, 0, 1)),
+        ('V', ('WQ', 0, 2, 1)),
+        ('PE', ('WT', 2, 0, 0)),
         ('V', ('L', 1, 0, 3)),
-        ('PE', ('O1', 2, 11)),
-        ('PE', ('O1', 2, 3)),
+        ('S', ('WC', 2, 2, 1)),
+        ('PE', ('WT', 2, 2, 0)),
+        ('V', ('DQ', 0, 0)),
+        ('S', ('WC', 2, 0, 0)),
+        ('PE', ('WT', 2, 1, 0)),
         ('V', ('WQ', 2, 2, 1)),
-        ('V', ('WQ', 2, 2, 0)),
-        ('PE', ('O1', 2, 8)),
-        ('V', ('WC', 2, 0, 0)),
-        ('D', ('S1', 2, 0)),
-        ('S', ('WC', 1, 2, 1)),
-        ('V', ('DQ', 0, 1)),
-        ('PE', ('WT', 1, 0, 0)),
-        ('S', ('WC', 1, 0, 1)),
-        ('V', ('WQ', 2, 0, 0)),
-        ('PE', ('WT', 1, 1, 0)),
-        ('V', ('X1', 2, 10)),
-        ('S', ('X1', 2, 3)),
-        ('PE', ('O1', 2, 9)),
-        ('V', ('DP', 1, 0, 2)),
-        ('S', ('WC', 1, 0, 0)),
-        ('D', ('S1', 2, 2)),
-        ('PE', ('O1', 0, 6)),
-        ('V', ('WQ', 1, 0, 1)),
-        ('S', ('WC', 1, 1, 0)),
-        ('V', ('WQ', 1, 0, 0)),
-        ('PE', ('O1', 0, 8)),
-        ('S', ('D', 1, 0, 2)),
-        ('V', ('D', 1, 0, 0)),
-        ('PE', ('DT', 0, 1, 0)),
-        ('S', ('X1', 2, 11)),
-        ('V', ('C', 1, 0, 2)),
-        ('V', ('DP', 1, 0, 1)),
-        ('PE', ('WT', 1, 1, 1)),
-        ('S', ('X1', 0, 8)),
-        ('D', ('S1', 2, 10)),
-        ('V', ('C', 1, 0, 0)),
-        ('V', ('WQ', 1, 1, 0)),
-        ('PE', ('WT', 2, 1, 1)),
-        ('S', ('DC', 0, 1, 0)),
-        ('V', ('F', 1, 0, 0)),
-        ('S', ('D', 1, 0, 1)),
-        ('PE', ('O1', 0, 9)),
-        ('V', ('TQ', 0, 1, 0)),
-        ('V', ('WQ', 1, 2, 1)),
-        ('S', ('WC', 2, 1, 1)),
         ('PE', ('WT', 2, 0, 1)),
-        ('V', ('DP', 1, 0, 3)),
-        ('S', ('WC', 1, 1, 1)),
-        ('V', ('C', 1, 0, 1)),
-        ('PE', ('O1', 0, 4)),
-        ('V', ('WQ', 2, 1, 1)),
-        ('V', ('F', 1, 0, 1)),
+        ('V', ('WQ', 2, 0, 0)),
+        ('D', ('ld', 'p10')),
+        ('S', ('WC', 2, 1, 0)),
+        ('V', ('WQ', 0, 0, 0)),
+        ('V', ('WC', 2, 2, 0)),
         ('S', ('WC', 2, 0, 1)),
-        ('PE', ('WT', 1, 2, 0)),
-        ('V', ('WQ', 1, 1, 1)),
-        ('S', ('X1', 0, 9)),
-        ('PE', ('DT', 1, 0, 0)),
+        ('PE', ('WT', 2, 1, 1)),
+        ('V', ('WQ', 2, 1, 0)),
+        ('S', ('VI', 1, 1)),
+        ('PE', ('PI', 'VI', 1, 0, 0)),
+        ('V', ('VI', 1, 2)),
+        ('PE', ('PI', 'VI', 1, 0, 1)),
+        ('D', ('ld', 'w1')),
         ('V', ('WQ', 2, 0, 1)),
-        ('S', ('X1', 0, 4)),
-        ('V', ('WC', 1, 2, 0)),
-        ('D', ('S1', 0, 8)),
-        ('PE', ('O1', 0, 5)),
-        ('S', ('X1', 0, 6)),
-        ('V', ('DC', 1, 0, 0)),
-        ('PE', ('O1', 0, 0)),
+        ('V', ('VQ', 1, 2)),
+        ('V', ('WQ', 0, 0, 1)),
+        ('S', ('WC', 2, 1, 1)),
+        ('PE', ('O1', 2, 8)),
+        ('V', ('VQ', 1, 1)),
+        ('S', ('IC', 'VI', 1, 0, 0)),
+        ('PE', ('O1', 2, 10)),
+        ('V', ('D', 1, 0, 1)),
         ('S', ('X1', 2, 8)),
-        ('V', ('WQ', 1, 2, 0)),
-        ('V', ('TQ', 1, 0, 0)),
-        ('PE', ('O1', 0, 2)),
-        ('S', ('X1', 0, 5)),
-        ('V', ('F', 1, 0, 2)),
-        ('PE', ('O1', 0, 1)),
-        ('S', ('X1', 2, 9)),
-        ('D', ('S1', 0, 4)),
-        ('V', ('L', 1, 1, 0)),
-        ('PE', ('O0', 0, 0, 0)),
-        ('S', ('X1', 0, 0)),
-        ('V', ('L', 1, 1, 1)),
-        ('S', ('D', 1, 0, 3)),
-        ('PE', ('O1', 0, 3)),
-        ('D', ('S1', 2, 8)),
-        ('V', ('D', 1, 1, 0)),
-        ('S', ('X1', 0, 1)),
-        ('PE', ('O0', 0, 0, 2)),
+        ('PE', ('O1', 2, 4)),
+        ('V', ('DP', 1, 0, 0)),
+        ('S', ('IC', 'VI', 1, 0, 1)),
+        ('PE', ('O1', 2, 11)),
+        ('V', ('C', 1, 0, 1)),
+        ('S', ('X1', 2, 10)),
+        ('V', ('D', 1, 0, 3)),
+        ('PE', ('O1', 2, 5)),
+        ('D', ('ld', 'p01')),
+        ('S', ('D', 1, 0, 0)),
+        ('PE', ('O1', 2, 9)),
+        ('V', ('VQ', 1, 0)),
+        ('PE', ('O1', 2, 6)),
+        ('S', ('X1', 2, 11)),
+        ('V', ('C', 1, 0, 0)),
         ('V', ('C', 1, 0, 3)),
-        ('V', ('L', 1, 1, 2)),
-        ('S', ('X0', 0, 0, 0)),
-        ('PE', ('O0', 0, 0, 1)),
-        ('D', ('S1', 0, 0)),
-        ('V', ('F', 1, 0, 3)),
+        ('V', ('DP', 1, 0, 2)),
+        ('S', ('X1', 2, 4)),
+        ('PE', ('WT', 1, 2, 1)),
+        ('V', ('F', 1, 0, 0)),
+        ('S', ('X1', 2, 6)),
+        ('PE', ('WT', 1, 2, 0)),
+        ('D', ('ld', 'p11')),
+        ('V', ('WQ', 2, 1, 1)),
+        ('S', ('X1', 2, 5)),
+        ('PE', ('WT', 1, 0, 1)),
+        ('V', ('L', 0, 1, 0)),
+        ('S', ('WC', 1, 2, 1)),
+        ('PE', ('O1', 2, 2)),
+        ('V', ('F', 1, 0, 1)),
+        ('S', ('WC', 1, 0, 1)),
+        ('PE', ('WT', 1, 1, 1)),
+        ('V', ('WQ', 1, 2, 1)),
+        ('S', ('WC', 1, 2, 0)),
+        ('V', ('L', 0, 1, 1)),
+        ('PE', ('DT', 1, 0, 0)),
+        ('S', ('WC', 1, 1, 1)),
+        ('D', ('S1', 2, 4)),
+        ('V', ('WQ', 1, 0, 1)),
+        ('PE', ('WT', 1, 0, 0)),
+        ('V', ('WQ', 1, 2, 0)),
+        ('S', ('DC', 1, 0, 0)),
+        ('V', ('WQ', 1, 1, 1)),
+        ('PE', ('O1', 2, 7)),
+        ('V', ('D', 0, 1, 0)),
+        ('S', ('WC', 1, 0, 0)),
+        ('D', ('S1', 2, 10)),
+        ('PE', ('O1', 2, 3)),
+        ('S', ('D', 1, 0, 2)),
+        ('V', ('WQ', 1, 0, 0)),
+        ('PE', ('WT', 1, 1, 0)),
+        ('V', ('TQ', 1, 0, 0)),
+        ('S', ('X1', 2, 7)),
+        ('V', ('DP', 0, 1, 1)),
+        ('PE', ('O0', 0, 0, 0)),
+        ('S', ('X1', 2, 2)),
+        ('D', ('S1', 2, 6)),
+        ('V', ('WC', 1, 1, 0)),
+        ('S', ('D', 0, 1, 1)),
+        ('V', ('C', 1, 0, 2)),
         ('PE', ('O0', 0, 1, 0)),
-        ('V', ('X0', 0, 0, 2)),
-        ('S', ('X0', 0, 0, 1)),
-        ('V', ('X1', 0, 2)),
-        ('D', ('S0', 0, 0)),
-        ('PE', ('DT', 1, 0, 1)),
-        ('V', ('DI', 1, 0)),
-        ('S', ('X1', 0, 3)),
-        ('PE', ('O0', 0, 1, 1)),
-        ('S', ('X0', 0, 1, 0)),
-        ('S', ('DC', 1, 0, 1)),
+        ('V', ('C', 0, 1, 0)),
+        ('V', ('WQ', 2, 2, 0)),
+        ('V', ('F', 0, 1, 0)),
+        ('S', ('X0', 0, 0, 0)),
+        ('PE', ('O0', 0, 0, 2)),
+        ('V', ('C', 0, 1, 1)),
+        ('S', ('X1', 2, 3)),
+        ('V', ('F', 1, 0, 2)),
+        ('S', ('X1', 2, 9)),
+        ('D', ('S1', 2, 2)),
         ('PE', ('O0', 0, 1, 2)),
-        ('V', ('L', 1, 1, 3)),
-        ('D', ('S1', 0, 2)),
-        ('S', ('X0', 0, 1, 1)),
-        ('V', ('TQ', 1, 0, 1)),
-        ('PE', ('O1', 0, 7)),
-        ('V', ('DQ', 1, 0)),
+        ('V', ('F', 0, 1, 1)),
+        ('S', ('X0', 0, 1, 0)),
+        ('V', ('F', 1, 0, 3)),
+        ('PE', ('DT', 0, 1, 0)),
+        ('S', ('X0', 0, 0, 2)),
+        ('V', ('L', 0, 1, 2)),
+        ('D', ('S1', 2, 8)),
+        ('PE', ('DT', 1, 0, 1)),
         ('S', ('X0', 0, 1, 2)),
+        ('V', ('WQ', 1, 1, 0)),
+        ('S', ('DC', 0, 1, 0)),
+        ('PE', ('O1', 2, 0)),
+        ('V', ('D', 0, 1, 2)),
+        ('S', ('DC', 1, 0, 1)),
+        ('PE', ('O0', 0, 0, 1)),
+        ('V', ('L', 0, 1, 3)),
+        ('S', ('X1', 2, 0)),
+        ('PE', ('O0', 0, 1, 1)),
+        ('V', ('TQ', 1, 0, 1)),
+        ('S', ('DI', 1, 0)),
+        ('V', ('C', 0, 1, 2)),
+        ('V', ('D', 0, 1, 3)),
         ('PE', ('O0', 0, 2, 0)),
-        ('V', ('DP', 1, 1, 3)),
-        ('S', ('X1', 0, 7)),
-        ('D', ('S0', 0, 1)),
-        ('V', ('C', 1, 1, 0)),
-        ('V', ('D', 1, 1, 2)),
+        ('V', ('F', 0, 1, 2)),
         ('PE', ('O0', 0, 3, 0)),
-        ('S', ('D', 1, 1, 3)),
-        ('S', ('X0', 0, 2, 0)),
+        ('V', ('C', 0, 1, 3)),
+        ('V', ('X0', 0, 1, 1)),
+        ('PE', ('O0', 0, 2, 1)),
+        ('V', ('F', 0, 1, 3)),
+        ('D', ('S0', 0, 1)),
+        ('S', ('X0', 0, 0, 1)),
+        ('V', ('X0', 0, 2, 0)),
+        ('S', ('DI', 0, 1)),
+        ('PE', ('O0', 0, 3, 2)),
+        ('V', ('DQ', 1, 0)),
         ('PE', ('O0', 0, 2, 2)),
-        ('V', ('F', 1, 1, 0)),
-        ('D', ('S1', 0, 6)),
-        ('S', ('X0', 0, 3, 0)),
-        ('V', ('C', 1, 1, 3)),
-        ('V', ('DP', 1, 1, 1)),
+        ('V', ('X0', 0, 2, 1)),
+        ('D', ('S0', 0, 0)),
+        ('V', ('L', 1, 1, 0)),
         ('PE', ('O0', 0, 3, 1)),
         ('V', ('X0', 0, 2, 2)),
-        ('S', ('D', 1, 1, 1)),
-        ('PE', ('O0', 0, 2, 1)),
-        ('V', ('C', 1, 1, 2)),
-        ('S', ('X0', 0, 3, 1)),
-        ('V', ('C', 1, 1, 1)),
-        ('V', ('F', 1, 1, 1)),
-        ('PE', ('O0', 0, 3, 2)),
-        ('S', ('X0', 0, 2, 1)),
-        ('V', ('F', 1, 1, 2)),
-        ('PE', ('O1', 0, 10)),
-        ('D', ('S0', 0, 2)),
-        ('S', ('X0', 0, 3, 2)),
-        ('V', ('F', 1, 1, 3)),
-        ('PE', ('DT', 1, 1, 0)),
-        ('S', ('X1', 0, 10)),
-        ('PE', ('DT', 1, 1, 1)),
-        ('S', ('DI', 1, 1)),
-        ('V', ('DC', 1, 1, 0)),
+        ('S', ('X0', 0, 3, 0)),
         ('PE', ('DT', 0, 1, 1)),
+        ('V', ('DQ', 0, 1)),
+        ('D', ('S0', 0, 2)),
+        ('S', ('X0', 0, 3, 1)),
+        ('V', ('D', 1, 1, 0)),
+        ('PE', ('O1', 2, 1)),
+        ('S', ('X0', 0, 3, 2)),
+        ('PE', ('O1', 0, 4)),
+        ('V', ('TQ', 0, 1, 0)),
+        ('S', ('X1', 2, 1)),
+        ('PE', ('O1', 0, 6)),
+        ('V', ('C', 1, 1, 0)),
+        ('V', ('L', 1, 1, 1)),
         ('D', ('S0', 0, 3)),
-        ('V', ('TQ', 1, 1, 0)),
-        ('PE', ('O1', 0, 11)),
-        ('V', ('DC', 0, 1, 1)),
-        ('PE', ('O0', 1, 0, 0)),
+        ('S', ('X1', 0, 4)),
+        ('PE', ('O1', 0, 5)),
+        ('V', ('F', 1, 1, 0)),
+        ('S', ('DC', 0, 1, 1)),
+        ('PE', ('O1', 0, 7)),
+        ('V', ('D', 1, 1, 1)),
+        ('S', ('X1', 0, 5)),
+        ('PE', ('O1', 0, 8)),
+        ('D', ('S1', 2, 0)),
         ('V', ('TQ', 0, 1, 1)),
+        ('PE', ('O1', 0, 2)),
+        ('S', ('X1', 0, 8)),
+        ('V', ('C', 1, 1, 1)),
+        ('V', ('L', 1, 1, 2)),
+        ('PE', ('O1', 0, 9)),
+        ('S', ('X1', 0, 2)),
+        ('D', ('S1', 0, 4)),
+        ('V', ('F', 1, 1, 1)),
+        ('PE', ('O1', 0, 3)),
+        ('S', ('X1', 0, 9)),
+        ('V', ('D', 1, 1, 2)),
+        ('PE', ('DT', 1, 1, 0)),
+        ('S', ('X1', 0, 3)),
+        ('D', ('S1', 0, 8)),
+        ('V', ('X1', 0, 6)),
+        ('PE', ('O1', 0, 0)),
+        ('S', ('DC', 1, 1, 0)),
+        ('V', ('C', 1, 1, 2)),
+        ('PE', ('O1', 0, 10)),
+        ('V', ('L', 1, 1, 3)),
+        ('S', ('X1', 0, 7)),
+        ('D', ('S1', 0, 2)),
+        ('PE', ('O1', 0, 1)),
+        ('S', ('X1', 0, 0)),
+        ('V', ('F', 1, 1, 2)),
+        ('PE', ('O1', 0, 11)),
+        ('V', ('TQ', 1, 1, 0)),
+        ('S', ('X1', 0, 1)),
+        ('V', ('DP', 1, 1, 3)),
+        ('PE', ('O0', 1, 0, 0)),
+        ('D', ('S1', 0, 6)),
+        ('V', ('X1', 0, 10)),
+        ('S', ('D', 1, 1, 3)),
         ('PE', ('O0', 1, 1, 0)),
         ('S', ('X1', 0, 11)),
-        ('V', ('DQ', 1, 1)),
-        ('S', ('X0', 1, 0, 0)),
-        ('D', ('S1', 0, 10)),
-        ('PE', ('O1', 1, 0)),
-        ('V', ('X0', 1, 1, 0)),
-        ('S', ('DC', 1, 1, 1)),
-        ('PE', ('O0', 1, 1, 1)),
-        ('S', ('X1', 1, 0)),
-        ('V', ('TQ', 1, 1, 1)),
-        ('PE', ('O1', 1, 1)),
-        ('V', ('X0', 1, 1, 1)),
-        ('PE', ('O0', 1, 1, 2)),
-        ('S', ('X1', 1, 1)),
-        ('PE', ('O1', 1, 2)),
-        ('D', ('S1', 1, 0)),
-        ('V', ('X0', 1, 1, 2)),
-        ('PE', ('O1', 1, 6)),
-        ('S', ('X1', 1, 2)),
-        ('PE', ('O1', 1, 3)),
-        ('D', ('S0', 1, 1)),
-        ('PE', ('O1', 1, 7)),
-        ('V', ('X1', 1, 3)),
-        ('PE', ('O1', 1, 8)),
-        ('S', ('X1', 1, 6)),
-        ('PE', ('O0', 1, 0, 2)),
-        ('D', ('S1', 1, 2)),
-        ('V', ('X1', 1, 7)),
-        ('PE', ('O1', 1, 9)),
-        ('S', ('X0', 1, 0, 2)),
-        ('V', ('X1', 1, 8)),
+        ('V', ('C', 1, 1, 3)),
+        ('D', ('S1', 0, 0)),
+        ('V', ('F', 1, 1, 3)),
         ('PE', ('O0', 1, 0, 1)),
-        ('D', ('S1', 1, 6)),
-        ('V', ('X1', 1, 9)),
-        ('PE', ('O1', 1, 4)),
+        ('S', ('X0', 1, 0, 0)),
+        ('V', ('DI', 1, 1)),
+        ('S', ('X0', 1, 1, 0)),
+        ('PE', ('O0', 1, 0, 2)),
+        ('D', ('S1', 0, 10)),
         ('S', ('X0', 1, 0, 1)),
-        ('PE', ('O0', 1, 2, 0)),
-        ('D', ('S1', 1, 8)),
-        ('V', ('X1', 1, 4)),
-        ('PE', ('O1', 1, 5)),
-        ('S', ('X0', 1, 2, 0)),
+        ('PE', ('O0', 1, 1, 1)),
+        ('S', ('X0', 1, 0, 2)),
+        ('V', ('DQ', 1, 1)),
+        ('PE', ('O0', 1, 1, 2)),
         ('D', ('S0', 1, 0)),
-        ('PE', ('O0', 1, 2, 2)),
-        ('S', ('X1', 1, 5)),
-        ('PE', ('O0', 1, 2, 1)),
-        ('S', ('X0', 1, 2, 2)),
-        ('D', ('S1', 1, 4)),
+        ('V', ('X0', 1, 1, 1)),
         ('PE', ('O1', 1, 10)),
-        ('S', ('X0', 1, 2, 1)),
-        ('PE', ('O0', 1, 3, 0)),
-        ('V', ('X1', 1, 10)),
-        ('D', ('S0', 1, 2)),
+        ('S', ('X0', 1, 1, 2)),
+        ('PE', ('O1', 1, 8)),
+        ('S', ('X1', 1, 10)),
+        ('D', ('S0', 1, 1)),
         ('PE', ('O1', 1, 11)),
-        ('V', ('X0', 1, 3, 0)),
-        ('PE', ('O0', 1, 3, 1)),
+        ('S', ('X1', 1, 8)),
+        ('PE', ('O1', 1, 9)),
         ('S', ('X1', 1, 11)),
-        ('PE', ('O0', 1, 3, 2)),
+        ('PE', ('O1', 1, 0)),
+        ('V', ('X1', 1, 9)),
         ('D', ('S1', 1, 10)),
-        ('S', ('X0', 1, 3, 1)),
-        ('S', ('X0', 1, 3, 2)),
-        ('D', ('S0', 1, 3)),
+        ('PE', ('O1', 1, 6)),
+        ('V', ('X1', 1, 0)),
+        ('PE', ('O1', 1, 1)),
+        ('V', ('X1', 1, 6)),
+        ('PE', ('O1', 1, 4)),
+        ('D', ('S1', 1, 8)),
+        ('V', ('X1', 1, 1)),
+        ('PE', ('O1', 1, 2)),
+        ('PE', ('O1', 1, 5)),
+        ('S', ('X1', 1, 4)),
+        ('D', ('S1', 1, 0)),
+        ('PE', ('O1', 1, 7)),
+        ('S', ('X1', 1, 5)),
+        ('PE', ('DT', 1, 1, 2)),
+        ('S', ('X1', 1, 2)),
+        ('V', ('X1', 1, 7)),
+        ('D', ('S1', 1, 4)),
+        ('PE', ('O1', 1, 3)),
+        ('S', ('DC', 1, 1, 2)),
+        ('V', ('TQ', 1, 1, 2)),
+        ('PE', ('DT', 1, 1, 1)),
+        ('S', ('X1', 1, 3)),
+        ('PE', ('O0', 1, 3, 0)),
+        ('D', ('S1', 1, 6)),
+        ('V', ('DC', 1, 1, 1)),
+        ('V', ('TQ', 1, 1, 1)),
+        ('PE', ('O0', 1, 2, 0)),
+        ('S', ('X0', 1, 3, 0)),
+        ('D', ('S1', 1, 2)),
+        ('PE', ('O0', 1, 3, 2)),
+        ('S', ('X0', 1, 2, 0)),
+        ('PE', ('O0', 1, 2, 1)),
+        ('D', ('S0', 1, 3, 0)),
+        ('V', ('X0', 1, 3, 2)),
+        ('D', ('S0', 1, 2, 0)),
+        ('PE', ('O0', 1, 2, 2)),
+        ('V', ('X0', 1, 2, 1)),
+        ('D', ('S0', 1, 3, 2)),
+        ('PE', ('O0', 1, 3, 1)),
+        ('S', ('X0', 1, 2, 2)),
+        ('D', ('S0', 1, 2, 1)),
+        ('D', ('S0', 1, 2, 2)),
+        ('V', ('X0', 1, 3, 1)),
+        ('D', ('S0', 1, 3, 1)),
     ]
 
     with ExitStack() as ctx:
@@ -463,6 +485,8 @@ def tile_naswinattention_pa_v_kernel(
         nc.vector.memset(ones[:], 1.0)
         ident_bf = keep.tile([P, P], BF16, name="ident_bf")
         make_identity(nc, ident_bf[:])
+        zeros = keep.tile([P, 512], BF16, name="zeros")
+        nc.vector.memset(zeros[:], 0.0)
         warm = keep.tile([P, 1], F32, name="warm")
         nc.vector.memset(warm[:], 0.0)
         nc.scalar.copy(warm[:], warm[:])
@@ -530,37 +554,40 @@ def tile_naswinattention_pa_v_kernel(
             cols = slice(f * 512, (f + 1) * 512)
             quantize(dz_codes[g][:, cols], dz_scales[g][:, cols], t_inter.pop(("DI", f, g))[:], E5M2X4)
 
-        def transposes(key, words):
+        def transposes(key, words, count):
             bank = tps.tile([P, 2, 256], F32, tag="tp", name="bank")
-            t_bank[key] = bank
-            for jj in range(2):
+            t_bank[key] = bank[:, :, 0 : count * P]
+            for jj in range(count):
                 for u in range(2):
                     nc.tensor.transpose(bank[:, u, jj * P : (jj + 1) * P], words[:, jj, u : 256 : 2], ident[:])
 
         def transposed_copy(engine, key):
             t = work.tile([P, 1024], BF16, align_bytes=64, tag="grouped", bufs=GROUPED_BUFS, name="grouped")
-            t_grp[key] = t
-            dst = t[:].bitcast(F32).rearrange("p (r u) -> p r u", u=2)
-            copy(engine, dst, t_bank.pop(key)[:].rearrange("p u r -> p r u"))
+            src = t_bank.pop(key)
+            t_grp[key] = t[:, 0 : 4 * src.shape[2]]
+            dst = t_grp[key].bitcast(F32).rearrange("p (r u) -> p r u", u=2)
+            copy(engine, dst, src.rearrange("p u r -> p r u"))
 
-        def dz_transpose(f, g, h):
+        def dz_transpose(f, g, unit):
+            js = UNITS[f, g][unit]
             if f == 2:
                 words = grad_raw[2][:, g, :].bitcast(F32).rearrange("p (j w) -> p j w", j=J)
             else:
                 words = dz_tiles[f, g][:].bitcast(F32)
-            transposes(("D", f, g, h), words[:, 2 * h : 2 * h + 2, :])
+            transposes(("D", f, g, unit), words[:, js[0] : js[-1] + 1, :], len(js))
 
-        def dzt_quantize(f, g, h):
-            cols = slice(g * 512 + h * 256, g * 512 + (h + 1) * 256)
-            quantize(dzt_codes[f][:, cols], dzt_scales[f][:, cols], t_grp.pop(("D", f, g, h))[:], E5M2X4)
+        def dzt_quantize(f, g, unit):
+            js = UNITS[f, g][unit]
+            cols = slice((J * g + js[0]) * P, (J * g + js[-1] + 1) * P)
+            quantize(dzt_codes[f][:, cols], dzt_scales[f][:, cols], t_grp.pop(("D", f, g, unit)), E5M2X4)
 
         def w_transpose(n, f, h):
             words = w_raw[n][:].bitcast(F32)
-            transposes(("W", n, f, h), words[:, 2 * h : 2 * h + 2, 256 * f : 256 * (f + 1)])
+            transposes(("W", n, f, h), words[:, 2 * h : 2 * h + 2, 256 * f : 256 * (f + 1)], 2)
 
         def w_quantize(n, f, h):
             cols = slice(n * 512 + h * 256, n * 512 + (h + 1) * 256)
-            quantize(w_codes[f][:, cols], w_scales[f][:, cols], t_grp.pop(("W", n, f, h))[:], E4M3X4)
+            quantize(w_codes[f][:, cols], w_scales[f][:, cols], t_grp.pop(("W", n, f, h)), E4M3X4)
 
         def out1(f, i):
             acc = accs.tile([P, 512], F32, tag="acc", name="acc")
@@ -612,8 +639,15 @@ def tile_naswinattention_pa_v_kernel(
                 t_acc.pop((0, g, j, n))[:].rearrange("p (i r) -> p r i", i=4),
             )
 
-        def out0_store(g, j):
-            nc.sync.dma_start(out=out0_rows[g, j], in_=t_res.pop((0, g, j))[:].rearrange("p n w -> p (n w)"))
+        def out0_store(g, j, n=None):
+            if n is None:
+                nc.sync.dma_start(out=out0_rows[g, j], in_=t_res[0, g, j][:].rearrange("p n w -> p (n w)"))
+            else:
+                nc.sync.dma_start(out=out0_rows[g, j][:, n * 512 : (n + 1) * 512], in_=t_res[0, g, j][:, n, :])
+
+        def dummy(k):
+            bank = tps.tile([P, 512], F32, tag="tp", name="bank")
+            nc.tensor.matmul(bank[:], lhsT=ones[:], rhs=zeros[:], start=True, stop=True)
 
         def scaled_grad(f, g, j):
             lead[f, g, j] = work.tile([P, INNER], F32, tag="lead", bufs=LEAD_BUFS, name="lead")
@@ -692,6 +726,7 @@ def tile_naswinattention_pa_v_kernel(
             "S0": out0_store,
             "L": scaled_grad,
             "DP": products,
+            "DM": dummy,
             "C": coefs,
             "F": finish,
         }

@@ -35,379 +35,378 @@ def tile_naswinattention_pa_v_kernel(
     UNITS = {(0, 0): [[0, 1], [2, 3]], (0, 1): [[0, 1], [2, 3]], (1, 0): [[0, 1], [2, 3]], (1, 1): [[0, 1], [2], [3]], (2, 0): [[0, 1], [2, 3]], (2, 1): [[0, 1], [2, 3]]}
     SEQ = [
         ('D', ('ld', 'g2')),
-        ('PE', ('DM', 11)),
+        ('PE', ('DM', 8)),
         ('D', ('ld', 'g0')),
-        ('PE', ('DM', 10)),
-        ('PE', ('DM', 7)),
-        ('V', ('DI', 2, 0)),
-        ('PE', ('DT', 2, 0, 0)),
-        ('PE', ('DT', 2, 1, 0)),
-        ('S', ('DC', 2, 0, 0)),
-        ('PE', ('PI', 'DI', 2, 1, 0)),
-        ('D', ('ld', 'p00')),
-        ('S', ('DC', 2, 1, 0)),
-        ('V', ('DQ', 2, 0)),
-        ('PE', ('DT', 2, 0, 1)),
-        ('S', ('IC', 'DI', 2, 1, 0)),
-        ('V', ('TQ', 2, 0, 0)),
-        ('PE', ('PI', 'DI', 2, 1, 1)),
-        ('V', ('TQ', 2, 1, 0)),
-        ('S', ('DC', 2, 0, 1)),
-        ('V', ('L', 0, 0, 0)),
+        ('PE', ('DM', 4)),
         ('PE', ('DM', 15)),
+        ('S', ('DI', 2, 0)),
+        ('PE', ('DT', 2, 1, 1)),
+        ('PE', ('PI', 'DI', 2, 1, 0)),
+        ('V', ('DC', 2, 1, 1)),
+        ('D', ('ld', 'w1')),
+        ('PE', ('DT', 2, 1, 0)),
+        ('V', ('TQ', 2, 1, 1)),
+        ('PE', ('DM', 3)),
+        ('V', ('DC', 2, 1, 0)),
+        ('S', ('IC', 'DI', 2, 1, 0)),
+        ('PE', ('DM', 10)),
+        ('V', ('DQ', 2, 0)),
+        ('PE', ('DT', 2, 0, 0)),
+        ('V', ('TQ', 2, 1, 0)),
+        ('PE', ('DM', 9)),
+        ('V', ('L', 0, 0, 0)),
+        ('S', ('DC', 2, 0, 0)),
+        ('PE', ('DT', 2, 0, 1)),
+        ('PE', ('PI', 'DI', 2, 1, 1)),
+        ('V', ('TQ', 2, 0, 0)),
+        ('V', ('L', 0, 0, 1)),
+        ('D', ('ld', 'p00')),
+        ('PE', ('DM', 11)),
+        ('V', ('DC', 2, 0, 1)),
         ('S', ('IC', 'DI', 2, 1, 1)),
         ('PE', ('DM', 12)),
-        ('V', ('TQ', 2, 0, 1)),
-        ('PE', ('DM', 1)),
-        ('V', ('L', 0, 0, 1)),
-        ('PE', ('DM', 0)),
-        ('D', ('ld', 'v0')),
-        ('PE', ('DM', 4)),
-        ('V', ('DQ', 2, 1)),
-        ('PE', ('DT', 2, 1, 1)),
         ('V', ('L', 0, 0, 2)),
-        ('PE', ('DM', 2)),
-        ('S', ('DC', 2, 1, 1)),
-        ('PE', ('DM', 14)),
-        ('V', ('DP', 0, 0, 1)),
-        ('V', ('D', 0, 0, 0)),
-        ('S', ('D', 0, 0, 1)),
-        ('V', ('TQ', 2, 1, 1)),
-        ('V', ('C', 0, 0, 0)),
-        ('V', ('DP', 0, 0, 2)),
-        ('D', ('ld', 'w0')),
-        ('V', ('F', 0, 0, 0)),
-        ('S', ('D', 0, 0, 2)),
-        ('V', ('C', 0, 0, 1)),
-        ('V', ('L', 0, 0, 3)),
-        ('PE', ('PI', 'VI', 0, 2, 0)),
-        ('S', ('VI', 0, 0)),
-        ('V', ('C', 0, 0, 2)),
-        ('V', ('F', 0, 0, 1)),
-        ('PE', ('PI', 'VI', 0, 1, 0)),
-        ('V', ('D', 0, 0, 3)),
-        ('V', ('F', 0, 0, 2)),
-        ('PE', ('DT', 0, 0, 0)),
-        ('D', ('ld', 'g1')),
-        ('S', ('IC', 'VI', 0, 1, 0)),
-        ('V', ('VQ', 0, 0)),
-        ('S', ('DC', 0, 0, 0)),
-        ('PE', ('PI', 'VI', 0, 1, 1)),
-        ('V', ('C', 0, 0, 3)),
-        ('V', ('IC', 'VI', 0, 2, 0)),
-        ('PE', ('WT', 0, 2, 0)),
-        ('V', ('F', 0, 0, 3)),
-        ('S', ('IC', 'VI', 0, 1, 1)),
-        ('PE', ('WT', 0, 1, 1)),
-        ('S', ('WC', 0, 2, 0)),
-        ('V', ('TQ', 0, 0, 0)),
-        ('D', ('ld', 'w2')),
-        ('PE', ('DT', 0, 0, 1)),
-        ('V', ('VQ', 0, 1)),
-        ('S', ('WC', 0, 1, 1)),
-        ('PE', ('PI', 'DI', 0, 0, 0)),
-        ('V', ('WQ', 0, 2, 0)),
-        ('S', ('DC', 0, 0, 1)),
-        ('V', ('WQ', 0, 1, 1)),
-        ('PE', ('WT', 0, 1, 0)),
-        ('V', ('L', 1, 0, 0)),
-        ('S', ('IC', 'DI', 0, 0, 0)),
-        ('PE', ('WT', 0, 0, 1)),
-        ('V', ('TQ', 0, 0, 1)),
-        ('S', ('WC', 0, 1, 0)),
-        ('V', ('L', 1, 0, 1)),
-        ('PE', ('PI', 'VI', 0, 2, 1)),
-        ('S', ('WC', 0, 0, 1)),
-        ('PE', ('WT', 0, 2, 1)),
-        ('V', ('WQ', 0, 1, 0)),
-        ('S', ('IC', 'VI', 0, 2, 1)),
-        ('V', ('L', 1, 0, 2)),
-        ('PE', ('WT', 0, 0, 0)),
-        ('D', ('ld', 'v1')),
-        ('S', ('WC', 0, 2, 1)),
-        ('V', ('VQ', 0, 2)),
-        ('PE', ('PI', 'DI', 0, 0, 1)),
-        ('V', ('WC', 0, 0, 0)),
-        ('PE', ('WT', 2, 2, 1)),
-        ('S', ('IC', 'DI', 0, 0, 1)),
-        ('V', ('WQ', 0, 2, 1)),
-        ('PE', ('WT', 2, 0, 0)),
-        ('V', ('L', 1, 0, 3)),
-        ('S', ('WC', 2, 2, 1)),
-        ('PE', ('WT', 2, 2, 0)),
-        ('V', ('DQ', 0, 0)),
-        ('S', ('WC', 2, 0, 0)),
-        ('PE', ('WT', 2, 1, 0)),
-        ('V', ('WQ', 2, 2, 1)),
-        ('PE', ('WT', 2, 0, 1)),
-        ('V', ('WQ', 2, 0, 0)),
-        ('D', ('ld', 'p10')),
-        ('S', ('WC', 2, 1, 0)),
-        ('V', ('WQ', 0, 0, 0)),
-        ('V', ('WC', 2, 2, 0)),
-        ('S', ('WC', 2, 0, 1)),
-        ('PE', ('WT', 2, 1, 1)),
-        ('V', ('WQ', 2, 1, 0)),
-        ('S', ('VI', 1, 1)),
-        ('PE', ('PI', 'VI', 1, 0, 0)),
-        ('V', ('VI', 1, 2)),
-        ('PE', ('PI', 'VI', 1, 0, 1)),
-        ('D', ('ld', 'w1')),
-        ('V', ('WQ', 2, 0, 1)),
-        ('V', ('VQ', 1, 2)),
-        ('V', ('WQ', 0, 0, 1)),
-        ('S', ('WC', 2, 1, 1)),
-        ('PE', ('O1', 2, 8)),
-        ('V', ('VQ', 1, 1)),
-        ('S', ('IC', 'VI', 1, 0, 0)),
-        ('PE', ('O1', 2, 10)),
-        ('V', ('D', 1, 0, 1)),
-        ('S', ('X1', 2, 8)),
-        ('PE', ('O1', 2, 4)),
-        ('V', ('DP', 1, 0, 0)),
-        ('S', ('IC', 'VI', 1, 0, 1)),
-        ('PE', ('O1', 2, 11)),
-        ('V', ('C', 1, 0, 1)),
-        ('S', ('X1', 2, 10)),
-        ('V', ('D', 1, 0, 3)),
-        ('PE', ('O1', 2, 5)),
-        ('D', ('ld', 'p01')),
-        ('S', ('D', 1, 0, 0)),
-        ('PE', ('O1', 2, 9)),
-        ('V', ('VQ', 1, 0)),
-        ('PE', ('O1', 2, 6)),
-        ('S', ('X1', 2, 11)),
-        ('V', ('C', 1, 0, 0)),
-        ('V', ('C', 1, 0, 3)),
-        ('V', ('DP', 1, 0, 2)),
-        ('S', ('X1', 2, 4)),
-        ('PE', ('WT', 1, 2, 1)),
-        ('V', ('F', 1, 0, 0)),
-        ('S', ('X1', 2, 6)),
-        ('PE', ('WT', 1, 2, 0)),
-        ('D', ('ld', 'p11')),
-        ('V', ('WQ', 2, 1, 1)),
-        ('S', ('X1', 2, 5)),
+        ('PE', ('WT', 1, 1, 0)),
+        ('V', ('TQ', 2, 0, 1)),
         ('PE', ('WT', 1, 0, 1)),
-        ('V', ('L', 0, 1, 0)),
-        ('S', ('WC', 1, 2, 1)),
-        ('PE', ('O1', 2, 2)),
-        ('V', ('F', 1, 0, 1)),
-        ('S', ('WC', 1, 0, 1)),
+        ('S', ('WC', 1, 1, 0)),
+        ('V', ('L', 0, 0, 3)),
         ('PE', ('WT', 1, 1, 1)),
-        ('V', ('WQ', 1, 2, 1)),
+        ('S', ('WC', 1, 0, 1)),
+        ('D', ('ld', 'v1')),
+        ('V', ('DQ', 2, 1)),
+        ('PE', ('WT', 1, 2, 0)),
+        ('S', ('WC', 1, 1, 1)),
+        ('V', ('WQ', 1, 0, 1)),
+        ('PE', ('WT', 1, 2, 1)),
+        ('V', ('WQ', 1, 1, 0)),
         ('S', ('WC', 1, 2, 0)),
+        ('PE', ('WT', 1, 0, 0)),
+        ('V', ('DP', 0, 0, 2)),
+        ('S', ('WC', 1, 2, 1)),
+        ('V', ('WQ', 1, 1, 1)),
+        ('V', ('D', 0, 0, 3)),
+        ('S', ('D', 0, 0, 2)),
+        ('PE', ('DM', 5)),
+        ('S', ('WC', 1, 0, 0)),
+        ('PE', ('DM', 0)),
+        ('V', ('DP', 0, 0, 0)),
+        ('D', ('ld', 'g1')),
+        ('V', ('C', 0, 0, 3)),
+        ('V', ('WQ', 1, 0, 0)),
+        ('S', ('D', 0, 0, 0)),
+        ('V', ('D', 0, 0, 1)),
+        ('PE', ('PI', 'VI', 1, 2, 0)),
+        ('S', ('VI', 1, 0)),
+        ('V', ('C', 0, 0, 0)),
+        ('V', ('WQ', 1, 2, 1)),
+        ('V', ('C', 0, 0, 1)),
+        ('V', ('F', 0, 0, 0)),
+        ('PE', ('PI', 'VI', 1, 1, 0)),
+        ('V', ('WQ', 1, 2, 0)),
+        ('D', ('ld', 'v0')),
+        ('V', ('C', 0, 0, 2)),
+        ('PE', ('PI', 'VI', 1, 2, 1)),
+        ('V', ('F', 0, 0, 1)),
+        ('S', ('IC', 'VI', 1, 2, 0)),
+        ('V', ('L', 1, 0, 0)),
+        ('S', ('IC', 'VI', 1, 1, 0)),
+        ('V', ('F', 0, 0, 2)),
+        ('PE', ('PI', 'VI', 1, 1, 1)),
+        ('S', ('IC', 'VI', 1, 2, 1)),
+        ('V', ('VQ', 1, 0)),
+        ('PE', ('DT', 0, 0, 0)),
+        ('S', ('IC', 'VI', 1, 1, 1)),
+        ('V', ('F', 0, 0, 3)),
+        ('S', ('DC', 0, 0, 0)),
+        ('D', ('ld', 'p10')),
+        ('V', ('L', 1, 0, 1)),
+        ('PE', ('DT', 0, 0, 1)),
+        ('S', ('DI', 0, 0)),
+        ('V', ('VQ', 1, 2)),
+        ('PE', ('PI', 'VI', 0, 1, 0)),
+        ('V', ('VQ', 1, 1)),
+        ('V', ('VI', 0, 0)),
+        ('PE', ('PI', 'VI', 0, 1, 1)),
+        ('D', ('ld', 'w0')),
+        ('S', ('IC', 'VI', 0, 1, 0)),
+        ('V', ('DQ', 0, 0)),
+        ('S', ('DC', 0, 0, 1)),
+        ('V', ('VQ', 0, 0)),
+        ('S', ('IC', 'VI', 0, 1, 1)),
+        ('V', ('TQ', 0, 0, 1)),
+        ('S', ('VI', 0, 2)),
+        ('PE', ('O1', 2, 2)),
+        ('V', ('VQ', 0, 1)),
+        ('PE', ('O1', 2, 0)),
+        ('V', ('D', 1, 0, 1)),
+        ('PE', ('O1', 2, 4)),
+        ('D', ('ld', 'w2')),
+        ('V', ('L', 1, 0, 2)),
+        ('PE', ('O1', 2, 6)),
+        ('V', ('C', 1, 0, 1)),
+        ('PE', ('O1', 2, 5)),
+        ('V', ('DP', 1, 0, 0)),
+        ('S', ('X1', 2, 4)),
+        ('V', ('D', 1, 0, 2)),
+        ('PE', ('WT', 0, 0, 0)),
+        ('S', ('D', 1, 0, 0)),
+        ('PE', ('WT', 0, 1, 0)),
+        ('S', ('X1', 2, 6)),
+        ('V', ('VQ', 0, 2)),
+        ('PE', ('WT', 0, 1, 1)),
+        ('S', ('WC', 0, 0, 0)),
+        ('V', ('C', 1, 0, 2)),
+        ('V', ('L', 1, 0, 3)),
+        ('PE', ('O1', 2, 7)),
+        ('S', ('WC', 0, 1, 0)),
+        ('D', ('ld', 'p11')),
+        ('V', ('WQ', 0, 0, 0)),
+        ('PE', ('WT', 0, 2, 0)),
+        ('S', ('X1', 2, 5)),
+        ('V', ('DP', 1, 0, 3)),
+        ('PE', ('WT', 0, 0, 1)),
+        ('S', ('X1', 2, 7)),
+        ('V', ('WQ', 0, 1, 0)),
+        ('V', ('WC', 0, 1, 1)),
+        ('S', ('WC', 0, 2, 0)),
+        ('PE', ('O1', 2, 10)),
+        ('V', ('C', 1, 0, 0)),
+        ('V', ('TQ', 0, 0, 0)),
+        ('S', ('WC', 0, 0, 1)),
+        ('PE', ('WT', 2, 0, 1)),
+        ('V', ('WQ', 0, 2, 0)),
+        ('D', ('S1', 2, 6)),
+        ('V', ('WQ', 0, 1, 1)),
+        ('S', ('X1', 2, 10)),
+        ('PE', ('WT', 2, 2, 1)),
+        ('V', ('WQ', 0, 0, 1)),
+        ('S', ('WC', 2, 0, 1)),
+        ('V', ('F', 1, 0, 0)),
+        ('PE', ('WT', 2, 1, 0)),
+        ('S', ('X1', 2, 0)),
+        ('V', ('WQ', 2, 0, 1)),
+        ('PE', ('WT', 2, 2, 0)),
+        ('D', ('S1', 2, 4)),
+        ('V', ('F', 1, 0, 1)),
+        ('S', ('WC', 2, 1, 0)),
+        ('PE', ('O1', 2, 11)),
+        ('V', ('L', 0, 1, 0)),
+        ('S', ('WC', 2, 2, 0)),
+        ('D', ('ld', 'p01')),
+        ('PE', ('WT', 0, 2, 1)),
+        ('S', ('WC', 2, 2, 1)),
+        ('V', ('WQ', 2, 1, 0)),
+        ('V', ('WQ', 2, 2, 0)),
+        ('PE', ('WT', 2, 1, 1)),
+        ('S', ('X1', 2, 11)),
         ('V', ('L', 0, 1, 1)),
         ('PE', ('DT', 1, 0, 0)),
-        ('S', ('WC', 1, 1, 1)),
-        ('D', ('S1', 2, 4)),
-        ('V', ('WQ', 1, 0, 1)),
-        ('PE', ('WT', 1, 0, 0)),
-        ('V', ('WQ', 1, 2, 0)),
+        ('S', ('D', 1, 0, 3)),
+        ('V', ('WC', 2, 1, 1)),
+        ('PE', ('O1', 2, 8)),
         ('S', ('DC', 1, 0, 0)),
-        ('V', ('WQ', 1, 1, 1)),
-        ('PE', ('O1', 2, 7)),
-        ('V', ('D', 0, 1, 0)),
-        ('S', ('WC', 1, 0, 0)),
+        ('V', ('WQ', 2, 2, 1)),
+        ('V', ('WQ', 2, 1, 1)),
+        ('PE', ('WT', 2, 0, 0)),
+        ('S', ('WC', 0, 2, 1)),
         ('D', ('S1', 2, 10)),
-        ('PE', ('O1', 2, 3)),
-        ('S', ('D', 1, 0, 2)),
-        ('V', ('WQ', 1, 0, 0)),
-        ('PE', ('WT', 1, 1, 0)),
         ('V', ('TQ', 1, 0, 0)),
-        ('S', ('X1', 2, 7)),
-        ('V', ('DP', 0, 1, 1)),
-        ('PE', ('O0', 0, 0, 0)),
-        ('S', ('X1', 2, 2)),
-        ('D', ('S1', 2, 6)),
-        ('V', ('WC', 1, 1, 0)),
-        ('S', ('D', 0, 1, 1)),
-        ('V', ('C', 1, 0, 2)),
-        ('PE', ('O0', 0, 1, 0)),
-        ('V', ('C', 0, 1, 0)),
-        ('V', ('WQ', 2, 2, 0)),
-        ('V', ('F', 0, 1, 0)),
-        ('S', ('X0', 0, 0, 0)),
-        ('PE', ('O0', 0, 0, 2)),
-        ('V', ('C', 0, 1, 1)),
-        ('S', ('X1', 2, 3)),
+        ('V', ('C', 1, 0, 3)),
         ('V', ('F', 1, 0, 2)),
-        ('S', ('X1', 2, 9)),
-        ('D', ('S1', 2, 2)),
-        ('PE', ('O0', 0, 1, 2)),
-        ('V', ('F', 0, 1, 1)),
-        ('S', ('X0', 0, 1, 0)),
+        ('S', ('X1', 2, 8)),
+        ('PE', ('O1', 2, 9)),
+        ('S', ('WC', 2, 0, 0)),
+        ('PE', ('O1', 2, 3)),
+        ('V', ('WQ', 0, 2, 1)),
         ('V', ('F', 1, 0, 3)),
-        ('PE', ('DT', 0, 1, 0)),
-        ('S', ('X0', 0, 0, 2)),
-        ('V', ('L', 0, 1, 2)),
+        ('S', ('X1', 2, 9)),
+        ('PE', ('O0', 0, 1, 0)),
+        ('V', ('WQ', 2, 0, 0)),
+        ('S', ('X1', 2, 2)),
         ('D', ('S1', 2, 8)),
-        ('PE', ('DT', 1, 0, 1)),
-        ('S', ('X0', 0, 1, 2)),
-        ('V', ('WQ', 1, 1, 0)),
-        ('S', ('DC', 0, 1, 0)),
-        ('PE', ('O1', 2, 0)),
-        ('V', ('D', 0, 1, 2)),
-        ('S', ('DC', 1, 0, 1)),
-        ('PE', ('O0', 0, 0, 1)),
-        ('V', ('L', 0, 1, 3)),
-        ('S', ('X1', 2, 0)),
-        ('PE', ('O0', 0, 1, 1)),
-        ('V', ('TQ', 1, 0, 1)),
+        ('V', ('D', 0, 1, 0)),
+        ('PE', ('O0', 0, 0, 0)),
         ('S', ('DI', 1, 0)),
+        ('V', ('L', 0, 1, 2)),
+        ('PE', ('O0', 0, 1, 1)),
+        ('V', ('C', 0, 1, 0)),
+        ('V', ('D', 0, 1, 1)),
+        ('PE', ('O0', 0, 0, 1)),
+        ('V', ('D', 0, 1, 2)),
+        ('PE', ('DT', 1, 0, 1)),
+        ('S', ('X1', 2, 3)),
+        ('S', ('X0', 0, 1, 0)),
+        ('D', ('S1', 2, 2)),
+        ('V', ('C', 0, 1, 1)),
+        ('PE', ('O0', 0, 0, 2)),
+        ('V', ('F', 0, 1, 0)),
+        ('S', ('DC', 1, 0, 1)),
         ('V', ('C', 0, 1, 2)),
-        ('V', ('D', 0, 1, 3)),
-        ('PE', ('O0', 0, 2, 0)),
-        ('V', ('F', 0, 1, 2)),
-        ('PE', ('O0', 0, 3, 0)),
-        ('V', ('C', 0, 1, 3)),
-        ('V', ('X0', 0, 1, 1)),
-        ('PE', ('O0', 0, 2, 1)),
-        ('V', ('F', 0, 1, 3)),
-        ('D', ('S0', 0, 1)),
-        ('S', ('X0', 0, 0, 1)),
-        ('V', ('X0', 0, 2, 0)),
-        ('S', ('DI', 0, 1)),
-        ('PE', ('O0', 0, 3, 2)),
-        ('V', ('DQ', 1, 0)),
-        ('PE', ('O0', 0, 2, 2)),
-        ('V', ('X0', 0, 2, 1)),
-        ('D', ('S0', 0, 0)),
-        ('V', ('L', 1, 1, 0)),
-        ('PE', ('O0', 0, 3, 1)),
-        ('V', ('X0', 0, 2, 2)),
-        ('S', ('X0', 0, 3, 0)),
-        ('PE', ('DT', 0, 1, 1)),
-        ('V', ('DQ', 0, 1)),
-        ('D', ('S0', 0, 2)),
-        ('S', ('X0', 0, 3, 1)),
-        ('V', ('D', 1, 1, 0)),
+        ('V', ('L', 0, 1, 3)),
+        ('PE', ('O0', 0, 1, 2)),
+        ('S', ('X0', 0, 0, 0)),
+        ('S', ('X0', 0, 1, 1)),
+        ('V', ('TQ', 1, 0, 1)),
         ('PE', ('O1', 2, 1)),
-        ('S', ('X0', 0, 3, 2)),
-        ('PE', ('O1', 0, 4)),
-        ('V', ('TQ', 0, 1, 0)),
+        ('V', ('DP', 0, 1, 3)),
+        ('S', ('X0', 0, 0, 2)),
+        ('PE', ('O0', 0, 3, 0)),
+        ('V', ('F', 0, 1, 1)),
+        ('S', ('X0', 0, 1, 2)),
+        ('V', ('L', 1, 1, 0)),
+        ('S', ('D', 0, 1, 3)),
+        ('PE', ('O0', 0, 2, 0)),
+        ('D', ('S0', 0, 1)),
+        ('V', ('F', 0, 1, 2)),
+        ('S', ('X0', 0, 3, 0)),
+        ('PE', ('O0', 0, 3, 2)),
+        ('V', ('C', 0, 1, 3)),
+        ('V', ('DP', 1, 1, 0)),
         ('S', ('X1', 2, 1)),
-        ('PE', ('O1', 0, 6)),
-        ('V', ('C', 1, 1, 0)),
-        ('V', ('L', 1, 1, 1)),
-        ('D', ('S0', 0, 3)),
-        ('S', ('X1', 0, 4)),
-        ('PE', ('O1', 0, 5)),
-        ('V', ('F', 1, 1, 0)),
-        ('S', ('DC', 0, 1, 1)),
-        ('PE', ('O1', 0, 7)),
-        ('V', ('D', 1, 1, 1)),
-        ('S', ('X1', 0, 5)),
-        ('PE', ('O1', 0, 8)),
+        ('PE', ('O0', 0, 3, 1)),
+        ('V', ('F', 0, 1, 3)),
+        ('S', ('X0', 0, 0, 1)),
         ('D', ('S1', 2, 0)),
-        ('V', ('TQ', 0, 1, 1)),
-        ('PE', ('O1', 0, 2)),
-        ('S', ('X1', 0, 8)),
-        ('V', ('C', 1, 1, 1)),
+        ('S', ('D', 1, 1, 0)),
+        ('V', ('L', 1, 1, 1)),
+        ('PE', ('DT', 0, 1, 0)),
+        ('S', ('X0', 0, 3, 1)),
+        ('V', ('DI', 0, 1)),
+        ('PE', ('DT', 0, 1, 1)),
+        ('D', ('S0', 0, 0)),
+        ('S', ('DC', 0, 1, 0)),
+        ('PE', ('O0', 0, 2, 1)),
+        ('S', ('X0', 0, 3, 2)),
+        ('V', ('TQ', 0, 1, 0)),
+        ('S', ('X0', 0, 2, 0)),
+        ('V', ('DQ', 0, 1)),
+        ('PE', ('O0', 0, 2, 2)),
+        ('D', ('S0', 0, 3)),
+        ('S', ('DC', 0, 1, 1)),
         ('V', ('L', 1, 1, 2)),
-        ('PE', ('O1', 0, 9)),
-        ('S', ('X1', 0, 2)),
-        ('D', ('S1', 0, 4)),
-        ('V', ('F', 1, 1, 1)),
-        ('PE', ('O1', 0, 3)),
-        ('S', ('X1', 0, 9)),
+        ('PE', ('O1', 0, 2)),
+        ('S', ('X0', 0, 2, 1)),
+        ('V', ('C', 1, 1, 0)),
+        ('V', ('DP', 1, 1, 1)),
+        ('PE', ('O1', 0, 8)),
+        ('S', ('X0', 0, 2, 2)),
+        ('V', ('TQ', 0, 1, 1)),
+        ('PE', ('O1', 0, 4)),
         ('V', ('D', 1, 1, 2)),
-        ('PE', ('DT', 1, 1, 0)),
+        ('S', ('D', 1, 1, 1)),
+        ('D', ('S0', 0, 2)),
+        ('PE', ('O1', 0, 9)),
+        ('S', ('X1', 0, 8)),
+        ('PE', ('O1', 0, 3)),
+        ('V', ('C', 1, 1, 1)),
+        ('V', ('F', 1, 1, 0)),
+        ('S', ('X1', 0, 2)),
+        ('PE', ('O1', 0, 10)),
+        ('V', ('C', 1, 1, 2)),
+        ('V', ('X1', 0, 4)),
+        ('S', ('X1', 0, 9)),
+        ('PE', ('O1', 0, 0)),
+        ('V', ('F', 1, 1, 1)),
         ('S', ('X1', 0, 3)),
         ('D', ('S1', 0, 8)),
-        ('V', ('X1', 0, 6)),
-        ('PE', ('O1', 0, 0)),
-        ('S', ('DC', 1, 1, 0)),
-        ('V', ('C', 1, 1, 2)),
-        ('PE', ('O1', 0, 10)),
-        ('V', ('L', 1, 1, 3)),
-        ('S', ('X1', 0, 7)),
-        ('D', ('S1', 0, 2)),
-        ('PE', ('O1', 0, 1)),
+        ('PE', ('O1', 0, 5)),
+        ('V', ('DQ', 1, 0)),
         ('S', ('X1', 0, 0)),
+        ('PE', ('O1', 0, 1)),
         ('V', ('F', 1, 1, 2)),
+        ('D', ('S1', 0, 2)),
+        ('PE', ('DT', 1, 1, 0)),
+        ('S', ('X1', 0, 1)),
+        ('V', ('X1', 0, 5)),
+        ('PE', ('DT', 1, 1, 1)),
+        ('S', ('DC', 1, 1, 0)),
+        ('V', ('L', 1, 1, 3)),
+        ('PE', ('O1', 0, 6)),
+        ('D', ('S1', 0, 0)),
+        ('S', ('DC', 1, 1, 1)),
         ('PE', ('O1', 0, 11)),
         ('V', ('TQ', 1, 1, 0)),
-        ('S', ('X1', 0, 1)),
-        ('V', ('DP', 1, 1, 3)),
-        ('PE', ('O0', 1, 0, 0)),
-        ('D', ('S1', 0, 6)),
-        ('V', ('X1', 0, 10)),
-        ('S', ('D', 1, 1, 3)),
-        ('PE', ('O0', 1, 1, 0)),
-        ('S', ('X1', 0, 11)),
-        ('V', ('C', 1, 1, 3)),
-        ('D', ('S1', 0, 0)),
-        ('V', ('F', 1, 1, 3)),
-        ('PE', ('O0', 1, 0, 1)),
-        ('S', ('X0', 1, 0, 0)),
-        ('V', ('DI', 1, 1)),
-        ('S', ('X0', 1, 1, 0)),
-        ('PE', ('O0', 1, 0, 2)),
-        ('D', ('S1', 0, 10)),
-        ('S', ('X0', 1, 0, 1)),
-        ('PE', ('O0', 1, 1, 1)),
-        ('S', ('X0', 1, 0, 2)),
-        ('V', ('DQ', 1, 1)),
-        ('PE', ('O0', 1, 1, 2)),
-        ('D', ('S0', 1, 0)),
-        ('V', ('X0', 1, 1, 1)),
-        ('PE', ('O1', 1, 10)),
-        ('S', ('X0', 1, 1, 2)),
-        ('PE', ('O1', 1, 8)),
-        ('S', ('X1', 1, 10)),
-        ('D', ('S0', 1, 1)),
-        ('PE', ('O1', 1, 11)),
-        ('S', ('X1', 1, 8)),
-        ('PE', ('O1', 1, 9)),
-        ('S', ('X1', 1, 11)),
-        ('PE', ('O1', 1, 0)),
-        ('V', ('X1', 1, 9)),
-        ('D', ('S1', 1, 10)),
-        ('PE', ('O1', 1, 6)),
-        ('V', ('X1', 1, 0)),
-        ('PE', ('O1', 1, 1)),
-        ('V', ('X1', 1, 6)),
-        ('PE', ('O1', 1, 4)),
-        ('D', ('S1', 1, 8)),
-        ('V', ('X1', 1, 1)),
-        ('PE', ('O1', 1, 2)),
-        ('PE', ('O1', 1, 5)),
-        ('S', ('X1', 1, 4)),
-        ('D', ('S1', 1, 0)),
-        ('PE', ('O1', 1, 7)),
-        ('S', ('X1', 1, 5)),
-        ('PE', ('DT', 1, 1, 2)),
-        ('S', ('X1', 1, 2)),
-        ('V', ('X1', 1, 7)),
-        ('D', ('S1', 1, 4)),
-        ('PE', ('O1', 1, 3)),
-        ('S', ('DC', 1, 1, 2)),
-        ('V', ('TQ', 1, 1, 2)),
-        ('PE', ('DT', 1, 1, 1)),
-        ('S', ('X1', 1, 3)),
-        ('PE', ('O0', 1, 3, 0)),
-        ('D', ('S1', 1, 6)),
-        ('V', ('DC', 1, 1, 1)),
+        ('S', ('X1', 0, 10)),
         ('V', ('TQ', 1, 1, 1)),
+        ('V', ('DP', 1, 1, 3)),
+        ('PE', ('O1', 0, 7)),
+        ('S', ('X1', 0, 11)),
+        ('V', ('X1', 0, 6)),
+        ('D', ('S1', 0, 4)),
         ('PE', ('O0', 1, 2, 0)),
-        ('S', ('X0', 1, 3, 0)),
-        ('D', ('S1', 1, 2)),
-        ('PE', ('O0', 1, 3, 2)),
+        ('S', ('D', 1, 1, 3)),
+        ('PE', ('O0', 1, 0, 0)),
+        ('S', ('X1', 0, 7)),
+        ('V', ('C', 1, 1, 3)),
+        ('D', ('S1', 0, 10)),
+        ('V', ('F', 1, 1, 3)),
         ('S', ('X0', 1, 2, 0)),
         ('PE', ('O0', 1, 2, 1)),
-        ('D', ('S0', 1, 3, 0)),
-        ('V', ('X0', 1, 3, 2)),
+        ('V', ('DI', 1, 1)),
+        ('S', ('X0', 1, 0, 0)),
+        ('PE', ('O0', 1, 0, 2)),
+        ('D', ('S1', 0, 6)),
+        ('S', ('X0', 1, 2, 1)),
+        ('PE', ('O0', 1, 0, 1)),
+        ('S', ('X0', 1, 0, 2)),
+        ('V', ('DQ', 1, 1)),
         ('D', ('S0', 1, 2, 0)),
         ('PE', ('O0', 1, 2, 2)),
-        ('V', ('X0', 1, 2, 1)),
-        ('D', ('S0', 1, 3, 2)),
-        ('PE', ('O0', 1, 3, 1)),
-        ('S', ('X0', 1, 2, 2)),
+        ('V', ('X0', 1, 0, 1)),
         ('D', ('S0', 1, 2, 1)),
+        ('PE', ('O1', 1, 8)),
+        ('D', ('S0', 1, 0)),
+        ('S', ('X0', 1, 2, 2)),
+        ('PE', ('O1', 1, 6)),
+        ('V', ('X1', 1, 8)),
+        ('PE', ('O1', 1, 9)),
+        ('S', ('X1', 1, 6)),
+        ('PE', ('O1', 1, 7)),
+        ('V', ('X1', 1, 9)),
         ('D', ('S0', 1, 2, 2)),
+        ('PE', ('O1', 1, 0)),
+        ('S', ('X1', 1, 7)),
+        ('D', ('S1', 1, 8)),
+        ('PE', ('O1', 1, 2)),
+        ('S', ('X1', 1, 0)),
+        ('PE', ('O1', 1, 1)),
+        ('V', ('X1', 1, 2)),
+        ('PE', ('O1', 1, 3)),
+        ('D', ('S1', 1, 6)),
+        ('S', ('X1', 1, 1)),
+        ('PE', ('O1', 1, 4)),
+        ('V', ('X1', 1, 3)),
+        ('PE', ('O0', 1, 1, 0)),
+        ('V', ('X1', 1, 4)),
+        ('D', ('S1', 1, 0)),
+        ('PE', ('O1', 1, 5)),
+        ('PE', ('O0', 1, 1, 2)),
+        ('V', ('X0', 1, 1, 0)),
+        ('D', ('S1', 1, 2)),
+        ('V', ('X1', 1, 5)),
+        ('PE', ('O0', 1, 1, 1)),
+        ('V', ('X0', 1, 1, 2)),
+        ('D', ('S1', 1, 4)),
+        ('PE', ('DT', 1, 1, 2)),
+        ('S', ('X0', 1, 1, 1)),
+        ('PE', ('O1', 1, 10)),
+        ('V', ('DC', 1, 1, 2)),
+        ('V', ('TQ', 1, 1, 2)),
+        ('D', ('S0', 1, 1)),
+        ('PE', ('O1', 1, 11)),
+        ('S', ('X1', 1, 10)),
+        ('PE', ('O0', 1, 3, 0)),
+        ('S', ('X1', 1, 11)),
+        ('D', ('S1', 1, 10)),
+        ('PE', ('O0', 1, 3, 1)),
+        ('S', ('X0', 1, 3, 0)),
+        ('PE', ('O0', 1, 3, 2)),
         ('V', ('X0', 1, 3, 1)),
+        ('D', ('S0', 1, 3, 0)),
+        ('S', ('X0', 1, 3, 2)),
         ('D', ('S0', 1, 3, 1)),
+        ('D', ('S0', 1, 3, 2)),
     ]
 
     with ExitStack() as ctx:

@@ -14,418 +14,89 @@ ADD = mybir.AluOpType.add
 COPY = mybir.ActivationFunctionType.Copy
 
 P = 128
-TOK, DIM, FEAT = 1024, 1536, 1536
+TOKENS, DIM, FEATURES = 1024, 1536, 1536
 HEADS, HD = 4, 128
 INNER = HEADS * HD
 J = 4
-GROUP = P * J
-GROUPS = TOK // GROUP
-FLOPS = 2 * 2 * TOK * DIM * FEAT
-BYTES = 2 * (TOK * DIM + DIM * FEAT + 2 * HD + TOK * FEAT) + 4 * (
-    TOK * 2 * INNER + TOK * 2 * HEADS + TOK * DIM + DIM * FEAT
+GROUPS = TOKENS // (P * J)
+BANK = 512
+THIRDS = FEATURES // BANK
+Q, K, V = 0, 1, 2
+
+FLOPS = 2 * 2 * TOKENS * DIM * FEATURES
+BYTES = 2 * (TOKENS * DIM + DIM * FEATURES + 2 * HD + TOKENS * FEATURES) + 4 * (
+    2 * TOKENS * INNER + 2 * TOKENS * HEADS + TOKENS * DIM + DIM * FEATURES
 )
+TRANSPOSE_BANKS = 3
+LAST_DZ = (1, 1)
+
+ORDER = """
+lg.2.0.1 k lg.0 k k iz.2.0.V tz.2.0.0 lg.2.1.1 k qz.2.0 k k gz.2.0.0.V tz.2.0.1 a.0.0.0 ls.0.0 k k
+gz.2.0.1.S qt.2.0.0 k a.0.0.1 tz.2.1.1 qt.2.0.1 mz.2.1.0 a.0.0.2 gz.2.1.1.S tz.2.1.0 lx.0 qt.2.1.1
+cz.2.1.0.S a.0.0.3 mz.2.1.1 gz.2.1.0.S m.0.0.0 cz.2.1.1.S d.0.0.1.V d.0.0.0.S qt.2.1.0 c.0.0.0
+m.0.0.2 c.0.0.1 lw.2 qz.2.1 d.0.0.2.S f.0.0.0 mx.0.0.0 ix.0.2.S ix.0.1.V c.0.0.2 f.0.0.1 mx.0.0.1
+qx.0.1 lx.1 cx.0.0.0.S tz.0.0.0 f.0.0.2 cx.0.0.1.S m.0.0.3 tw.2.2.0 gz.0.0.0.S qx.0.0 tw.2.0.1
+d.0.0.3.S qt.0.0.0 tw.2.1.1 qx.0.2 gw.2.0.1.S c.0.0.3 gw.2.1.1.S qw.2.0.1 tw.2.2.1 f.0.0.3 lg.1
+gw.2.2.0.S qw.2.1.1 tw.2.0.0 qw.2.2.0 ix.1.1.S ix.1.0.V tz.0.0.1 gw.2.2.1.V lw.0 qx.1.0 tw.2.1.0
+gz.0.0.1.V gw.2.0.0.S a.1.0.0 ix.1.2.S p1.2.2 qx.1.1 a.1.0.1 p1.2.0 qw.2.2.1 ls.1.0 a.1.0.2 p1.2.4
+gw.2.1.0.S qx.1.2 p1.2.1 e1.2.0.S a.1.0.3 e1.2.4.S tw.0.1.1 e1.2.1.S e1.2.2.V p1.2.10 lw.1
+gw.0.1.1.S qt.0.0.1 tw.0.0.0 qw.2.0.0 e1.2.10.S qw.2.1.0 qw.0.1.1 p1.2.5 gw.0.0.0.S m.1.0.3 tw.0.1.0
+d.1.0.0.V e1.2.5.S tw.0.2.1 d.1.0.3.S qw.0.0.0 p1.2.3 gw.0.1.0.S c.1.0.0 d.1.0.2.V tw.0.0.1 ls.0.1
+gw.0.2.1.S tw.0.2.0 qw.0.1.0 e1.2.3.S m.1.0.1 p1.2.6 gw.0.0.1.S c.1.0.3 c.1.0.2 f.1.0.0 gw.0.2.0.S
+tw.1.1.1 d.1.0.1.S qw.0.0.1 tw.1.2.0 a.0.1.0 s1.2.4 gw.1.1.1.S p1.2.7 qw.0.2.0 gw.1.2.0.S qw.0.2.1
+tw.1.0.0 qw.1.1.1 s1.2.2 c.1.0.1 qw.1.2.0 tw.1.1.0 m.0.1.0 gw.1.0.0.S tw.1.0.1 f.1.0.1 gw.1.1.0.S
+mz.0.0.0 s1.2.0 e1.2.6.S qw.1.0.0 a.0.1.1 tz.1.0.0 d.0.1.0.S ls.1.1 cz.0.0.0.V p1.2.8 e1.2.7.S
+d.0.1.1.V p1.2.11 gw.1.0.1.S gz.1.0.0.S mz.0.0.1 qw.1.0.1 e1.2.8.S c.0.1.1 f.1.0.2 p1.2.9 e1.2.11.S
+qt.1.0.0 s1.2.6 cz.0.0.1.S tw.1.2.1 f.1.0.3 e1.2.9.S p0.0.0.0 a.0.1.2 gw.1.2.1.S s1.2.10 c.0.1.0
+qw.1.1.0 iz.1.0.S tz.1.0.1 a.0.1.3 p0.0.0.2 qw.1.2.1 s1.2.8 m.0.1.3 p0.0.1.0 f.0.1.0 p0.0.0.1
+d.0.1.2.V gz.1.0.1.S e0.0.1.0.S p0.0.1.2 f.0.1.1 e0.0.0.0.S p0.0.1.1 c.0.1.2 qt.1.0.1 d.0.1.3.S
+f.0.1.2 e0.0.1.2.S p0.0.3.0 c.0.1.3 a.1.1.0 e0.0.0.1.S p0.0.2.0 f.0.1.3 e0.0.1.1.S e0.0.0.2.S
+p0.0.3.2 d.1.1.0.V s0.0.1 iz.0.1.S p0.0.3.1 qz.0.0 e0.0.3.0.V p0.0.2.2 s0.0.0 a.1.1.1 tz.0.1.1
+e0.0.3.1.V e0.0.3.2.S tz.0.1.0 qz.0.1 e0.0.2.0.S s0.0.3 p0.0.2.1 m.1.1.1 gz.0.1.0.S c.1.1.0 qz.1.0
+e0.0.2.2.S p1.0.10 e0.0.2.1.V d.1.1.1.S p1.0.0 f.1.1.0 p1.0.11 s0.0.2 e1.0.10.S p1.0.6 c.1.1.1
+e1.0.0.S qt.0.1.0 f.1.1.1 p1.0.1 e1.0.11.S p1.0.7 gz.0.1.1.V e1.0.6.S s1.0.10 a.1.1.2 e1.0.1.S
+tz.1.1.0 e1.0.7.S qt.0.1.1 p1.0.8 a.1.1.3 s1.0.0 gz.1.1.0.S p1.0.2 d.1.1.2.V e1.0.8.S p1.0.9
+e1.0.2.S s1.0.6 p1.0.3 qt.1.1.0 e1.0.9.S c.1.1.2 p1.0.4 m.1.1.3 p0.1.0.0 f.1.1.2 d.1.1.3.S s1.0.8
+e1.0.3.V p1.0.5 e1.0.4.S c.1.1.3 p0.1.0.2 e0.1.0.0.S f.1.1.3 s1.0.2 e1.0.5.S p0.1.1.0 iz.1.1.V
+e0.1.0.2.S s1.0.4 p0.1.0.1 e0.1.1.0.V p0.1.1.2 e0.1.0.1.S qz.1.1 p0.1.1.1 s0.1.0 e0.1.1.2.S p1.1.2
+e0.1.1.1.V p1.1.10 e1.1.2.S p1.1.3 s0.1.1 e1.1.10.S p1.1.11 e1.1.3.S p1.1.4 e1.1.11.V tz.1.1.1
+s1.1.2 e1.1.4.V p1.1.5 gz.1.1.1.V p1.1.8 qt.1.1.1 e1.1.5.V s1.1.10 p1.1.6 e1.1.8.V p1.1.9 p1.1.7
+e1.1.6.V s1.1.4 e1.1.9.S tz.1.1.2 e1.1.7.V p0.1.2.0 gz.1.1.2.V s1.1.8 p1.1.0 qt.1.1.2 e0.1.2.0.V
+p0.1.2.1 e1.1.0.S s1.1.6 p1.1.1 e0.1.2.1.S p0.1.2.2 e1.1.1.S st.1.2.0 p0.1.3.0 st.1.2.1 e0.1.2.2.S
+s1.1.0 p0.1.3.1 e0.1.3.0.S p0.1.3.2 e0.1.3.1.S st.1.2.2 st.1.3.0 e0.1.3.2.S st.1.3.1 st.1.3.2
+"""
 
 
 def tile_naswinattention_pa_v_kernel(
     tc, vid, w_qkv, b_qkv, q_scale, k_scale, qk_pre, qk_rstd, grad_q, grad_k, grad_v, out_0, out_1
 ):
     nc = tc.nc
-    TP_BUFS, ACC_BUFS = 3, 5
-    BIG_BUFS, PRE_BUFS, INTER_BUFS, GROUPED_BUFS, RES_BUFS, DZ_BUFS, LEAD_BUFS, PROD_BUFS = 4, 3, 3, 5, 4, 3, 4, 1
-    UNITS = {(0, 0): [[0, 1], [2, 3]], (0, 1): [[0, 1], [2, 3]], (1, 0): [[0, 1], [2, 3]], (1, 1): [[0, 1], [2], [3]], (2, 0): [[0, 1], [2, 3]], (2, 1): [[0, 1], [2, 3]]}
-    SEQ = [
-        ('D', ('ld', 'g2')),
-        ('PE', ('DM', 8)),
-        ('D', ('ld', 'g0')),
-        ('PE', ('DM', 4)),
-        ('PE', ('DM', 15)),
-        ('S', ('DI', 2, 0)),
-        ('PE', ('DT', 2, 1, 1)),
-        ('PE', ('PI', 'DI', 2, 1, 0)),
-        ('V', ('DC', 2, 1, 1)),
-        ('D', ('ld', 'w1')),
-        ('PE', ('DT', 2, 1, 0)),
-        ('V', ('TQ', 2, 1, 1)),
-        ('PE', ('DM', 3)),
-        ('V', ('DC', 2, 1, 0)),
-        ('S', ('IC', 'DI', 2, 1, 0)),
-        ('PE', ('DM', 10)),
-        ('V', ('DQ', 2, 0)),
-        ('PE', ('DT', 2, 0, 0)),
-        ('V', ('TQ', 2, 1, 0)),
-        ('PE', ('DM', 9)),
-        ('V', ('L', 0, 0, 0)),
-        ('S', ('DC', 2, 0, 0)),
-        ('PE', ('DT', 2, 0, 1)),
-        ('PE', ('PI', 'DI', 2, 1, 1)),
-        ('V', ('TQ', 2, 0, 0)),
-        ('V', ('L', 0, 0, 1)),
-        ('D', ('ld', 'p00')),
-        ('PE', ('DM', 11)),
-        ('V', ('DC', 2, 0, 1)),
-        ('S', ('IC', 'DI', 2, 1, 1)),
-        ('PE', ('DM', 12)),
-        ('V', ('L', 0, 0, 2)),
-        ('PE', ('WT', 1, 1, 0)),
-        ('V', ('TQ', 2, 0, 1)),
-        ('PE', ('WT', 1, 0, 1)),
-        ('S', ('WC', 1, 1, 0)),
-        ('V', ('L', 0, 0, 3)),
-        ('PE', ('WT', 1, 1, 1)),
-        ('S', ('WC', 1, 0, 1)),
-        ('D', ('ld', 'v1')),
-        ('V', ('DQ', 2, 1)),
-        ('PE', ('WT', 1, 2, 0)),
-        ('S', ('WC', 1, 1, 1)),
-        ('V', ('WQ', 1, 0, 1)),
-        ('PE', ('WT', 1, 2, 1)),
-        ('V', ('WQ', 1, 1, 0)),
-        ('S', ('WC', 1, 2, 0)),
-        ('PE', ('WT', 1, 0, 0)),
-        ('V', ('DP', 0, 0, 2)),
-        ('S', ('WC', 1, 2, 1)),
-        ('V', ('WQ', 1, 1, 1)),
-        ('V', ('D', 0, 0, 3)),
-        ('S', ('D', 0, 0, 2)),
-        ('PE', ('DM', 5)),
-        ('S', ('WC', 1, 0, 0)),
-        ('PE', ('DM', 0)),
-        ('V', ('DP', 0, 0, 0)),
-        ('D', ('ld', 'g1')),
-        ('V', ('C', 0, 0, 3)),
-        ('V', ('WQ', 1, 0, 0)),
-        ('S', ('D', 0, 0, 0)),
-        ('V', ('D', 0, 0, 1)),
-        ('PE', ('PI', 'VI', 1, 2, 0)),
-        ('S', ('VI', 1, 0)),
-        ('V', ('C', 0, 0, 0)),
-        ('V', ('WQ', 1, 2, 1)),
-        ('V', ('C', 0, 0, 1)),
-        ('V', ('F', 0, 0, 0)),
-        ('PE', ('PI', 'VI', 1, 1, 0)),
-        ('V', ('WQ', 1, 2, 0)),
-        ('D', ('ld', 'v0')),
-        ('V', ('C', 0, 0, 2)),
-        ('PE', ('PI', 'VI', 1, 2, 1)),
-        ('V', ('F', 0, 0, 1)),
-        ('S', ('IC', 'VI', 1, 2, 0)),
-        ('V', ('L', 1, 0, 0)),
-        ('S', ('IC', 'VI', 1, 1, 0)),
-        ('V', ('F', 0, 0, 2)),
-        ('PE', ('PI', 'VI', 1, 1, 1)),
-        ('S', ('IC', 'VI', 1, 2, 1)),
-        ('V', ('VQ', 1, 0)),
-        ('PE', ('DT', 0, 0, 0)),
-        ('S', ('IC', 'VI', 1, 1, 1)),
-        ('V', ('F', 0, 0, 3)),
-        ('S', ('DC', 0, 0, 0)),
-        ('D', ('ld', 'p10')),
-        ('V', ('L', 1, 0, 1)),
-        ('PE', ('DT', 0, 0, 1)),
-        ('S', ('DI', 0, 0)),
-        ('V', ('VQ', 1, 2)),
-        ('PE', ('PI', 'VI', 0, 1, 0)),
-        ('V', ('VQ', 1, 1)),
-        ('V', ('VI', 0, 0)),
-        ('PE', ('PI', 'VI', 0, 1, 1)),
-        ('D', ('ld', 'w0')),
-        ('S', ('IC', 'VI', 0, 1, 0)),
-        ('V', ('DQ', 0, 0)),
-        ('S', ('DC', 0, 0, 1)),
-        ('V', ('VQ', 0, 0)),
-        ('S', ('IC', 'VI', 0, 1, 1)),
-        ('V', ('TQ', 0, 0, 1)),
-        ('S', ('VI', 0, 2)),
-        ('PE', ('O1', 2, 2)),
-        ('V', ('VQ', 0, 1)),
-        ('PE', ('O1', 2, 0)),
-        ('V', ('D', 1, 0, 1)),
-        ('PE', ('O1', 2, 4)),
-        ('D', ('ld', 'w2')),
-        ('V', ('L', 1, 0, 2)),
-        ('PE', ('O1', 2, 6)),
-        ('V', ('C', 1, 0, 1)),
-        ('PE', ('O1', 2, 5)),
-        ('V', ('DP', 1, 0, 0)),
-        ('S', ('X1', 2, 4)),
-        ('V', ('D', 1, 0, 2)),
-        ('PE', ('WT', 0, 0, 0)),
-        ('S', ('D', 1, 0, 0)),
-        ('PE', ('WT', 0, 1, 0)),
-        ('S', ('X1', 2, 6)),
-        ('V', ('VQ', 0, 2)),
-        ('PE', ('WT', 0, 1, 1)),
-        ('S', ('WC', 0, 0, 0)),
-        ('V', ('C', 1, 0, 2)),
-        ('V', ('L', 1, 0, 3)),
-        ('PE', ('O1', 2, 7)),
-        ('S', ('WC', 0, 1, 0)),
-        ('D', ('ld', 'p11')),
-        ('V', ('WQ', 0, 0, 0)),
-        ('PE', ('WT', 0, 2, 0)),
-        ('S', ('X1', 2, 5)),
-        ('V', ('DP', 1, 0, 3)),
-        ('PE', ('WT', 0, 0, 1)),
-        ('S', ('X1', 2, 7)),
-        ('V', ('WQ', 0, 1, 0)),
-        ('V', ('WC', 0, 1, 1)),
-        ('S', ('WC', 0, 2, 0)),
-        ('PE', ('O1', 2, 10)),
-        ('V', ('C', 1, 0, 0)),
-        ('V', ('TQ', 0, 0, 0)),
-        ('S', ('WC', 0, 0, 1)),
-        ('PE', ('WT', 2, 0, 1)),
-        ('V', ('WQ', 0, 2, 0)),
-        ('D', ('S1', 2, 6)),
-        ('V', ('WQ', 0, 1, 1)),
-        ('S', ('X1', 2, 10)),
-        ('PE', ('WT', 2, 2, 1)),
-        ('V', ('WQ', 0, 0, 1)),
-        ('S', ('WC', 2, 0, 1)),
-        ('V', ('F', 1, 0, 0)),
-        ('PE', ('WT', 2, 1, 0)),
-        ('S', ('X1', 2, 0)),
-        ('V', ('WQ', 2, 0, 1)),
-        ('PE', ('WT', 2, 2, 0)),
-        ('D', ('S1', 2, 4)),
-        ('V', ('F', 1, 0, 1)),
-        ('S', ('WC', 2, 1, 0)),
-        ('PE', ('O1', 2, 11)),
-        ('V', ('L', 0, 1, 0)),
-        ('S', ('WC', 2, 2, 0)),
-        ('D', ('ld', 'p01')),
-        ('PE', ('WT', 0, 2, 1)),
-        ('S', ('WC', 2, 2, 1)),
-        ('V', ('WQ', 2, 1, 0)),
-        ('V', ('WQ', 2, 2, 0)),
-        ('PE', ('WT', 2, 1, 1)),
-        ('S', ('X1', 2, 11)),
-        ('V', ('L', 0, 1, 1)),
-        ('PE', ('DT', 1, 0, 0)),
-        ('S', ('D', 1, 0, 3)),
-        ('V', ('WC', 2, 1, 1)),
-        ('PE', ('O1', 2, 8)),
-        ('S', ('DC', 1, 0, 0)),
-        ('V', ('WQ', 2, 2, 1)),
-        ('V', ('WQ', 2, 1, 1)),
-        ('PE', ('WT', 2, 0, 0)),
-        ('S', ('WC', 0, 2, 1)),
-        ('D', ('S1', 2, 10)),
-        ('V', ('TQ', 1, 0, 0)),
-        ('V', ('C', 1, 0, 3)),
-        ('V', ('F', 1, 0, 2)),
-        ('S', ('X1', 2, 8)),
-        ('PE', ('O1', 2, 9)),
-        ('S', ('WC', 2, 0, 0)),
-        ('PE', ('O1', 2, 3)),
-        ('V', ('WQ', 0, 2, 1)),
-        ('V', ('F', 1, 0, 3)),
-        ('S', ('X1', 2, 9)),
-        ('PE', ('O0', 0, 1, 0)),
-        ('V', ('WQ', 2, 0, 0)),
-        ('S', ('X1', 2, 2)),
-        ('D', ('S1', 2, 8)),
-        ('V', ('D', 0, 1, 0)),
-        ('PE', ('O0', 0, 0, 0)),
-        ('S', ('DI', 1, 0)),
-        ('V', ('L', 0, 1, 2)),
-        ('PE', ('O0', 0, 1, 1)),
-        ('V', ('C', 0, 1, 0)),
-        ('V', ('D', 0, 1, 1)),
-        ('PE', ('O0', 0, 0, 1)),
-        ('V', ('D', 0, 1, 2)),
-        ('PE', ('DT', 1, 0, 1)),
-        ('S', ('X1', 2, 3)),
-        ('S', ('X0', 0, 1, 0)),
-        ('D', ('S1', 2, 2)),
-        ('V', ('C', 0, 1, 1)),
-        ('PE', ('O0', 0, 0, 2)),
-        ('V', ('F', 0, 1, 0)),
-        ('S', ('DC', 1, 0, 1)),
-        ('V', ('C', 0, 1, 2)),
-        ('V', ('L', 0, 1, 3)),
-        ('PE', ('O0', 0, 1, 2)),
-        ('S', ('X0', 0, 0, 0)),
-        ('S', ('X0', 0, 1, 1)),
-        ('V', ('TQ', 1, 0, 1)),
-        ('PE', ('O1', 2, 1)),
-        ('V', ('DP', 0, 1, 3)),
-        ('S', ('X0', 0, 0, 2)),
-        ('PE', ('O0', 0, 3, 0)),
-        ('V', ('F', 0, 1, 1)),
-        ('S', ('X0', 0, 1, 2)),
-        ('V', ('L', 1, 1, 0)),
-        ('S', ('D', 0, 1, 3)),
-        ('PE', ('O0', 0, 2, 0)),
-        ('D', ('S0', 0, 1)),
-        ('V', ('F', 0, 1, 2)),
-        ('S', ('X0', 0, 3, 0)),
-        ('PE', ('O0', 0, 3, 2)),
-        ('V', ('C', 0, 1, 3)),
-        ('V', ('DP', 1, 1, 0)),
-        ('S', ('X1', 2, 1)),
-        ('PE', ('O0', 0, 3, 1)),
-        ('V', ('F', 0, 1, 3)),
-        ('S', ('X0', 0, 0, 1)),
-        ('D', ('S1', 2, 0)),
-        ('S', ('D', 1, 1, 0)),
-        ('V', ('L', 1, 1, 1)),
-        ('PE', ('DT', 0, 1, 0)),
-        ('S', ('X0', 0, 3, 1)),
-        ('V', ('DI', 0, 1)),
-        ('PE', ('DT', 0, 1, 1)),
-        ('D', ('S0', 0, 0)),
-        ('S', ('DC', 0, 1, 0)),
-        ('PE', ('O0', 0, 2, 1)),
-        ('S', ('X0', 0, 3, 2)),
-        ('V', ('TQ', 0, 1, 0)),
-        ('S', ('X0', 0, 2, 0)),
-        ('V', ('DQ', 0, 1)),
-        ('PE', ('O0', 0, 2, 2)),
-        ('D', ('S0', 0, 3)),
-        ('S', ('DC', 0, 1, 1)),
-        ('V', ('L', 1, 1, 2)),
-        ('PE', ('O1', 0, 2)),
-        ('S', ('X0', 0, 2, 1)),
-        ('V', ('C', 1, 1, 0)),
-        ('V', ('DP', 1, 1, 1)),
-        ('PE', ('O1', 0, 8)),
-        ('S', ('X0', 0, 2, 2)),
-        ('V', ('TQ', 0, 1, 1)),
-        ('PE', ('O1', 0, 4)),
-        ('V', ('D', 1, 1, 2)),
-        ('S', ('D', 1, 1, 1)),
-        ('D', ('S0', 0, 2)),
-        ('PE', ('O1', 0, 9)),
-        ('S', ('X1', 0, 8)),
-        ('PE', ('O1', 0, 3)),
-        ('V', ('C', 1, 1, 1)),
-        ('V', ('F', 1, 1, 0)),
-        ('S', ('X1', 0, 2)),
-        ('PE', ('O1', 0, 10)),
-        ('V', ('C', 1, 1, 2)),
-        ('V', ('X1', 0, 4)),
-        ('S', ('X1', 0, 9)),
-        ('PE', ('O1', 0, 0)),
-        ('V', ('F', 1, 1, 1)),
-        ('S', ('X1', 0, 3)),
-        ('D', ('S1', 0, 8)),
-        ('PE', ('O1', 0, 5)),
-        ('V', ('DQ', 1, 0)),
-        ('S', ('X1', 0, 0)),
-        ('PE', ('O1', 0, 1)),
-        ('V', ('F', 1, 1, 2)),
-        ('D', ('S1', 0, 2)),
-        ('PE', ('DT', 1, 1, 0)),
-        ('S', ('X1', 0, 1)),
-        ('V', ('X1', 0, 5)),
-        ('PE', ('DT', 1, 1, 1)),
-        ('S', ('DC', 1, 1, 0)),
-        ('V', ('L', 1, 1, 3)),
-        ('PE', ('O1', 0, 6)),
-        ('D', ('S1', 0, 0)),
-        ('S', ('DC', 1, 1, 1)),
-        ('PE', ('O1', 0, 11)),
-        ('V', ('TQ', 1, 1, 0)),
-        ('S', ('X1', 0, 10)),
-        ('V', ('TQ', 1, 1, 1)),
-        ('V', ('DP', 1, 1, 3)),
-        ('PE', ('O1', 0, 7)),
-        ('S', ('X1', 0, 11)),
-        ('V', ('X1', 0, 6)),
-        ('D', ('S1', 0, 4)),
-        ('PE', ('O0', 1, 2, 0)),
-        ('S', ('D', 1, 1, 3)),
-        ('PE', ('O0', 1, 0, 0)),
-        ('S', ('X1', 0, 7)),
-        ('V', ('C', 1, 1, 3)),
-        ('D', ('S1', 0, 10)),
-        ('V', ('F', 1, 1, 3)),
-        ('S', ('X0', 1, 2, 0)),
-        ('PE', ('O0', 1, 2, 1)),
-        ('V', ('DI', 1, 1)),
-        ('S', ('X0', 1, 0, 0)),
-        ('PE', ('O0', 1, 0, 2)),
-        ('D', ('S1', 0, 6)),
-        ('S', ('X0', 1, 2, 1)),
-        ('PE', ('O0', 1, 0, 1)),
-        ('S', ('X0', 1, 0, 2)),
-        ('V', ('DQ', 1, 1)),
-        ('D', ('S0', 1, 2, 0)),
-        ('PE', ('O0', 1, 2, 2)),
-        ('V', ('X0', 1, 0, 1)),
-        ('D', ('S0', 1, 2, 1)),
-        ('PE', ('O1', 1, 8)),
-        ('D', ('S0', 1, 0)),
-        ('S', ('X0', 1, 2, 2)),
-        ('PE', ('O1', 1, 6)),
-        ('V', ('X1', 1, 8)),
-        ('PE', ('O1', 1, 9)),
-        ('S', ('X1', 1, 6)),
-        ('PE', ('O1', 1, 7)),
-        ('V', ('X1', 1, 9)),
-        ('D', ('S0', 1, 2, 2)),
-        ('PE', ('O1', 1, 0)),
-        ('S', ('X1', 1, 7)),
-        ('D', ('S1', 1, 8)),
-        ('PE', ('O1', 1, 2)),
-        ('S', ('X1', 1, 0)),
-        ('PE', ('O1', 1, 1)),
-        ('V', ('X1', 1, 2)),
-        ('PE', ('O1', 1, 3)),
-        ('D', ('S1', 1, 6)),
-        ('S', ('X1', 1, 1)),
-        ('PE', ('O1', 1, 4)),
-        ('V', ('X1', 1, 3)),
-        ('PE', ('O0', 1, 1, 0)),
-        ('V', ('X1', 1, 4)),
-        ('D', ('S1', 1, 0)),
-        ('PE', ('O1', 1, 5)),
-        ('PE', ('O0', 1, 1, 2)),
-        ('V', ('X0', 1, 1, 0)),
-        ('D', ('S1', 1, 2)),
-        ('V', ('X1', 1, 5)),
-        ('PE', ('O0', 1, 1, 1)),
-        ('V', ('X0', 1, 1, 2)),
-        ('D', ('S1', 1, 4)),
-        ('PE', ('DT', 1, 1, 2)),
-        ('S', ('X0', 1, 1, 1)),
-        ('PE', ('O1', 1, 10)),
-        ('V', ('DC', 1, 1, 2)),
-        ('V', ('TQ', 1, 1, 2)),
-        ('D', ('S0', 1, 1)),
-        ('PE', ('O1', 1, 11)),
-        ('S', ('X1', 1, 10)),
-        ('PE', ('O0', 1, 3, 0)),
-        ('S', ('X1', 1, 11)),
-        ('D', ('S1', 1, 10)),
-        ('PE', ('O0', 1, 3, 1)),
-        ('S', ('X0', 1, 3, 0)),
-        ('PE', ('O0', 1, 3, 2)),
-        ('V', ('X0', 1, 3, 1)),
-        ('D', ('S0', 1, 3, 0)),
-        ('S', ('X0', 1, 3, 2)),
-        ('D', ('S0', 1, 3, 1)),
-        ('D', ('S0', 1, 3, 2)),
-    ]
-
     with ExitStack() as ctx:
         keep = ctx.enter_context(tc.tile_pool(name="keep", bufs=1))
         raws = ctx.enter_context(tc.tile_pool(name="raws", bufs=1))
         work = ctx.enter_context(tc.tile_pool(name="work", bufs=2))
-        outs = ctx.enter_context(tc.tile_pool(name="outs", bufs=8))
-        tps = ctx.enter_context(tc.psum_pool(name="tps", bufs=TP_BUFS))
-        accs = ctx.enter_context(tc.psum_pool(name="accs", bufs=ACC_BUFS))
+        outs = ctx.enter_context(tc.tile_pool(name="outs", bufs=1))
+        banks = ctx.enter_context(tc.psum_pool(name="banks", bufs=TRANSPOSE_BANKS))
+        accs = ctx.enter_context(tc.psum_pool(name="accs", bufs=8 - TRANSPOSE_BANKS))
         ctx.enter_context(tc.manual_schedule())
 
-        dz_codes = [keep.tile([P, FEAT], U32, align_bytes=64, name=f"dzc{g}") for g in range(GROUPS)]
-        dz_scales = [keep.tile([P, FEAT], U8, align_bytes=64, name=f"dzs{g}") for g in range(GROUPS)]
-        vid_codes = [keep.tile([P, DIM], U32, align_bytes=64, name=f"vc{g}") for g in range(GROUPS)]
-        vid_scales = [keep.tile([P, DIM], U8, align_bytes=64, name=f"vs{g}") for g in range(GROUPS)]
-        dzt_codes = [keep.tile([P, TOK], U32, align_bytes=64, name=f"dtc{f}") for f in range(3)]
-        dzt_scales = [keep.tile([P, TOK], U8, align_bytes=64, name=f"dts{f}") for f in range(3)]
-        w_codes = [keep.tile([P, DIM], U32, align_bytes=64, name=f"wc{f}") for f in range(3)]
-        w_scales = [keep.tile([P, DIM], U8, align_bytes=64, name=f"ws{f}") for f in range(3)]
+        def quantised(name, count, width):
+            return [
+                (
+                    keep.tile([P, width], U32, align_bytes=64, name=f"{name}_codes{i}"),
+                    keep.tile([P, width], U8, align_bytes=64, name=f"{name}_scales{i}"),
+                )
+                for i in range(count)
+            ]
+
+        dz_tok = quantised("dz_tok", GROUPS, FEATURES)
+        vid_tok = quantised("vid_tok", GROUPS, DIM)
+        dz_feat = quantised("dz_feat", THIRDS, TOKENS)
+        w_feat = quantised("w_feat", THIRDS, DIM)
+
+        def quantize(operand, cols, values, fmt):
+            codes, scales = operand
+            nc.vector.quantize_mx(out=codes[:, cols].bitcast(fmt), scales=scales[:, cols], in_=values)
 
         gains_row = keep.tile([P, 2 * HD], BF16, name="gains_row")
         nc.vector.memset(gains_row[:], 0.0)
@@ -434,70 +105,58 @@ def tile_naswinattention_pa_v_kernel(
         rstd = keep.tile([P, GROUPS, J * 2 * HEADS], F32, name="rstd")
         nc.scalar.dma_start(out=rstd[:], in_=qk_rstd.rearrange("(g p j) c h -> p g (j c h)", g=GROUPS, j=J))
 
-        def load_grad(grad, name):
-            raw = raws.tile([P, GROUPS, J * INNER], BF16, name=name)
-            for n in range(2):
-                rows = grad[n].rearrange("(g x b j) h d -> b x g (j h d)", g=GROUPS, b=2, j=J)
-                for b in range(2):
-                    nc.sync.dma_start(out=raw[2 * n + b : P : 4, :, :], in_=rows[b])
-            return raw
+        def rstd_cols(which, j):
+            lo = (2 * j + which) * HEADS
+            return slice(lo, lo + HEADS)
 
-        vid_raw = {}
-        pre_raw = {}
-        w_raw = {}
-        grad_raw = {}
-        vid_rows = vid.rearrange("(g p j) w -> g p j w", g=GROUPS, j=J)
-        pre_rows = qk_pre.rearrange("(g p j) c h d -> g c p j (h d)", g=GROUPS, j=J)
-        w_rows = w_qkv.rearrange("(n r i) f -> n r i f", n=3, i=4)
-
-        def load_vid(g):
-            vid_raw[g] = raws.tile([P, J, DIM], BF16, tag="big", bufs=BIG_BUFS, name=f"vid{g}")
-            for h in range(2):
-                nc.sync.dma_start(out=vid_raw[g][:, 2 * h : 2 * h + 2, :], in_=vid_rows[g][:, 2 * h : 2 * h + 2, :])
-
-        def load_w(n):
-            w_raw[n] = raws.tile([P, 4, FEAT], BF16, tag="big", bufs=BIG_BUFS, name=f"w{n}")
-            for h in range(2):
-                nc.sync.dma_start(out=w_raw[n][:, 2 * h : 2 * h + 2, :], in_=w_rows[n][:, 2 * h : 2 * h + 2, :])
-
-        def load_pre(f, g):
-            pre_raw[f, g] = raws.tile([P, J, INNER], F32, tag="pre", bufs=PRE_BUFS, name=f"pre{f}{g}")
-            nc.sync.dma_start(out=pre_raw[f, g][:], in_=pre_rows[g, f])
-
-        def pre(f, g, j, lo, hi):
-            return pre_raw[f, g][:, j, lo:hi]
-
-        def load(name):
-            k = [int(x) for x in name[1:]]
-            if name[0] == "g":
-                grad_raw[k[0]] = load_grad((grad_q, grad_k, grad_v)[k[0]], f"grad{k[0]}")
-            elif name[0] == "v":
-                load_vid(*k)
-            elif name[0] == "w":
-                load_w(*k)
-            else:
-                load_pre(*k)
-
-        ident = keep.tile([P, P], F32, name="ident")
-        make_identity(nc, ident[:])
+        identity = keep.tile([P, P], F32, name="identity")
+        make_identity(nc, identity[:])
         ones = keep.tile([P, P], BF16, name="ones")
         nc.vector.memset(ones[:], 1.0)
-        ident_bf = keep.tile([P, P], BF16, name="ident_bf")
-        make_identity(nc, ident_bf[:])
-        zeros = keep.tile([P, 512], BF16, name="zeros")
+        identity_bf16 = keep.tile([P, P], BF16, name="identity_bf16")
+        make_identity(nc, identity_bf16[:])
+        zeros = keep.tile([P, BANK], BF16, name="zeros")
         nc.vector.memset(zeros[:], 0.0)
-        warm = keep.tile([P, 1], F32, name="warm")
-        nc.vector.memset(warm[:], 0.0)
-        nc.scalar.copy(warm[:], warm[:])
+        table = keep.tile([P, 1], F32, name="table")
+        nc.vector.memset(table[:], 0.0)
+        nc.scalar.copy(table[:], table[:])
         gains = keep.tile([P, 2 * HD], F32, name="gains")
-        gains_ps = tps.tile([P, 2 * HD], F32, tag="tp", name="gains_ps")
-        nc.tensor.matmul(gains_ps[:], lhsT=ones[:], rhs=gains_row[:], start=True, stop=True)
-        nc.scalar.copy(gains[:], gains_ps[:])
-        nr2 = keep.tile([P, GROUPS, J * 2 * HEADS], F32, name="nr2")
-        nc.vector.scalar_tensor_tensor(out=nr2[:], in0=rstd[:], scalar=-1.0 / HD, in1=rstd[:], op0=MULT, op1=MULT)
+        gains_bank = banks.tile([P, 2 * HD], F32, tag="bank", name="gains_bank")
+        nc.tensor.matmul(gains_bank[:], lhsT=ones[:], rhs=gains_row[:], start=True, stop=True)
+        nc.scalar.copy(gains[:], gains_bank[:])
+        neg_r2 = keep.tile([P, GROUPS, J * 2 * HEADS], F32, name="neg_r2")
+        nc.vector.scalar_tensor_tensor(
+            out=neg_r2[:], in0=rstd[:], scalar=-1.0 / HD, in1=rstd[:], op0=MULT, op1=MULT
+        )
 
-        t_inter, t_bank, t_grp, t_acc, t_res = {}, {}, {}, {}, {}
-        dz_tiles, lead, sums, coef, prods = {}, {}, {}, {}, {}
+        grads = (grad_q, grad_k, grad_v)
+        grad_raw, vid_raw, w_raw, saved = {}, {}, {}, {}
+
+        def load_grad(which, first=0, count=GROUPS):
+            if which not in grad_raw:
+                grad_raw[which] = raws.tile([P, GROUPS, J * INNER], BF16, name=f"grad{which}")
+            groups = slice(first, first + count)
+            for n in range(2):
+                rows = grads[which][n].rearrange("(g x b j) h d -> b x g (j h d)", g=GROUPS, b=2, j=J)
+                for b in range(2):
+                    nc.sync.dma_start(out=grad_raw[which][2 * n + b : P : 4, groups, :], in_=rows[b][:, groups, :])
+
+        def load_vid(g):
+            rows = vid.rearrange("(g p j) w -> g p j w", g=GROUPS, j=J)[g]
+            vid_raw[g] = raws.tile([P, J, DIM], BF16, tag="big", bufs=4, name=f"vid{g}")
+            for half in (slice(0, 2), slice(2, 4)):
+                nc.sync.dma_start(out=vid_raw[g][:, half, :], in_=rows[:, half, :])
+
+        def load_w(n):
+            rows = w_qkv.rearrange("(n r i) f -> n r i f", n=THIRDS, i=4)[n]
+            w_raw[n] = raws.tile([P, 4, FEATURES], BF16, tag="big", bufs=4, name=f"w{n}")
+            for half in (slice(0, 2), slice(2, 4)):
+                nc.sync.dma_start(out=w_raw[n][:, half, :], in_=rows[:, half, :])
+
+        def load_saved(which, g):
+            rows = qk_pre.rearrange("(g p j) c h d -> g c p j (h d)", g=GROUPS, j=J)[g, which]
+            saved[which, g] = raws.tile([P, J, INNER], F32, tag="saved", bufs=3, name=f"saved{which}{g}")
+            nc.sync.dma_start(out=saved[which, g][:], in_=rows)
 
         def copy(engine, dst, src):
             if engine == "V":
@@ -505,245 +164,272 @@ def tile_naswinattention_pa_v_kernel(
             else:
                 nc.scalar.copy(dst, src)
 
-        def il_source(kind, a, c):
-            if kind == "VI":
-                return vid_raw[a][:, :, c * 512 : (c + 1) * 512]
-            if a == 2:
-                return grad_raw[2][:, c, :].rearrange("p (j w) -> p j w", j=J)
-            return dz_tiles[a, c][:]
+        dz, scaled, products, dots, coefs = {}, {}, {}, {}, {}
 
-        def new_inter(key):
-            t_inter[key] = work.tile([P, J * INNER], BF16, align_bytes=64, tag="inter", bufs=INTER_BUFS, name="inter")
-            return t_inter[key]
+        def head(h):
+            return slice(h * HD, (h + 1) * HD)
 
-        def il_direct(engine, kind, a, c):
-            copy(
-                engine,
-                new_inter((kind, a, c))[:].rearrange("p (c i t) -> p c t i", i=4, t=J),
-                il_source(kind, a, c).rearrange("p t (c i) -> p c t i", i=4),
-            )
-
-        def il_tensor(kind, a, c, h):
-            bank = tps.tile([P, 1024], BF16, tag="tp", name="bank")
-            t_bank["PI", kind, a, c, h] = bank
-            src = il_source(kind, a, c).rearrange("p t w -> p w t")
-            for q in range(2):
-                lo = 256 * h + 128 * q
-                nc.tensor.matmul(
-                    bank[:, 512 * q : 512 * (q + 1)].rearrange("p (w t) -> p w t", t=J),
-                    lhsT=ident_bf[:],
-                    rhs=src[:, lo : lo + 128, :],
-                    start=True,
-                    stop=True,
-                )
-
-        def il_copy(engine, kind, a, c, h):
-            if h == 0:
-                new_inter((kind, a, c))
-            copy(engine, t_inter[kind, a, c][:, 1024 * h : 1024 * (h + 1)], t_bank.pop(("PI", kind, a, c, h))[:])
-
-        def quantize(codes, scales, src, fmt):
-            nc.vector.quantize_mx(out=codes.bitcast(fmt), scales=scales, in_=src)
-
-        def vid_quantize(g, c):
-            cols = slice(c * 512, (c + 1) * 512)
-            quantize(vid_codes[g][:, cols], vid_scales[g][:, cols], t_inter.pop(("VI", g, c))[:], E4M3X4)
-
-        def dz_quantize(f, g):
-            cols = slice(f * 512, (f + 1) * 512)
-            quantize(dz_codes[g][:, cols], dz_scales[g][:, cols], t_inter.pop(("DI", f, g))[:], E5M2X4)
-
-        def transposes(key, words, count):
-            bank = tps.tile([P, 2, 256], F32, tag="tp", name="bank")
-            t_bank[key] = bank[:, :, 0 : count * P]
-            for jj in range(count):
-                for u in range(2):
-                    nc.tensor.transpose(bank[:, u, jj * P : (jj + 1) * P], words[:, jj, u : 256 : 2], ident[:])
-
-        def transposed_copy(engine, key):
-            t = work.tile([P, 1024], BF16, align_bytes=64, tag="grouped", bufs=GROUPED_BUFS, name="grouped")
-            src = t_bank.pop(key)
-            t_grp[key] = t[:, 0 : 4 * src.shape[2]]
-            dst = t_grp[key].bitcast(F32).rearrange("p (r u) -> p r u", u=2)
-            copy(engine, dst, src.rearrange("p u r -> p r u"))
-
-        def dz_transpose(f, g, unit):
-            js = UNITS[f, g][unit]
-            if f == 2:
-                words = grad_raw[2][:, g, :].bitcast(F32).rearrange("p (j w) -> p j w", j=J)
-            else:
-                words = dz_tiles[f, g][:].bitcast(F32)
-            transposes(("D", f, g, unit), words[:, js[0] : js[-1] + 1, :], len(js))
-
-        def dzt_quantize(f, g, unit):
-            js = UNITS[f, g][unit]
-            cols = slice((J * g + js[0]) * P, (J * g + js[-1] + 1) * P)
-            quantize(dzt_codes[f][:, cols], dzt_scales[f][:, cols], t_grp.pop(("D", f, g, unit)), E5M2X4)
-
-        def w_transpose(n, f, h):
-            words = w_raw[n][:].bitcast(F32)
-            transposes(("W", n, f, h), words[:, 2 * h : 2 * h + 2, 256 * f : 256 * (f + 1)], 2)
-
-        def w_quantize(n, f, h):
-            cols = slice(n * 512 + h * 256, n * 512 + (h + 1) * 256)
-            quantize(w_codes[f][:, cols], w_scales[f][:, cols], t_grp.pop(("W", n, f, h)), E4M3X4)
-
-        def out1(f, i):
-            acc = accs.tile([P, 512], F32, tag="acc", name="acc")
-            t_acc[1, f, i] = acc
-            for g in range(GROUPS):
-                nc.tensor.matmul_mx(
-                    out=acc[:],
-                    lhsT=vid_codes[g][:, i * P : (i + 1) * P].bitcast(E4M3X4),
-                    lhsT_scale=vid_scales[g][:, i * P : (i + 1) * P],
-                    rhs=dz_codes[g][:, f * 512 : (f + 1) * 512].bitcast(E5M2X4),
-                    rhs_scale=dz_scales[g][:, f * 512 : (f + 1) * 512],
-                    start=(g == 0),
-                    stop=(g == GROUPS - 1),
-                )
-
-        def out1_copy(engine, f, i):
-            if (1, f, i // 2) not in t_res:
-                t_res[1, f, i // 2] = outs.tile([P, 3, 512], F32, tag="res", bufs=RES_BUFS, name="res")
-            copy(engine, t_res[1, f, i // 2][:, i % 2, :], t_acc.pop((1, f, i))[:])
-
-        def out1_store(f, i):
-            rows = out_1[i * P : (i + 2) * P, f * 512 : (f + 1) * 512]
-            nc.sync.dma_start(out=rows.rearrange("(a p) w -> p a w", p=P), in_=t_res[1, f, i // 2][:, 0:2, :])
-
-        out0_rows = out_0.rearrange("(g p j) w -> g j p w", g=GROUPS, j=J)
-
-        def out0(g, j, n):
-            cols = slice((J * g + j) * P, (J * g + j + 1) * P)
-            acc = accs.tile([P, 512], F32, tag="acc", name="acc")
-            t_acc[0, g, j, n] = acc
-            order = (2, 0, 1)
-            for f in order:
-                nc.tensor.matmul_mx(
-                    out=acc[:],
-                    lhsT=dzt_codes[f][:, cols].bitcast(E5M2X4),
-                    lhsT_scale=dzt_scales[f][:, cols],
-                    rhs=w_codes[f][:, n * 512 : (n + 1) * 512].bitcast(E4M3X4),
-                    rhs_scale=w_scales[f][:, n * 512 : (n + 1) * 512],
-                    start=(f == order[0]),
-                    stop=(f == order[-1]),
-                )
-
-        def out0_copy(engine, g, j, n):
-            if (0, g, j) not in t_res:
-                t_res[0, g, j] = outs.tile([P, 3, 512], F32, tag="res", bufs=RES_BUFS, name="res")
-            copy(
-                engine,
-                t_res[0, g, j][:, n, :].rearrange("p (r i) -> p r i", i=4),
-                t_acc.pop((0, g, j, n))[:].rearrange("p (i r) -> p r i", i=4),
-            )
-
-        def out0_store(g, j, n=None):
-            if n is None:
-                nc.sync.dma_start(out=out0_rows[g, j], in_=t_res[0, g, j][:].rearrange("p n w -> p (n w)"))
-            else:
-                nc.sync.dma_start(out=out0_rows[g, j][:, n * 512 : (n + 1) * 512], in_=t_res[0, g, j][:, n, :])
-
-        def dummy(k):
-            bank = tps.tile([P, 512], F32, tag="tp", name="bank")
-            nc.tensor.matmul(bank[:], lhsT=ones[:], rhs=zeros[:], start=True, stop=True)
-
-        def scaled_grad(f, g, j):
-            lead[f, g, j] = work.tile([P, INNER], F32, tag="lead", bufs=LEAD_BUFS, name="lead")
+        def scale_grad(which, g, j):
+            a = work.tile([P, INNER], F32, tag="scaled", bufs=4, name="scaled")
+            scaled[which, g, j] = a
+            r = rstd[:, g, rstd_cols(which, j)]
+            grad = grad_raw[which][:, g, j * INNER : (j + 1) * INNER]
             for h in range(HEADS):
                 nc.vector.scalar_tensor_tensor(
-                    out=lead[f, g, j][:, h * HD : (h + 1) * HD],
-                    in0=grad_raw[f][:, g, j * INNER + h * HD : j * INNER + (h + 1) * HD],
-                    scalar=rstd[:, g, (2 * j + f) * HEADS + h : (2 * j + f) * HEADS + h + 1],
-                    in1=gains[:, f * HD : (f + 1) * HD],
+                    out=a[:, head(h)],
+                    in0=grad[:, head(h)],
+                    scalar=r[:, h : h + 1],
+                    in1=gains[:, head(which)],
                     op0=MULT,
                     op1=MULT,
                 )
 
-        def dots(f, g, j):
-            s = work.tile([P, HEADS], F32, tag="sums", bufs=6, name="sums")
-            sums[f, g, j] = s
-            for h in range(HEADS):
-                junk = work.tile([P, HD], BF16, tag="junk", bufs=2, name="junk")
-                nc.vector.scalar_tensor_tensor(
-                    out=junk[:],
-                    in0=lead[f, g, j][:, h * HD : (h + 1) * HD],
-                    scalar=1.0,
-                    in1=pre(f, g, j, h * HD, (h + 1) * HD),
-                    op0=MULT,
-                    op1=MULT,
-                    accum_out=s[:, h : h + 1],
-                )
-
-        def products(f, g, j):
-            prods[f, g, j] = work.tile([P, INNER], F32, tag="prod", bufs=PROD_BUFS, name="prod")
-            nc.vector.tensor_tensor(out=prods[f, g, j][:], in0=lead[f, g, j][:], in1=pre(f, g, j, 0, INNER), op=MULT)
-
-        def dots_scalar(f, g, j):
-            s = work.tile([P, HEADS], F32, tag="sums", bufs=6, name="sums")
-            sums[f, g, j] = s
-            t = prods.pop((f, g, j))
-            for h in range(HEADS):
-                junk = work.tile([P, HD], BF16, tag="sjunk", bufs=2, name="sjunk")
-                nc.scalar.activation(junk[:], t[:, h * HD : (h + 1) * HD], COPY, accum_out=s[:, h : h + 1])
-
-        def coefs(f, g, j):
-            c = work.tile([P, HEADS], F32, tag="coefs", bufs=6, name="coefs")
-            coef[f, g, j] = c
+        def multiply(which, g, j):
+            t = work.tile([P, INNER], F32, tag="product", bufs=1, name="product")
+            products[which, g, j] = t
             nc.vector.tensor_tensor(
-                out=c[:],
-                in0=sums.pop((f, g, j))[:],
-                in1=nr2[:, g, (2 * j + f) * HEADS : (2 * j + f + 1) * HEADS],
-                op=MULT,
+                out=t[:], in0=scaled[which, g, j][:], in1=saved[which, g][:, j, :], op=MULT
             )
 
-        def finish(f, g, j):
+        def dot(which, g, j, engine):
+            s = work.tile([P, HEADS], F32, tag="dots", bufs=6, name="dots")
+            dots[which, g, j] = s
+            for h in range(HEADS):
+                if engine == "V":
+                    unread = work.tile([P, HD], BF16, tag="unread", bufs=2, name="unread")
+                    nc.vector.scalar_tensor_tensor(
+                        out=unread[:],
+                        in0=scaled[which, g, j][:, head(h)],
+                        scalar=1.0,
+                        in1=saved[which, g][:, j, head(h)],
+                        op0=MULT,
+                        op1=MULT,
+                        accum_out=s[:, h : h + 1],
+                    )
+                else:
+                    unread = work.tile([P, HD], BF16, tag="unread_scalar", bufs=2, name="unread_scalar")
+                    nc.scalar.activation(
+                        unread[:], products[which, g, j][:, head(h)], COPY, accum_out=s[:, h : h + 1]
+                    )
+
+        def coefficient(which, g, j):
+            c = work.tile([P, HEADS], F32, tag="coefs", bufs=6, name="coefs")
+            coefs[which, g, j] = c
+            nc.vector.tensor_tensor(
+                out=c[:], in0=dots[which, g, j][:], in1=neg_r2[:, g, rstd_cols(which, j)], op=MULT
+            )
+
+        def finish(which, g, j):
             if j == 0:
-                dz_tiles[f, g] = work.tile([P, J, INNER], BF16, tag="dz", bufs=DZ_BUFS, name="dz")
+                dz[which, g] = work.tile([P, J, INNER], BF16, tag="dz", bufs=3, name="dz")
             for h in range(HEADS):
                 nc.vector.scalar_tensor_tensor(
-                    out=dz_tiles[f, g][:, j, h * HD : (h + 1) * HD],
-                    in0=pre(f, g, j, h * HD, (h + 1) * HD),
-                    scalar=coef[f, g, j][:, h : h + 1],
-                    in1=lead[f, g, j][:, h * HD : (h + 1) * HD],
+                    out=dz[which, g][:, j, head(h)],
+                    in0=saved[which, g][:, j, head(h)],
+                    scalar=coefs[which, g, j][:, h : h + 1],
+                    in1=scaled[which, g, j][:, head(h)],
                     op0=MULT,
                     op1=ADD,
                 )
 
+        def dz_rows(which, g):
+            if which == V:
+                return grad_raw[V][:, g, :].rearrange("p (j w) -> p j w", j=J)
+            return dz[which, g][:]
+
+        interleaved, half_banks = {}, {}
+
+        def rows_to_interleave(what, a, b):
+            return vid_raw[a][:, :, b * BANK : (b + 1) * BANK] if what == "vid" else dz_rows(a, b)
+
+        def new_interleaved(what, a, b):
+            tile = work.tile([P, J * BANK], BF16, align_bytes=64, tag="interleaved", bufs=3, name="interleaved")
+            interleaved[what, a, b] = tile
+            return tile
+
+        def interleave(what, a, b, engine):
+            copy(
+                engine,
+                new_interleaved(what, a, b)[:].rearrange("p (c i j) -> p c j i", i=4, j=J),
+                rows_to_interleave(what, a, b).rearrange("p j (c i) -> p c j i", i=4),
+            )
+
+        def interleave_by_matmul(what, a, b, half):
+            bank = banks.tile([P, 2 * BANK], BF16, tag="bank", name="bank")
+            half_banks[what, a, b, half] = bank
+            rows = rows_to_interleave(what, a, b).rearrange("p j w -> p w j")
+            for q in range(2):
+                lo = 256 * half + 128 * q
+                nc.tensor.matmul(
+                    bank[:, BANK * q : BANK * (q + 1)].rearrange("p (w j) -> p w j", j=J),
+                    lhsT=identity_bf16[:],
+                    rhs=rows[:, lo : lo + 128, :],
+                    start=True,
+                    stop=True,
+                )
+
+        def copy_interleaved(what, a, b, half, engine):
+            if half == 0:
+                new_interleaved(what, a, b)
+            cols = slice(2 * BANK * half, 2 * BANK * (half + 1))
+            copy(engine, interleaved[what, a, b][:, cols], half_banks[what, a, b, half][:])
+
+        def quantize_vid(g, c):
+            quantize(vid_tok[g], slice(c * BANK, (c + 1) * BANK), interleaved["vid", g, c][:], E4M3X4)
+
+        def quantize_dz(which, g):
+            cols = slice(which * BANK, (which + 1) * BANK)
+            quantize(dz_tok[g], cols, interleaved["dz", which, g][:], E5M2X4)
+
+        word_banks, grouped = {}, {}
+
+        def transpose(key, words):
+            rows = words.shape[1]
+            bank = banks.tile([P, 2, 2 * P], F32, tag="bank", name="bank")
+            word_banks[key] = bank[:, :, 0 : rows * P]
+            for row in range(rows):
+                for u in range(2):
+                    nc.tensor.transpose(
+                        bank[:, u, row * P : (row + 1) * P], words[:, row, u : 256 : 2], identity[:]
+                    )
+
+        def copy_transposed(key, engine):
+            src = word_banks[key]
+            tile = work.tile([P, 2 * BANK], BF16, align_bytes=64, tag="grouped", bufs=5, name="grouped")
+            grouped[key] = tile[:, 0 : 4 * src.shape[2]]
+            copy(
+                engine,
+                grouped[key].bitcast(F32).rearrange("p (r u) -> p r u", u=2),
+                src.rearrange("p u r -> p r u"),
+            )
+
+        def slots(which, g, part):
+            if (which, g) == LAST_DZ and part > 0:
+                return slice(part + 1, part + 2)
+            return slice(2 * part, 2 * part + 2)
+
+        def tokens_of(g, js):
+            return slice((J * g + js.start) * P, (J * g + js.stop) * P)
+
+        def transpose_dz(which, g, part):
+            words = dz_rows(which, g)[:, slots(which, g, part), :].bitcast(F32)
+            transpose(("dz", which, g, part), words)
+
+        def copy_dz(which, g, part, engine):
+            copy_transposed(("dz", which, g, part), engine)
+
+        def quantize_dz_feat(which, g, part):
+            cols = tokens_of(g, slots(which, g, part))
+            quantize(dz_feat[which], cols, grouped["dz", which, g, part], E5M2X4)
+
+        def rows_of_w(n, half):
+            return slice((4 * n + 2 * half) * P, (4 * n + 2 * half + 2) * P)
+
+        def transpose_w(n, f, half):
+            words = w_raw[n][:, 2 * half : 2 * half + 2, f * BANK : (f + 1) * BANK].bitcast(F32)
+            transpose(("w", n, f, half), words)
+
+        def copy_w(n, f, half, engine):
+            copy_transposed(("w", n, f, half), engine)
+
+        def quantize_w(n, f, half):
+            quantize(w_feat[f], rows_of_w(n, half), grouped["w", n, f, half], E4M3X4)
+
+        sums, results = {}, {}
+
+        def accumulate(key, passes):
+            acc = accs.tile([P, BANK], F32, tag="acc", name="acc")
+            sums[key] = acc
+            for i, (left, left_cols, left_fmt, right, right_cols, right_fmt) in enumerate(passes):
+                nc.tensor.matmul_mx(
+                    out=acc[:],
+                    lhsT=left[0][:, left_cols].bitcast(left_fmt),
+                    lhsT_scale=left[1][:, left_cols],
+                    rhs=right[0][:, right_cols].bitcast(right_fmt),
+                    rhs_scale=right[1][:, right_cols],
+                    start=(i == 0),
+                    stop=(i == len(passes) - 1),
+                )
+
+        def result(key):
+            if key not in results:
+                results[key] = outs.tile([P, 3, BANK], F32, tag="result", bufs=4, name="result")
+            return results[key]
+
+        def weight_grad(which, i):
+            rows, cols = slice(i * P, (i + 1) * P), slice(which * BANK, (which + 1) * BANK)
+            accumulate(
+                (1, which, i), [(vid_tok[g], rows, E4M3X4, dz_tok[g], cols, E5M2X4) for g in range(GROUPS)]
+            )
+
+        def copy_weight_grad(which, i, engine):
+            copy(engine, result((1, which, i // 2))[:, i % 2, :], sums[1, which, i][:])
+
+        def store_weight_grad(which, i):
+            rows = out_1[i * P : (i + 2) * P, which * BANK : (which + 1) * BANK]
+            nc.sync.dma_start(
+                out=rows.rearrange("(a p) w -> p a w", p=P), in_=result((1, which, i // 2))[:, 0:2, :]
+            )
+
+        def vid_grad(g, j, n):
+            toks, cols = tokens_of(g, slice(j, j + 1)), slice(n * BANK, (n + 1) * BANK)
+            accumulate(
+                (0, g, j, n), [(dz_feat[f], toks, E5M2X4, w_feat[f], cols, E4M3X4) for f in (V, Q, K)]
+            )
+
+        def copy_vid_grad(g, j, n, engine):
+            copy(
+                engine,
+                result((0, g, j))[:, n, :].rearrange("p (r i) -> p r i", i=4),
+                sums[0, g, j, n][:].rearrange("p (i r) -> p r i", i=4),
+            )
+
+        vid_grad_rows = out_0.rearrange("(g p j) w -> g j p w", g=GROUPS, j=J)
+
+        def store_vid_grad(g, j):
+            nc.sync.dma_start(out=vid_grad_rows[g, j], in_=result((0, g, j))[:].rearrange("p n w -> p (n w)"))
+
+        def store_vid_grad_third(g, j, n):
+            cols = slice(n * BANK, (n + 1) * BANK)
+            nc.sync.dma_start(out=vid_grad_rows[g, j][:, cols], in_=result((0, g, j))[:, n, :])
+
+        def keep_clock():
+            bank = banks.tile([P, BANK], F32, tag="bank", name="bank")
+            nc.tensor.matmul(bank[:], lhsT=ones[:], rhs=zeros[:], start=True, stop=True)
+
         tasks = {
-            "ld": load,
-            "PI": il_tensor,
-            "VQ": vid_quantize,
-            "DQ": dz_quantize,
-            "DT": dz_transpose,
-            "TQ": dzt_quantize,
-            "WT": w_transpose,
-            "WQ": w_quantize,
-            "O1": out1,
-            "O0": out0,
-            "S1": out1_store,
-            "S0": out0_store,
-            "L": scaled_grad,
-            "DP": products,
-            "DM": dummy,
-            "C": coefs,
-            "F": finish,
+            "lg": load_grad,
+            "lx": load_vid,
+            "lw": load_w,
+            "ls": load_saved,
+            "a": scale_grad,
+            "m": multiply,
+            "d": dot,
+            "c": coefficient,
+            "f": finish,
+            "ix": lambda g, c, engine: interleave("vid", g, c, engine),
+            "iz": lambda which, g, engine: interleave("dz", which, g, engine),
+            "mx": lambda g, c, half: interleave_by_matmul("vid", g, c, half),
+            "mz": lambda which, g, half: interleave_by_matmul("dz", which, g, half),
+            "cx": lambda g, c, half, engine: copy_interleaved("vid", g, c, half, engine),
+            "cz": lambda which, g, half, engine: copy_interleaved("dz", which, g, half, engine),
+            "qx": quantize_vid,
+            "qz": quantize_dz,
+            "tz": transpose_dz,
+            "gz": copy_dz,
+            "qt": quantize_dz_feat,
+            "tw": transpose_w,
+            "gw": copy_w,
+            "qw": quantize_w,
+            "p1": weight_grad,
+            "e1": copy_weight_grad,
+            "s1": store_weight_grad,
+            "p0": vid_grad,
+            "e0": copy_vid_grad,
+            "s0": store_vid_grad,
+            "st": store_vid_grad_third,
+            "k": keep_clock,
         }
-        for engine, node in SEQ:
-            t = node[0]
-            if t in ("DI", "VI"):
-                il_direct(engine, *node)
-            elif t == "D":
-                (dots if engine == "V" else dots_scalar)(*node[1:])
-            elif t == "IC":
-                il_copy(engine, *node[1:])
-            elif t == "X1":
-                out1_copy(engine, *node[1:])
-            elif t == "X0":
-                out0_copy(engine, *node[1:])
-            elif t == "DC":
-                transposed_copy(engine, ("D",) + node[1:])
-            elif t == "WC":
-                transposed_copy(engine, ("W",) + node[1:])
-            else:
-                tasks[t](*node[1:])
+        for word in ORDER.split():
+            name, *args = word.split(".")
+            tasks[name](*[a if a in ("S", "V") else int(a) for a in args])

from contextlib import ExitStack

import concourse.mybir as mybir
from concourse.masks import make_identity

F32 = mybir.dt.float32
BF16 = mybir.dt.bfloat16
U32 = mybir.dt.uint32
U8 = mybir.dt.uint8
E4M3X4 = mybir.dt.float8_e4m3fn_x4
E5M2X4 = mybir.dt.float8_e5m2_x4
MULT = mybir.AluOpType.mult
ADD = mybir.AluOpType.add
COPY = mybir.ActivationFunctionType.Copy

P = 128
TOKENS, DIM, FEATURES = 1024, 1536, 1536
HEADS, HD = 4, 128
INNER = HEADS * HD
J = 4
GROUPS = TOKENS // (P * J)
BANK = 512
THIRDS = FEATURES // BANK
Q, K, V = 0, 1, 2

FLOPS = 2 * 2 * TOKENS * DIM * FEATURES
BYTES = 2 * (TOKENS * DIM + DIM * FEATURES + 2 * HD + TOKENS * FEATURES) + 4 * (
    2 * TOKENS * INNER + 2 * TOKENS * HEADS + TOKENS * DIM + DIM * FEATURES
)
TRANSPOSE_BANKS = 3
LAST_DZ = (1, 1)

ORDER = """
lg.2.0.1 k lg.0 k k iz.2.0.V tz.2.0.0 lg.2.1.1 k qz.2.0 k k gz.2.0.0.V tz.2.0.1 a.0.0.0 ls.0.0 k k
gz.2.0.1.S qt.2.0.0 k a.0.0.1 tz.2.1.1 qt.2.0.1 mz.2.1.0 a.0.0.2 gz.2.1.1.S tz.2.1.0 lx.0 qt.2.1.1
cz.2.1.0.S a.0.0.3 mz.2.1.1 gz.2.1.0.S m.0.0.0 cz.2.1.1.S d.0.0.1.V d.0.0.0.S qt.2.1.0 c.0.0.0
m.0.0.2 c.0.0.1 lw.2 qz.2.1 d.0.0.2.S f.0.0.0 mx.0.0.0 ix.0.2.S ix.0.1.V c.0.0.2 f.0.0.1 mx.0.0.1
qx.0.1 lx.1 cx.0.0.0.S tz.0.0.0 f.0.0.2 cx.0.0.1.S m.0.0.3 tw.2.2.0 gz.0.0.0.S qx.0.0 tw.2.0.1
d.0.0.3.S qt.0.0.0 tw.2.1.1 qx.0.2 gw.2.0.1.S c.0.0.3 gw.2.1.1.S qw.2.0.1 tw.2.2.1 f.0.0.3 lg.1
gw.2.2.0.S qw.2.1.1 tw.2.0.0 qw.2.2.0 ix.1.1.S ix.1.0.V tz.0.0.1 gw.2.2.1.V lw.0 qx.1.0 tw.2.1.0
gz.0.0.1.V gw.2.0.0.S a.1.0.0 ix.1.2.S p1.2.2 qx.1.1 a.1.0.1 p1.2.0 qw.2.2.1 ls.1.0 a.1.0.2 p1.2.4
gw.2.1.0.S qx.1.2 p1.2.1 e1.2.0.S a.1.0.3 e1.2.4.S tw.0.1.1 e1.2.1.S e1.2.2.V p1.2.10 lw.1
gw.0.1.1.S qt.0.0.1 tw.0.0.0 qw.2.0.0 e1.2.10.S qw.2.1.0 qw.0.1.1 p1.2.5 gw.0.0.0.S m.1.0.3 tw.0.1.0
d.1.0.0.V e1.2.5.S tw.0.2.1 d.1.0.3.S qw.0.0.0 p1.2.3 gw.0.1.0.S c.1.0.0 d.1.0.2.V tw.0.0.1 ls.0.1
gw.0.2.1.S tw.0.2.0 qw.0.1.0 e1.2.3.S m.1.0.1 p1.2.6 gw.0.0.1.S c.1.0.3 c.1.0.2 f.1.0.0 gw.0.2.0.S
tw.1.1.1 d.1.0.1.S qw.0.0.1 tw.1.2.0 a.0.1.0 s1.2.4 gw.1.1.1.S p1.2.7 qw.0.2.0 gw.1.2.0.S qw.0.2.1
tw.1.0.0 qw.1.1.1 s1.2.2 c.1.0.1 qw.1.2.0 tw.1.1.0 m.0.1.0 gw.1.0.0.S tw.1.0.1 f.1.0.1 gw.1.1.0.S
mz.0.0.0 s1.2.0 e1.2.6.S qw.1.0.0 a.0.1.1 tz.1.0.0 d.0.1.0.S ls.1.1 cz.0.0.0.V p1.2.8 e1.2.7.S
d.0.1.1.V p1.2.11 gw.1.0.1.S gz.1.0.0.S mz.0.0.1 qw.1.0.1 e1.2.8.S c.0.1.1 f.1.0.2 p1.2.9 e1.2.11.S
qt.1.0.0 s1.2.6 cz.0.0.1.S tw.1.2.1 f.1.0.3 e1.2.9.S p0.0.0.0 a.0.1.2 gw.1.2.1.S s1.2.10 c.0.1.0
qw.1.1.0 iz.1.0.S tz.1.0.1 a.0.1.3 p0.0.0.2 qw.1.2.1 s1.2.8 m.0.1.3 p0.0.1.0 f.0.1.0 p0.0.0.1
d.0.1.2.V gz.1.0.1.S e0.0.1.0.S p0.0.1.2 f.0.1.1 e0.0.0.0.S p0.0.1.1 c.0.1.2 qt.1.0.1 d.0.1.3.S
f.0.1.2 e0.0.1.2.S p0.0.3.0 c.0.1.3 a.1.1.0 e0.0.0.1.S p0.0.2.0 f.0.1.3 e0.0.1.1.S e0.0.0.2.S
p0.0.3.2 d.1.1.0.V s0.0.1 iz.0.1.S p0.0.3.1 qz.0.0 e0.0.3.0.V p0.0.2.2 s0.0.0 a.1.1.1 tz.0.1.1
e0.0.3.1.V e0.0.3.2.S tz.0.1.0 qz.0.1 e0.0.2.0.S s0.0.3 p0.0.2.1 m.1.1.1 gz.0.1.0.S c.1.1.0 qz.1.0
e0.0.2.2.S p1.0.10 e0.0.2.1.V d.1.1.1.S p1.0.0 f.1.1.0 p1.0.11 s0.0.2 e1.0.10.S p1.0.6 c.1.1.1
e1.0.0.S qt.0.1.0 f.1.1.1 p1.0.1 e1.0.11.S p1.0.7 gz.0.1.1.V e1.0.6.S s1.0.10 a.1.1.2 e1.0.1.S
tz.1.1.0 e1.0.7.S qt.0.1.1 p1.0.8 a.1.1.3 s1.0.0 gz.1.1.0.S p1.0.2 d.1.1.2.V e1.0.8.S p1.0.9
e1.0.2.S s1.0.6 p1.0.3 qt.1.1.0 e1.0.9.S c.1.1.2 p1.0.4 m.1.1.3 p0.1.0.0 f.1.1.2 d.1.1.3.S s1.0.8
e1.0.3.V p1.0.5 e1.0.4.S c.1.1.3 p0.1.0.2 e0.1.0.0.S f.1.1.3 s1.0.2 e1.0.5.S p0.1.1.0 iz.1.1.V
e0.1.0.2.S s1.0.4 p0.1.0.1 e0.1.1.0.V p0.1.1.2 e0.1.0.1.S qz.1.1 p0.1.1.1 s0.1.0 e0.1.1.2.S p1.1.2
e0.1.1.1.V p1.1.10 e1.1.2.S p1.1.3 s0.1.1 e1.1.10.S p1.1.11 e1.1.3.S p1.1.4 e1.1.11.V tz.1.1.1
s1.1.2 e1.1.4.V p1.1.5 gz.1.1.1.V p1.1.8 qt.1.1.1 e1.1.5.V s1.1.10 p1.1.6 e1.1.8.V p1.1.9 p1.1.7
e1.1.6.V s1.1.4 e1.1.9.S tz.1.1.2 e1.1.7.V p0.1.2.0 gz.1.1.2.V s1.1.8 p1.1.0 qt.1.1.2 e0.1.2.0.V
p0.1.2.1 e1.1.0.S s1.1.6 p1.1.1 e0.1.2.1.S p0.1.2.2 e1.1.1.S st.1.2.0 p0.1.3.0 st.1.2.1 e0.1.2.2.S
s1.1.0 p0.1.3.1 e0.1.3.0.S p0.1.3.2 e0.1.3.1.S st.1.2.2 st.1.3.0 e0.1.3.2.S st.1.3.1 st.1.3.2
"""


def tile_naswinattention_pa_v_kernel(
    tc, vid, w_qkv, b_qkv, q_scale, k_scale, qk_pre, qk_rstd, grad_q, grad_k, grad_v, out_0, out_1
):
    nc = tc.nc
    with ExitStack() as ctx:
        keep = ctx.enter_context(tc.tile_pool(name="keep", bufs=1))
        raws = ctx.enter_context(tc.tile_pool(name="raws", bufs=1))
        work = ctx.enter_context(tc.tile_pool(name="work", bufs=2))
        outs = ctx.enter_context(tc.tile_pool(name="outs", bufs=1))
        banks = ctx.enter_context(tc.psum_pool(name="banks", bufs=TRANSPOSE_BANKS))
        accs = ctx.enter_context(tc.psum_pool(name="accs", bufs=8 - TRANSPOSE_BANKS))
        ctx.enter_context(tc.manual_schedule())

        def quantised(name, count, width):
            return [
                (
                    keep.tile([P, width], U32, align_bytes=64, name=f"{name}_codes{i}"),
                    keep.tile([P, width], U8, align_bytes=64, name=f"{name}_scales{i}"),
                )
                for i in range(count)
            ]

        dz_tok = quantised("dz_tok", GROUPS, FEATURES)
        vid_tok = quantised("vid_tok", GROUPS, DIM)
        dz_feat = quantised("dz_feat", THIRDS, TOKENS)
        w_feat = quantised("w_feat", THIRDS, DIM)

        def quantize(operand, cols, values, fmt):
            codes, scales = operand
            nc.vector.quantize_mx(out=codes[:, cols].bitcast(fmt), scales=scales[:, cols], in_=values)

        gains_row = keep.tile([P, 2 * HD], BF16, name="gains_row")
        nc.vector.memset(gains_row[:], 0.0)
        nc.scalar.dma_start(out=gains_row[0:1, 0:HD], in_=q_scale.unsqueeze(0))
        nc.scalar.dma_start(out=gains_row[0:1, HD : 2 * HD], in_=k_scale.unsqueeze(0))
        rstd = keep.tile([P, GROUPS, J * 2 * HEADS], F32, name="rstd")
        nc.scalar.dma_start(out=rstd[:], in_=qk_rstd.rearrange("(g p j) c h -> p g (j c h)", g=GROUPS, j=J))

        def rstd_cols(which, j):
            lo = (2 * j + which) * HEADS
            return slice(lo, lo + HEADS)

        identity = keep.tile([P, P], F32, name="identity")
        make_identity(nc, identity[:])
        ones = keep.tile([P, P], BF16, name="ones")
        nc.vector.memset(ones[:], 1.0)
        identity_bf16 = keep.tile([P, P], BF16, name="identity_bf16")
        make_identity(nc, identity_bf16[:])
        zeros = keep.tile([P, BANK], BF16, name="zeros")
        nc.vector.memset(zeros[:], 0.0)
        table = keep.tile([P, 1], F32, name="table")
        nc.vector.memset(table[:], 0.0)
        nc.scalar.copy(table[:], table[:])
        gains = keep.tile([P, 2 * HD], F32, name="gains")
        gains_bank = banks.tile([P, 2 * HD], F32, tag="bank", name="gains_bank")
        nc.tensor.matmul(gains_bank[:], lhsT=ones[:], rhs=gains_row[:], start=True, stop=True)
        nc.scalar.copy(gains[:], gains_bank[:])
        neg_r2 = keep.tile([P, GROUPS, J * 2 * HEADS], F32, name="neg_r2")
        nc.vector.scalar_tensor_tensor(
            out=neg_r2[:], in0=rstd[:], scalar=-1.0 / HD, in1=rstd[:], op0=MULT, op1=MULT
        )

        grads = (grad_q, grad_k, grad_v)
        grad_raw, vid_raw, w_raw, saved = {}, {}, {}, {}

        def load_grad(which, first=0, count=GROUPS):
            if which not in grad_raw:
                grad_raw[which] = raws.tile([P, GROUPS, J * INNER], BF16, name=f"grad{which}")
            groups = slice(first, first + count)
            for n in range(2):
                rows = grads[which][n].rearrange("(g x b j) h d -> b x g (j h d)", g=GROUPS, b=2, j=J)
                for b in range(2):
                    nc.sync.dma_start(out=grad_raw[which][2 * n + b : P : 4, groups, :], in_=rows[b][:, groups, :])

        def load_vid(g):
            rows = vid.rearrange("(g p j) w -> g p j w", g=GROUPS, j=J)[g]
            vid_raw[g] = raws.tile([P, J, DIM], BF16, tag="big", bufs=4, name=f"vid{g}")
            for half in (slice(0, 2), slice(2, 4)):
                nc.sync.dma_start(out=vid_raw[g][:, half, :], in_=rows[:, half, :])

        def load_w(n):
            rows = w_qkv.rearrange("(n r i) f -> n r i f", n=THIRDS, i=4)[n]
            w_raw[n] = raws.tile([P, 4, FEATURES], BF16, tag="big", bufs=4, name=f"w{n}")
            for half in (slice(0, 2), slice(2, 4)):
                nc.sync.dma_start(out=w_raw[n][:, half, :], in_=rows[:, half, :])

        def load_saved(which, g):
            rows = qk_pre.rearrange("(g p j) c h d -> g c p j (h d)", g=GROUPS, j=J)[g, which]
            saved[which, g] = raws.tile([P, J, INNER], F32, tag="saved", bufs=3, name=f"saved{which}{g}")
            nc.sync.dma_start(out=saved[which, g][:], in_=rows)

        def copy(engine, dst, src):
            if engine == "V":
                nc.vector.tensor_copy(out=dst, in_=src)
            else:
                nc.scalar.copy(dst, src)

        dz, scaled, products, dots, coefs = {}, {}, {}, {}, {}

        def head(h):
            return slice(h * HD, (h + 1) * HD)

        def scale_grad(which, g, j):
            a = work.tile([P, INNER], F32, tag="scaled", bufs=4, name="scaled")
            scaled[which, g, j] = a
            r = rstd[:, g, rstd_cols(which, j)]
            grad = grad_raw[which][:, g, j * INNER : (j + 1) * INNER]
            for h in range(HEADS):
                nc.vector.scalar_tensor_tensor(
                    out=a[:, head(h)],
                    in0=grad[:, head(h)],
                    scalar=r[:, h : h + 1],
                    in1=gains[:, head(which)],
                    op0=MULT,
                    op1=MULT,
                )

        def multiply(which, g, j):
            t = work.tile([P, INNER], F32, tag="product", bufs=1, name="product")
            products[which, g, j] = t
            nc.vector.tensor_tensor(
                out=t[:], in0=scaled[which, g, j][:], in1=saved[which, g][:, j, :], op=MULT
            )

        def dot(which, g, j, engine):
            s = work.tile([P, HEADS], F32, tag="dots", bufs=6, name="dots")
            dots[which, g, j] = s
            for h in range(HEADS):
                if engine == "V":
                    unread = work.tile([P, HD], BF16, tag="unread", bufs=2, name="unread")
                    nc.vector.scalar_tensor_tensor(
                        out=unread[:],
                        in0=scaled[which, g, j][:, head(h)],
                        scalar=1.0,
                        in1=saved[which, g][:, j, head(h)],
                        op0=MULT,
                        op1=MULT,
                        accum_out=s[:, h : h + 1],
                    )
                else:
                    unread = work.tile([P, HD], BF16, tag="unread_scalar", bufs=2, name="unread_scalar")
                    nc.scalar.activation(
                        unread[:], products[which, g, j][:, head(h)], COPY, accum_out=s[:, h : h + 1]
                    )

        def coefficient(which, g, j):
            c = work.tile([P, HEADS], F32, tag="coefs", bufs=6, name="coefs")
            coefs[which, g, j] = c
            nc.vector.tensor_tensor(
                out=c[:], in0=dots[which, g, j][:], in1=neg_r2[:, g, rstd_cols(which, j)], op=MULT
            )

        def finish(which, g, j):
            if j == 0:
                dz[which, g] = work.tile([P, J, INNER], BF16, tag="dz", bufs=3, name="dz")
            for h in range(HEADS):
                nc.vector.scalar_tensor_tensor(
                    out=dz[which, g][:, j, head(h)],
                    in0=saved[which, g][:, j, head(h)],
                    scalar=coefs[which, g, j][:, h : h + 1],
                    in1=scaled[which, g, j][:, head(h)],
                    op0=MULT,
                    op1=ADD,
                )

        def dz_rows(which, g):
            if which == V:
                return grad_raw[V][:, g, :].rearrange("p (j w) -> p j w", j=J)
            return dz[which, g][:]

        interleaved, half_banks = {}, {}

        def rows_to_interleave(what, a, b):
            return vid_raw[a][:, :, b * BANK : (b + 1) * BANK] if what == "vid" else dz_rows(a, b)

        def new_interleaved(what, a, b):
            tile = work.tile([P, J * BANK], BF16, align_bytes=64, tag="interleaved", bufs=3, name="interleaved")
            interleaved[what, a, b] = tile
            return tile

        def interleave(what, a, b, engine):
            copy(
                engine,
                new_interleaved(what, a, b)[:].rearrange("p (c i j) -> p c j i", i=4, j=J),
                rows_to_interleave(what, a, b).rearrange("p j (c i) -> p c j i", i=4),
            )

        def interleave_by_matmul(what, a, b, half):
            bank = banks.tile([P, 2 * BANK], BF16, tag="bank", name="bank")
            half_banks[what, a, b, half] = bank
            rows = rows_to_interleave(what, a, b).rearrange("p j w -> p w j")
            for q in range(2):
                lo = 256 * half + 128 * q
                nc.tensor.matmul(
                    bank[:, BANK * q : BANK * (q + 1)].rearrange("p (w j) -> p w j", j=J),
                    lhsT=identity_bf16[:],
                    rhs=rows[:, lo : lo + 128, :],
                    start=True,
                    stop=True,
                )

        def copy_interleaved(what, a, b, half, engine):
            if half == 0:
                new_interleaved(what, a, b)
            cols = slice(2 * BANK * half, 2 * BANK * (half + 1))
            copy(engine, interleaved[what, a, b][:, cols], half_banks[what, a, b, half][:])

        def quantize_vid(g, c):
            quantize(vid_tok[g], slice(c * BANK, (c + 1) * BANK), interleaved["vid", g, c][:], E4M3X4)

        def quantize_dz(which, g):
            cols = slice(which * BANK, (which + 1) * BANK)
            quantize(dz_tok[g], cols, interleaved["dz", which, g][:], E5M2X4)

        word_banks, grouped = {}, {}

        def transpose(key, words):
            rows = words.shape[1]
            bank = banks.tile([P, 2, 2 * P], F32, tag="bank", name="bank")
            word_banks[key] = bank[:, :, 0 : rows * P]
            for row in range(rows):
                for u in range(2):
                    nc.tensor.transpose(
                        bank[:, u, row * P : (row + 1) * P], words[:, row, u : 256 : 2], identity[:]
                    )

        def copy_transposed(key, engine):
            src = word_banks[key]
            tile = work.tile([P, 2 * BANK], BF16, align_bytes=64, tag="grouped", bufs=5, name="grouped")
            grouped[key] = tile[:, 0 : 4 * src.shape[2]]
            copy(
                engine,
                grouped[key].bitcast(F32).rearrange("p (r u) -> p r u", u=2),
                src.rearrange("p u r -> p r u"),
            )

        def slots(which, g, part):
            if (which, g) == LAST_DZ and part > 0:
                return slice(part + 1, part + 2)
            return slice(2 * part, 2 * part + 2)

        def tokens_of(g, js):
            return slice((J * g + js.start) * P, (J * g + js.stop) * P)

        def transpose_dz(which, g, part):
            words = dz_rows(which, g)[:, slots(which, g, part), :].bitcast(F32)
            transpose(("dz", which, g, part), words)

        def copy_dz(which, g, part, engine):
            copy_transposed(("dz", which, g, part), engine)

        def quantize_dz_feat(which, g, part):
            cols = tokens_of(g, slots(which, g, part))
            quantize(dz_feat[which], cols, grouped["dz", which, g, part], E5M2X4)

        def rows_of_w(n, half):
            return slice((4 * n + 2 * half) * P, (4 * n + 2 * half + 2) * P)

        def transpose_w(n, f, half):
            words = w_raw[n][:, 2 * half : 2 * half + 2, f * BANK : (f + 1) * BANK].bitcast(F32)
            transpose(("w", n, f, half), words)

        def copy_w(n, f, half, engine):
            copy_transposed(("w", n, f, half), engine)

        def quantize_w(n, f, half):
            quantize(w_feat[f], rows_of_w(n, half), grouped["w", n, f, half], E4M3X4)

        sums, results = {}, {}

        def accumulate(key, passes):
            acc = accs.tile([P, BANK], F32, tag="acc", name="acc")
            sums[key] = acc
            for i, (left, left_cols, left_fmt, right, right_cols, right_fmt) in enumerate(passes):
                nc.tensor.matmul_mx(
                    out=acc[:],
                    lhsT=left[0][:, left_cols].bitcast(left_fmt),
                    lhsT_scale=left[1][:, left_cols],
                    rhs=right[0][:, right_cols].bitcast(right_fmt),
                    rhs_scale=right[1][:, right_cols],
                    start=(i == 0),
                    stop=(i == len(passes) - 1),
                )

        def result(key):
            if key not in results:
                results[key] = outs.tile([P, 3, BANK], F32, tag="result", bufs=4, name="result")
            return results[key]

        def weight_grad(which, i):
            rows, cols = slice(i * P, (i + 1) * P), slice(which * BANK, (which + 1) * BANK)
            accumulate(
                (1, which, i), [(vid_tok[g], rows, E4M3X4, dz_tok[g], cols, E5M2X4) for g in range(GROUPS)]
            )

        def copy_weight_grad(which, i, engine):
            copy(engine, result((1, which, i // 2))[:, i % 2, :], sums[1, which, i][:])

        def store_weight_grad(which, i):
            rows = out_1[i * P : (i + 2) * P, which * BANK : (which + 1) * BANK]
            nc.sync.dma_start(
                out=rows.rearrange("(a p) w -> p a w", p=P), in_=result((1, which, i // 2))[:, 0:2, :]
            )

        def vid_grad(g, j, n):
            toks, cols = tokens_of(g, slice(j, j + 1)), slice(n * BANK, (n + 1) * BANK)
            accumulate(
                (0, g, j, n), [(dz_feat[f], toks, E5M2X4, w_feat[f], cols, E4M3X4) for f in (V, Q, K)]
            )

        def copy_vid_grad(g, j, n, engine):
            copy(
                engine,
                result((0, g, j))[:, n, :].rearrange("p (r i) -> p r i", i=4),
                sums[0, g, j, n][:].rearrange("p (i r) -> p r i", i=4),
            )

        vid_grad_rows = out_0.rearrange("(g p j) w -> g j p w", g=GROUPS, j=J)

        def store_vid_grad(g, j):
            nc.sync.dma_start(out=vid_grad_rows[g, j], in_=result((0, g, j))[:].rearrange("p n w -> p (n w)"))

        def store_vid_grad_third(g, j, n):
            cols = slice(n * BANK, (n + 1) * BANK)
            nc.sync.dma_start(out=vid_grad_rows[g, j][:, cols], in_=result((0, g, j))[:, n, :])

        def keep_clock():
            bank = banks.tile([P, BANK], F32, tag="bank", name="bank")
            nc.tensor.matmul(bank[:], lhsT=ones[:], rhs=zeros[:], start=True, stop=True)

        tasks = {
            "lg": load_grad,
            "lx": load_vid,
            "lw": load_w,
            "ls": load_saved,
            "a": scale_grad,
            "m": multiply,
            "d": dot,
            "c": coefficient,
            "f": finish,
            "ix": lambda g, c, engine: interleave("vid", g, c, engine),
            "iz": lambda which, g, engine: interleave("dz", which, g, engine),
            "mx": lambda g, c, half: interleave_by_matmul("vid", g, c, half),
            "mz": lambda which, g, half: interleave_by_matmul("dz", which, g, half),
            "cx": lambda g, c, half, engine: copy_interleaved("vid", g, c, half, engine),
            "cz": lambda which, g, half, engine: copy_interleaved("dz", which, g, half, engine),
            "qx": quantize_vid,
            "qz": quantize_dz,
            "tz": transpose_dz,
            "gz": copy_dz,
            "qt": quantize_dz_feat,
            "tw": transpose_w,
            "gw": copy_w,
            "qw": quantize_w,
            "p1": weight_grad,
            "e1": copy_weight_grad,
            "s1": store_weight_grad,
            "p0": vid_grad,
            "e0": copy_vid_grad,
            "s0": store_vid_grad,
            "st": store_vid_grad_third,
            "k": keep_clock,
        }
        for word in ORDER.split():
            name, *args = word.split(".")
            tasks[name](*[a if a in ("S", "V") else int(a) for a in args])
